import numpy as np
import ml_dtypes


def mxq(x, axis, fmt="e4m3"):
    dtype, down = {"e4m3": (ml_dtypes.float8_e4m3fn, 7), "e5m2": (ml_dtypes.float8_e5m2, 14)}[fmt]
    v = np.moveaxis(np.asarray(x, np.float32).astype(ml_dtypes.bfloat16).astype(np.float64), axis, -1)
    blocks = v.reshape(v.shape[:-1] + (-1, 32))
    amax = np.abs(blocks).max(-1, keepdims=True)
    byte = np.maximum(np.where(amax > 0, np.frexp(amax)[1] - 1 + 127, 0) - down, 1)
    scale = np.exp2(byte - 127.0)
    codes = (blocks / scale).astype(np.float32).astype(dtype).astype(np.float64)
    return np.moveaxis((codes * scale).reshape(v.shape), -1, axis)


WIDE = False


def mx_kscale(k):
    if not WIDE:
        return np.ones(k)
    levels = np.array([18, -18])
    if k % 512:
        return np.exp2(np.random.permutation(np.resize(levels, k // 32))).repeat(32)
    a = np.empty((k // 512, 16))
    for p in range(k // 512):
        a[p, :8] = np.random.permutation(np.resize(levels, 8))
        for g in range(8):
            far = levels[np.abs(levels - a[p, g]) >= 10]
            a[p, g + 8] = far[np.random.randint(len(far))]
    return np.exp2(a.ravel()).repeat(32)


BF16 = ml_dtypes.bfloat16


def bf(x):
    return np.asarray(x, np.float32).astype(BF16)


def f64(x):
    return np.asarray(x).astype(np.float64)


G, S, M, H, E, C = 2, 512, 512, 1024, 4, 256


def setup_inputs():
    s = mx_kscale(E * C).reshape(E, C)
    u = mx_kscale(H)
    v = mx_kscale(M)
    dm0 = bf(np.random.standard_normal((G, S, E, C)) * 0.1)
    x0 = bf(np.random.standard_normal((G, S, M)))
    wi0 = bf(np.random.standard_normal((E, M, H)) * 10.0 / np.sqrt(S * M))
    g = bf(np.random.standard_normal((E, G, C, H)) * np.exp2(np.random.randint(-6, 1, (E, G, C, 1))) * 4.0 / s[:, None, :, None] * u)
    d = f64(dm0).reshape(G, S, E * C).transpose(0, 2, 1) @ f64(x0)
    d = d.reshape(G, E, C, M).transpose(1, 0, 2, 3).reshape(E, G * C, M)
    pre = (d @ f64(wi0)).reshape(E, G, C, H)
    return {"dispatch_mask": bf(f64(dm0) * s[None, None, :, :]),
            "x": bf(f64(x0) / v),
            "wi": bf(f64(wi0) * v[None, :, None] / u),
            "pre": np.asarray(pre, np.float32),
            "grad_out": g}


def reference(dispatch_mask, x, wi, pre, grad_out):
    dz2 = (f64(grad_out) * (f64(pre) > 0.0)).reshape(E, G * C, H)
    dh = mxq(dz2, 2, "e5m2") @ mxq(f64(wi), 2, "e4m3").transpose(0, 2, 1)
    dz1 = dh.reshape(E, G, C, M).transpose(1, 0, 2, 3).reshape(G, E * C, M)
    ddm = mxq(f64(x), 2, "e4m3") @ mxq(dz1, 2, "e5m2").transpose(0, 2, 1)
    dm = f64(dispatch_mask).reshape(G, S, E * C)
    dx = mxq(dm, 2, "e4m3") @ mxq(dz1, 1, "e5m2")
    return ddm.reshape(G, S, E, C), dx

@@ -1,0 +1,378 @@
+from contextlib import ExitStack
+
+import concourse.mybir as mybir
+from concourse.masks import make_identity
+
+G, S, M, H, E, C = 2, 512, 512, 1024, 4, 256
+FLOPS = 2 * E * G * C * H * M + 2 * 2 * G * S * M * E * C
+
+F32 = mybir.dt.float32
+BF16 = mybir.dt.bfloat16
+U32 = mybir.dt.uint32
+U8 = mybir.dt.uint8
+E4M3 = mybir.dt.float8_e4m3fn_x4
+E5M2 = mybir.dt.float8_e5m2_x4
+ALU = mybir.AluOpType
+
+P = 128
+N = 512
+PAIRS = E // 2
+
+BUFS = {
+    "pre": 4, "grad": 2, "weights": 3, "x": 1,
+    "dz2": 2, "grouped": 3, "x_grouped": 1,
+    "wi_codes": 2, "wi_scales": 2, "dz2_codes": 2, "dz2_scales": 2,
+    "dz1": 2, "dz1_by_m": 1, "dz1_by_slot": 2, "result": 6,
+}
+
+
+def tile_flaxpositionwisemoelayer_pa_v_kernel(tc, dispatch_mask, x, wi, pre, grad_out, out_0, out_1):
+    nc = tc.nc
+
+    mask_rows = dispatch_mask.rearrange("g (p t) e c -> g p t (e c)", t=4)
+    x_rows = x.rearrange("g (p t) m -> p g t m", t=4)
+    wi_rows = wi.rearrange("e (p t) h -> e p t h", t=4)
+    pre_rows = pre.rearrange("e g c h -> e (g c) h").rearrange("e (p j) h -> e p j h", j=4)
+    grad_rows = grad_out.rearrange("e g c h -> e (g c) h").rearrange("e (p j) h -> e p j h", j=4)
+    out0_rows = out_0.rearrange("g (p t) e c -> g p t (e c)", t=4)
+    out1_rows = out_1.rearrange("g (p t) m -> g p t m", t=4)
+
+    with ExitStack() as ctx:
+        keep = ctx.enter_context(tc.tile_pool(name="keep", bufs=1))
+        ring = ctx.enter_context(tc.tile_pool(name="ring", bufs=1))
+        psum = ctx.enter_context(tc.psum_pool(name="psum", bufs=4))
+
+        ident = keep.tile([P, P], F32, name="ident")
+        make_identity(nc, ident[:])
+
+        x_codes = keep.tile([P, G * S], U32, align_bytes=64, name="x_codes")
+        x_scales = keep.tile([P, G * S], U8, align_bytes=64, name="x_scales")
+        mask_codes = keep.tile([P, G, PAIRS * S], U32, align_bytes=64, name="mask_codes")
+        mask_scales = keep.tile([P, G, PAIRS * S], U8, align_bytes=64, name="mask_scales")
+        dz1_m_codes = keep.tile([P, PAIRS, G, N], U32, align_bytes=64, name="dz1_m_codes")
+        dz1_m_scales = keep.tile([P, PAIRS, G, N], U8, align_bytes=64, name="dz1_m_scales")
+        dz1_k_codes = keep.tile([P, PAIRS, G, N], U32, align_bytes=64, name="dz1_k_codes")
+        dz1_k_scales = keep.tile([P, PAIRS, G, N], U8, align_bytes=64, name="dz1_k_scales")
+
+        tiles = {}
+
+        def ring_tile(kind, key, shape, dtype):
+            if (kind, key) not in tiles:
+                tiles[kind, key] = ring.tile(shape, dtype, tag=kind, bufs=BUFS[kind], align_bytes=64, name=kind)
+            return tiles[kind, key]
+
+        def copy(engine, out, in_):
+            if engine == "s":
+                nc.scalar.copy(out=out, in_=in_)
+            else:
+                nc.vector.tensor_copy(out=out, in_=in_)
+
+
+        def load_pre(e, j, n):
+            half, first = divmod(j, 2)
+            t = ring_tile("pre", (e, half), [P, 2, H], F32)
+            nc.sync.dma_start(out=t[:, first : first + n, :], in_=pre_rows[e, :, j : j + n, :])
+
+        def load_grad(e, j, n):
+            t = ring_tile("grad", e, [P, 4, H], BF16)
+            nc.sync.dma_start(out=t[:, j : j + n, :], in_=grad_rows[e, :, j : j + n, :])
+
+        def load_wi(e, j, n):
+            t = ring_tile("weights", ("wi", e), [P, 4, H], BF16)
+            nc.sync.dma_start(out=t[:, j : j + n, :], in_=wi_rows[e, :, j : j + n, :])
+
+        def load_mask(g):
+            t = ring_tile("weights", ("mask", g), [P, 4, E * C], BF16)
+            nc.sync.dma_start(out=t[:], in_=mask_rows[g])
+
+        def load_x():
+            t = ring_tile("x", 0, [P, G, 4, M], BF16)
+            nc.sync.dma_start(out=t[:], in_=x_rows)
+
+
+        def turn(engine, source, grouped, block):
+            bank = psum.tile([P, 2, 2, P], F32, tag="turned", name="bank")
+            for i in range(2):
+                for u in range(2):
+                    nc.tensor.transpose(bank[:, i, u, :], source(i, u), ident[:])
+            words = grouped[:].bitcast(F32)[:, N * block : N * (block + 1)]
+            copy(engine, words.rearrange("p (i r u) -> p i r u", i=2, u=2), bank[:].rearrange("p i u r -> p i r u"))
+
+        def turn_row(engine, row, grouped, block):
+            words = row.bitcast(F32)
+            turn(engine, lambda i, u: words[:, 256 * i + u : 256 * (i + 1) : 2], grouped, block)
+
+        def turn_wi(e, half, engines):
+            for t in range(2):
+                row = 2 * half + t
+                grouped = ring_tile("grouped", ("wi", e), [P, 4096], BF16)
+                turn_row(engines[t], tiles["weights", ("wi", e)][:, row, :], grouped, row)
+
+        def turn_mask(g, half, engines):
+            for t in range(2):
+                row = 2 * half + t
+                grouped = ring_tile("grouped", ("mask", g), [P, 4096], BF16)
+                turn_row(engines[t], tiles["weights", ("mask", g)][:, row, :], grouped, row)
+
+        def turn_x(g, engines):
+            rows = tiles["x", 0]
+            for h in range(2):
+                grouped = ring_tile("x_grouped", 0, [P, 4096], BF16)
+                turn(engines[h], lambda i, u: rows[:, g, 2 * h + i, :].bitcast(F32)[:, u::2], grouped, 2 * g + h)
+
+        def turn_dz2(e, half, engines):
+            dz2 = tiles["dz2", (e, half)]
+            for a in range(2):
+                grouped = ring_tile("grouped", ("dz2", e), [P, 4096], BF16)
+                turn(engines[a], lambda i, u: dz2[:, u, i, 256 * a : 256 * (a + 1)].bitcast(F32), grouped, 2 * a + half)
+
+        def turn_dz1(pair, g, engines):
+            dz1 = tiles["dz1", pair]
+            for h in range(2):
+                grouped = ring_tile("dz1_by_slot", (pair, g), [P, 2048], BF16)
+                turn(engines[h], lambda i, u: dz1[:, 2 * h + i, g, u, :].bitcast(F32), grouped, h)
+
+
+        def relu_backward(e, half):
+            dz2 = ring_tile("dz2", (e, half), [P, 2, 2, N], BF16)
+            pre_words = tiles["pre", (e, half)][:].rearrange("p j (k u b) -> p u j k b", u=2, b=2)
+            grad = tiles["grad", e][:, 2 * half : 2 * half + 2, :].rearrange("p j (k u b) -> p u j k b", u=2, b=2)
+            for u in range(2):
+                nc.vector.scalar_tensor_tensor(
+                    out=dz2[:, u].rearrange("p j (k b) -> p j k b", b=2),
+                    in0=pre_words[:, u], scalar=0.0, in1=grad[:, u], op0=ALU.is_gt, op1=ALU.mult)
+
+        def quantize_wi(e):
+            codes = ring_tile("wi_codes", e, [P, 2 * M], U32)
+            scales = ring_tile("wi_scales", e, [P, 2 * M], U8)
+            nc.vector.quantize_mx(out=codes[:].bitcast(E4M3), scales=scales[:], in_=tiles["grouped", ("wi", e)][:])
+
+        def quantize_dz2(e, a):
+            codes = ring_tile("dz2_codes", e, [P, 2 * N], U32)
+            scales = ring_tile("dz2_scales", e, [P, 2 * N], U8)
+            cols = slice(N * a, N * (a + 1))
+            nc.vector.quantize_mx(
+                out=codes[:, cols].bitcast(E5M2), scales=scales[:, cols],
+                in_=tiles["grouped", ("dz2", e)][:, 4 * N * a : 4 * N * (a + 1)])
+
+        def quantize_mask(g):
+            nc.vector.quantize_mx(
+                out=mask_codes[:, g, :].bitcast(E4M3), scales=mask_scales[:, g, :], in_=tiles["grouped", ("mask", g)][:])
+
+        def quantize_x():
+            nc.vector.quantize_mx(out=x_codes[:].bitcast(E4M3), scales=x_scales[:], in_=tiles["x_grouped", 0][:])
+
+        def quantize_dz1_m(pair, g):
+            by_m = tiles["dz1_by_m", pair][:, g].rearrange("p i u s t -> p (i u s t)")
+            nc.vector.quantize_mx(
+                out=dz1_m_codes[:, pair, g, :].bitcast(E5M2), scales=dz1_m_scales[:, pair, g, :], in_=by_m)
+
+        def quantize_dz1_slots(pair, g):
+            nc.vector.quantize_mx(
+                out=dz1_k_codes[:, pair, g, :].bitcast(E5M2), scales=dz1_k_scales[:, pair, g, :],
+                in_=tiles["dz1_by_slot", (pair, g)][:])
+
+
+        def dh_pass(e, t, a):
+            if a == 0:
+                tiles["dh", (e, t)] = psum.tile([P, N], F32, tag="sums", name="dh")
+            w_cols = slice(256 * t + P * a, 256 * t + P * (a + 1))
+            d_cols = slice(N * a, N * (a + 1))
+            nc.tensor.matmul_mx(
+                out=tiles["dh", (e, t)][:],
+                lhsT=tiles["wi_codes", e][:, w_cols].bitcast(E4M3), lhsT_scale=tiles["wi_scales", e][:, w_cols],
+                rhs=tiles["dz2_codes", e][:, d_cols].bitcast(E5M2), rhs_scale=tiles["dz2_scales", e][:, d_cols],
+                start=(a == 0), stop=(a == 1))
+
+        def dh_first(e, t):
+            dh_pass(e, t, 0)
+
+        def dh_second(e, t, engine):
+            dh_pass(e, t, 1)
+            pair, i = divmod(e, 2)
+            dz1 = ring_tile("dz1", pair, [P, 4, G, 2, 256], BF16)
+            copy(engine,
+                 dz1[:, t, :, :, P * i : P * (i + 1)].rearrange("p g u (q b) -> p g u q b", b=2),
+                 tiles["dh", (e, t)][:].rearrange("p (u b g q) -> p g u q b", u=2, b=2, g=2))
+
+        def interleave_dz1(e):
+            pair, i = divmod(e, 2)
+            by_m = ring_tile("dz1_by_m", pair, [P, G, 2, 2, P, 4], BF16)
+            nc.vector.tensor_copy(
+                out=by_m[:, :, i], in_=tiles["dz1", pair][:, :, :, :, P * i : P * (i + 1)].rearrange("p t g u s -> p g u s t"))
+
+
+        def output_0(pair, g, half, engines):
+            result = ring_tile("result", ("out_0", pair, g, half), [P, 2, N], F32)
+            for t in range(2):
+                acc = psum.tile([P, N], F32, tag="sums", name="acc")
+                cols = slice(S * g + P * (2 * half + t), S * g + P * (2 * half + t + 1))
+                nc.tensor.matmul_mx(
+                    out=acc[:], lhsT=x_codes[:, cols].bitcast(E4M3), lhsT_scale=x_scales[:, cols],
+                    rhs=dz1_m_codes[:, pair, g, :].bitcast(E5M2), rhs_scale=dz1_m_scales[:, pair, g, :],
+                    start=True, stop=True)
+                copy(engines[t],
+                     result[:, t, :].rearrange("p (i q u b) -> p i q u b", i=2, u=2, b=2),
+                     acc[:].rearrange("p (i u q b) -> p i q u b", i=2, u=2, b=2))
+            nc.sync.dma_start(out=out0_rows[g, :, 2 * half : 2 * half + 2, N * pair : N * (pair + 1)], in_=result[:])
+
+        def out1_pass(g, row, pair):
+            if pair == 0:
+                tiles["out_1", (g, row)] = psum.tile([P, N], F32, tag="sums" if g == 0 else "turned", name="acc1")
+            cols = slice(256 * row + P * pair, 256 * row + P * (pair + 1))
+            nc.tensor.matmul_mx(
+                out=tiles["out_1", (g, row)][:],
+                lhsT=mask_codes[:, g, cols].bitcast(E4M3), lhsT_scale=mask_scales[:, g, cols],
+                rhs=dz1_k_codes[:, pair, g, :].bitcast(E5M2), rhs_scale=dz1_k_scales[:, pair, g, :],
+                start=(pair == 0), stop=(pair == 1))
+
+        def output_1_first(g, half):
+            for t in range(2):
+                out1_pass(g, 2 * half + t, 0)
+
+        def output_1_second(g, half, engines):
+            result = ring_tile("result", ("out_1", g, half), [P, 2, N], F32)
+            for t in range(2):
+                row = 2 * half + t
+                out1_pass(g, row, 1)
+                copy(engines[t],
+                     result[:, t, :].rearrange("p (m t) -> p m t", t=4),
+                     tiles["out_1", (g, row)][:].rearrange("p (t m) -> p m t", t=4))
+                if (g, half) == (G - 1, 1):
+                    nc.sync.dma_start(out=out1_rows[g, :, row, :], in_=result[:, t, :])
+            if (g, half) != (G - 1, 1):
+                nc.sync.dma_start(out=out1_rows[g, :, 2 * half : 2 * half + 2, :], in_=result[:])
+
+        with tc.manual_schedule():
+            load_wi(0, 0, 2)
+            load_pre(0, 0, 1)
+            load_grad(0, 0, 1)
+            load_pre(0, 1, 1)
+            load_grad(0, 1, 1)
+            load_pre(0, 2, 2)
+            load_grad(0, 2, 2)
+            load_wi(0, 2, 2)
+            load_grad(1, 0, 4)
+            load_wi(1, 0, 4)
+            load_pre(1, 0, 2)
+            load_pre(1, 2, 2)
+            load_x()
+            turn_wi(0, 0, "ss")
+            relu_backward(0, 0)
+            relu_backward(0, 1)
+            load_grad(2, 0, 4)
+            load_pre(2, 0, 2)
+            load_wi(2, 0, 4)
+            load_pre(2, 2, 2)
+            turn_wi(0, 1, "sv")
+            load_wi(3, 0, 4)
+            turn_dz2(0, 0, "vv")
+            quantize_wi(0)
+            turn_dz2(0, 1, "ss")
+            quantize_dz2(0, 0)
+            turn_wi(1, 0, "ss")
+            dh_first(0, 0)
+            dh_first(0, 1)
+            quantize_dz2(0, 1)
+            dh_second(0, 0, "s")
+            dh_first(0, 2)
+            relu_backward(1, 0)
+            load_pre(3, 0, 2)
+            dh_second(0, 1, "s")
+            relu_backward(1, 1)
+            load_grad(3, 0, 4)
+            load_pre(3, 2, 2)
+            dh_first(0, 3)
+            dh_second(0, 2, "s")
+            turn_wi(1, 1, "ss")
+            load_mask(0)
+            quantize_wi(1)
+            dh_second(0, 3, "s")
+            turn_dz2(1, 0, "ss")
+            turn_dz2(1, 1, "ss")
+            turn_x(0, "ss")
+            turn_x(1, "ss")
+            quantize_dz2(1, 0)
+            dh_first(1, 0)
+            dh_first(1, 1)
+            quantize_dz2(1, 1)
+            interleave_dz1(0)
+            dh_second(1, 0, "s")
+            dh_second(1, 1, "v")
+            dh_first(1, 2)
+            dh_first(1, 3)
+            relu_backward(2, 0)
+            dh_second(1, 2, "s")
+            dh_second(1, 3, "s")
+            turn_dz1(0, 0, "ss")
+            interleave_dz1(1)
+            quantize_dz1_m(0, 0)
+            quantize_dz1_m(0, 1)
+            relu_backward(2, 1)
+            turn_wi(2, 0, "ss")
+            turn_dz2(2, 0, "ss")
+            quantize_x()
+            turn_dz1(0, 1, "ss")
+            turn_wi(2, 1, "ss")
+            load_mask(1)
+            turn_wi(3, 0, "ss")
+            turn_dz2(2, 1, "ss")
+            quantize_wi(2)
+            turn_wi(3, 1, "ss")
+            quantize_dz2(2, 0)
+            output_0(0, 0, 0, "ss")
+            dh_first(2, 0)
+            dh_first(2, 1)
+            quantize_dz2(2, 1)
+            dh_second(2, 0, "s")
+            dh_first(2, 2)
+            relu_backward(3, 0)
+            relu_backward(3, 1)
+            dh_second(2, 1, "s")
+            dh_second(2, 2, "s")
+            output_0(0, 0, 1, "ss")
+            dh_first(2, 3)
+            dh_second(2, 3, "s")
+            turn_dz2(3, 0, "vs")
+            turn_dz2(3, 1, "ss")
+            quantize_wi(3)
+            quantize_dz2(3, 0)
+            quantize_dz2(3, 1)
+            turn_mask(0, 0, "ss")
+            turn_mask(0, 1, "ss")
+            interleave_dz1(2)
+            quantize_dz1_slots(0, 0)
+            dh_first(3, 0)
+            dh_first(3, 1)
+            dh_first(3, 2)
+            dh_second(3, 0, "s")
+            dh_first(3, 3)
+            dh_second(3, 1, "v")
+            dh_second(3, 2, "s")
+            dh_second(3, 3, "v")
+            output_0(0, 1, 0, "ss")
+            output_0(0, 1, 1, "ss")
+            turn_mask(1, 0, "ss")
+            interleave_dz1(3)
+            quantize_dz1_m(1, 0)
+            turn_dz1(1, 0, "vv")
+            output_0(1, 0, 0, "sv")
+            output_0(1, 0, 1, "ss")
+            quantize_dz1_m(1, 1)
+            quantize_mask(0)
+            turn_mask(1, 1, "sv")
+            quantize_dz1_slots(0, 1)
+            output_0(1, 1, 0, "ss")
+            output_0(1, 1, 1, "ss")
+            quantize_dz1_slots(1, 0)
+            quantize_mask(1)
+            turn_dz1(1, 1, "ss")
+            output_1_first(0, 0)
+            output_1_second(0, 0, "sv")
+            output_1_first(0, 1)
+            quantize_dz1_slots(1, 1)
+            output_1_second(0, 1, "sv")
+            output_1_first(1, 0)
+            output_1_second(1, 0, "sv")
+            output_1_first(1, 1)
+            output_1_second(1, 1, "sv")

@@ -19,11 +19,12 @@ N = 512
 PAIRS = E // 2
 
 BUFS = {
-    "pre": 4, "grad": 2, "weights": 3, "x": 1,
-    "dz2": 2, "grouped": 3, "x_grouped": 1,
+    "pre": 4, "grad": 2, "weights": 3,
+    "dz2": 3, "grouped": 4,
     "wi_codes": 2, "wi_scales": 2, "dz2_codes": 2, "dz2_scales": 2,
-    "dz1": 2, "dz1_by_m": 1, "dz1_by_slot": 2, "result": 6,
+    "dz1": 2, "dz1_by_m": 1, "dz1_by_slot": 3, "result": 6,
 }
+SHARES = {"x": "dz1_by_slot", "result_1": "pre"}
 
 
 def tile_flaxpositionwisemoelayer_pa_v_kernel(tc, dispatch_mask, x, wi, pre, grad_out, out_0, out_1):
@@ -40,7 +41,7 @@ def tile_flaxpositionwisemoelayer_pa_v_kernel(tc, dispatch_mask, x, wi, pre, gra
     with ExitStack() as ctx:
         keep = ctx.enter_context(tc.tile_pool(name="keep", bufs=1))
         ring = ctx.enter_context(tc.tile_pool(name="ring", bufs=1))
-        psum = ctx.enter_context(tc.psum_pool(name="psum", bufs=4))
+        psum = ctx.enter_context(tc.psum_pool(name="psum", bufs=8))
 
         ident = keep.tile([P, P], F32, name="ident")
         make_identity(nc, ident[:])
@@ -58,7 +59,8 @@ def tile_flaxpositionwisemoelayer_pa_v_kernel(tc, dispatch_mask, x, wi, pre, gra
 
         def ring_tile(kind, key, shape, dtype):
             if (kind, key) not in tiles:
-                tiles[kind, key] = ring.tile(shape, dtype, tag=kind, bufs=BUFS[kind], align_bytes=64, name=kind)
+                tag = SHARES.get(kind, kind)
+                tiles[kind, key] = ring.tile(shape, dtype, tag=tag, bufs=BUFS[tag], align_bytes=64, name=kind)
             return tiles[kind, key]
 
         def copy(engine, out, in_):
@@ -85,82 +87,91 @@ def tile_flaxpositionwisemoelayer_pa_v_kernel(tc, dispatch_mask, x, wi, pre, gra
             t = ring_tile("weights", ("mask", g), [P, 4, E * C], BF16)
             nc.sync.dma_start(out=t[:], in_=mask_rows[g])
 
-        def load_x():
-            t = ring_tile("x", 0, [P, G, 4, M], BF16)
-            nc.sync.dma_start(out=t[:], in_=x_rows)
+        def load_x(g):
+            t = ring_tile("x", g, [P, 4, M], BF16)
+            nc.sync.dma_start(out=t[:], in_=x_rows[:, g])
 
 
-        def turn(engine, source, grouped, block):
-            bank = psum.tile([P, 2, 2, P], F32, tag="turned", name="bank")
+        banks = {}
+
+        def empty(key, engine):
+            out, in_ = banks[key]()
+            copy(engine, out, in_)
+
+        def turn(key, source, grouped, block):
+            bank = psum.tile([P, 2, 2, P], F32, tag="bank", name="bank")
             for i in range(2):
                 for u in range(2):
                     nc.tensor.transpose(bank[:, i, u, :], source(i, u), ident[:])
-            words = grouped[:].bitcast(F32)[:, N * block : N * (block + 1)]
-            copy(engine, words.rearrange("p (i r u) -> p i r u", i=2, u=2), bank[:].rearrange("p i u r -> p i r u"))
+            banks[key] = lambda: (
+                grouped()[:].bitcast(F32)[:, N * block : N * (block + 1)].rearrange("p (i r u) -> p i r u", i=2, u=2),
+                bank[:].rearrange("p i u r -> p i r u"))
 
-        def turn_row(engine, row, grouped, block):
-            words = row.bitcast(F32)
-            turn(engine, lambda i, u: words[:, 256 * i + u : 256 * (i + 1) : 2], grouped, block)
+        def turn_row(kind, index, row):
+            words = tiles["weights", (kind, index)][:, row, :].bitcast(F32)
+            turn((kind, index, row), lambda i, u: words[:, 256 * i + u : 256 * (i + 1) : 2],
+                 lambda: ring_tile("grouped", (kind, index), [P, 4096], BF16), row)
 
-        def turn_wi(e, half, engines):
-            for t in range(2):
-                row = 2 * half + t
-                grouped = ring_tile("grouped", ("wi", e), [P, 4096], BF16)
-                turn_row(engines[t], tiles["weights", ("wi", e)][:, row, :], grouped, row)
+        def turn_x(g, h):
+            rows = tiles["x", g]
+            turn(("x", g, h), lambda i, u: rows[:, 2 * h + i, :].bitcast(F32)[:, u::2],
+                 lambda: ring_tile("grouped", "x", [P, 4096], BF16), 2 * g + h)
 
-        def turn_mask(g, half, engines):
-            for t in range(2):
-                row = 2 * half + t
-                grouped = ring_tile("grouped", ("mask", g), [P, 4096], BF16)
-                turn_row(engines[t], tiles["weights", ("mask", g)][:, row, :], grouped, row)
-
-        def turn_x(g, engines):
-            rows = tiles["x", 0]
-            for h in range(2):
-                grouped = ring_tile("x_grouped", 0, [P, 4096], BF16)
-                turn(engines[h], lambda i, u: rows[:, g, 2 * h + i, :].bitcast(F32)[:, u::2], grouped, 2 * g + h)
-
-        def turn_dz2(e, half, engines):
-            dz2 = tiles["dz2", (e, half)]
+        def turn_dz2(e, j):
+            dz2 = tiles["dz2", (e, j // 2)]
+            bank = psum.tile([P, 2, 2, P], F32, tag="bank", name="bank")
             for a in range(2):
-                grouped = ring_tile("grouped", ("dz2", e), [P, 4096], BF16)
-                turn(engines[a], lambda i, u: dz2[:, u, i, 256 * a : 256 * (a + 1)].bitcast(F32), grouped, 2 * a + half)
+                for u in range(2):
+                    nc.tensor.transpose(bank[:, a, u, :], dz2[:, u, j % 2, 256 * a : 256 * (a + 1)].bitcast(F32), ident[:])
+            banks["dz2", e, j] = lambda: (
+                ring_tile("grouped", ("dz2", e), [P, 4096], BF16)[:].bitcast(F32).rearrange(
+                    "p (a j r u) -> p a j r u", a=2, j=4, u=2)[:, :, j],
+                bank[:].rearrange("p a u r -> p a r u"))
 
-        def turn_dz1(pair, g, engines):
+        def turn_dz1(pair, g, h):
             dz1 = tiles["dz1", pair]
-            for h in range(2):
-                grouped = ring_tile("dz1_by_slot", (pair, g), [P, 2048], BF16)
-                turn(engines[h], lambda i, u: dz1[:, 2 * h + i, g, u, :].bitcast(F32), grouped, h)
+            turn(("slots", pair, g, h), lambda i, u: dz1[:, 2 * h + i, g, u, :].bitcast(F32),
+                 lambda: ring_tile("dz1_by_slot", (pair, g), [P, 2048], BF16), h)
 
 
-        def relu_backward(e, half):
+        def relu_backward(e, j, n):
+            half, first = divmod(j, 2)
             dz2 = ring_tile("dz2", (e, half), [P, 2, 2, N], BF16)
-            pre_words = tiles["pre", (e, half)][:].rearrange("p j (k u b) -> p u j k b", u=2, b=2)
-            grad = tiles["grad", e][:, 2 * half : 2 * half + 2, :].rearrange("p j (k u b) -> p u j k b", u=2, b=2)
+            pre_words = tiles["pre", (e, half)][:, first : first + n, :].rearrange("p j (k u b) -> p u j k b", u=2, b=2)
+            grad = tiles["grad", e][:, j : j + n, :].rearrange("p j (k u b) -> p u j k b", u=2, b=2)
             for u in range(2):
                 nc.vector.scalar_tensor_tensor(
-                    out=dz2[:, u].rearrange("p j (k b) -> p j k b", b=2),
+                    out=dz2[:, u, first : first + n].rearrange("p j (k b) -> p j k b", b=2),
                     in0=pre_words[:, u], scalar=0.0, in1=grad[:, u], op0=ALU.is_gt, op1=ALU.mult)
 
-        def quantize_wi(e):
+        def quantize_wi(e, row, n):
             codes = ring_tile("wi_codes", e, [P, 2 * M], U32)
             scales = ring_tile("wi_scales", e, [P, 2 * M], U8)
-            nc.vector.quantize_mx(out=codes[:].bitcast(E4M3), scales=scales[:], in_=tiles["grouped", ("wi", e)][:])
+            cols = slice(256 * row, 256 * (row + n))
+            nc.vector.quantize_mx(
+                out=codes[:, cols].bitcast(E4M3), scales=scales[:, cols],
+                in_=tiles["grouped", ("wi", e)][:, 1024 * row : 1024 * (row + n)])
 
-        def quantize_dz2(e, a):
+        def quantize_dz2(e, j, n):
             codes = ring_tile("dz2_codes", e, [P, 2 * N], U32)
             scales = ring_tile("dz2_scales", e, [P, 2 * N], U8)
-            cols = slice(N * a, N * (a + 1))
-            nc.vector.quantize_mx(
-                out=codes[:, cols].bitcast(E5M2), scales=scales[:, cols],
-                in_=tiles["grouped", ("dz2", e)][:, 4 * N * a : 4 * N * (a + 1)])
+            for a in range(2):
+                cols = slice(N * a + P * j, N * a + P * (j + n))
+                nc.vector.quantize_mx(
+                    out=codes[:, cols].bitcast(E5M2), scales=scales[:, cols],
+                    in_=tiles["grouped", ("dz2", e)][:, 4 * cols.start : 4 * cols.stop])
 
-        def quantize_mask(g):
+        def quantize_mask(g, half):
+            cols = slice(N * half, N * (half + 1))
             nc.vector.quantize_mx(
-                out=mask_codes[:, g, :].bitcast(E4M3), scales=mask_scales[:, g, :], in_=tiles["grouped", ("mask", g)][:])
+                out=mask_codes[:, g, cols].bitcast(E4M3), scales=mask_scales[:, g, cols],
+                in_=tiles["grouped", ("mask", g)][:, 4 * cols.start : 4 * cols.stop])
 
-        def quantize_x():
-            nc.vector.quantize_mx(out=x_codes[:].bitcast(E4M3), scales=x_scales[:], in_=tiles["x_grouped", 0][:])
+        def quantize_x(g):
+            cols = slice(S * g, S * (g + 1))
+            nc.vector.quantize_mx(
+                out=x_codes[:, cols].bitcast(E4M3), scales=x_scales[:, cols],
+                in_=tiles["grouped", "x"][:, 4 * cols.start : 4 * cols.stop])
 
         def quantize_dz1_m(pair, g):
             by_m = tiles["dz1_by_m", pair][:, g].rearrange("p i u s t -> p (i u s t)")
@@ -173,206 +184,186 @@ def tile_flaxpositionwisemoelayer_pa_v_kernel(tc, dispatch_mask, x, wi, pre, gra
                 in_=tiles["dz1_by_slot", (pair, g)][:])
 
 
-        def dh_pass(e, t, a):
-            if a == 0:
-                tiles["dh", (e, t)] = psum.tile([P, N], F32, tag="sums", name="dh")
-            w_cols = slice(256 * t + P * a, 256 * t + P * (a + 1))
-            d_cols = slice(N * a, N * (a + 1))
-            nc.tensor.matmul_mx(
-                out=tiles["dh", (e, t)][:],
-                lhsT=tiles["wi_codes", e][:, w_cols].bitcast(E4M3), lhsT_scale=tiles["wi_scales", e][:, w_cols],
-                rhs=tiles["dz2_codes", e][:, d_cols].bitcast(E5M2), rhs_scale=tiles["dz2_scales", e][:, d_cols],
-                start=(a == 0), stop=(a == 1))
-
-        def dh_first(e, t):
-            dh_pass(e, t, 0)
-
-        def dh_second(e, t, engine):
-            dh_pass(e, t, 1)
+        def dh(e, t):
+            sums = psum.tile([P, N], F32, tag="bank", name="dh")
+            for a in range(2):
+                w_cols = slice(256 * t + P * a, 256 * t + P * (a + 1))
+                d_cols = slice(N * a, N * (a + 1))
+                nc.tensor.matmul_mx(
+                    out=sums[:],
+                    lhsT=tiles["wi_codes", e][:, w_cols].bitcast(E4M3), lhsT_scale=tiles["wi_scales", e][:, w_cols],
+                    rhs=tiles["dz2_codes", e][:, d_cols].bitcast(E5M2), rhs_scale=tiles["dz2_scales", e][:, d_cols],
+                    start=(a == 0), stop=(a == 1))
             pair, i = divmod(e, 2)
-            dz1 = ring_tile("dz1", pair, [P, 4, G, 2, 256], BF16)
-            copy(engine,
-                 dz1[:, t, :, :, P * i : P * (i + 1)].rearrange("p g u (q b) -> p g u q b", b=2),
-                 tiles["dh", (e, t)][:].rearrange("p (u b g q) -> p g u q b", u=2, b=2, g=2))
+            banks["dh", e, t] = lambda: (
+                ring_tile("dz1", pair, [P, 4, G, 2, 256], BF16)[:, t, :, :, P * i : P * (i + 1)].rearrange(
+                    "p g u (q b) -> p g u q b", b=2),
+                sums[:].rearrange("p (u b g q) -> p g u q b", u=2, b=2, g=2))
 
-        def interleave_dz1(e):
+        def interleave_dz1(e, groups):
             pair, i = divmod(e, 2)
             by_m = ring_tile("dz1_by_m", pair, [P, G, 2, 2, P, 4], BF16)
             nc.vector.tensor_copy(
-                out=by_m[:, :, i], in_=tiles["dz1", pair][:, :, :, :, P * i : P * (i + 1)].rearrange("p t g u s -> p g u s t"))
+                out=by_m[:, groups, i],
+                in_=tiles["dz1", pair][:, :, groups, :, P * i : P * (i + 1)].rearrange("p t g u s -> p g u s t"))
 
 
-        def output_0(pair, g, half, engines):
-            result = ring_tile("result", ("out_0", pair, g, half), [P, 2, N], F32)
-            for t in range(2):
-                acc = psum.tile([P, N], F32, tag="sums", name="acc")
-                cols = slice(S * g + P * (2 * half + t), S * g + P * (2 * half + t + 1))
-                nc.tensor.matmul_mx(
-                    out=acc[:], lhsT=x_codes[:, cols].bitcast(E4M3), lhsT_scale=x_scales[:, cols],
-                    rhs=dz1_m_codes[:, pair, g, :].bitcast(E5M2), rhs_scale=dz1_m_scales[:, pair, g, :],
-                    start=True, stop=True)
-                copy(engines[t],
-                     result[:, t, :].rearrange("p (i q u b) -> p i q u b", i=2, u=2, b=2),
-                     acc[:].rearrange("p (i u q b) -> p i q u b", i=2, u=2, b=2))
-            nc.sync.dma_start(out=out0_rows[g, :, 2 * half : 2 * half + 2, N * pair : N * (pair + 1)], in_=result[:])
-
-        def out1_pass(g, row, pair):
-            if pair == 0:
-                tiles["out_1", (g, row)] = psum.tile([P, N], F32, tag="sums" if g == 0 else "turned", name="acc1")
-            cols = slice(256 * row + P * pair, 256 * row + P * (pair + 1))
+        def output_0(pair, g, row):
+            half, t = divmod(row, 2)
+            acc = psum.tile([P, N], F32, tag="bank", name="acc")
+            cols = slice(S * g + P * row, S * g + P * (row + 1))
             nc.tensor.matmul_mx(
-                out=tiles["out_1", (g, row)][:],
-                lhsT=mask_codes[:, g, cols].bitcast(E4M3), lhsT_scale=mask_scales[:, g, cols],
-                rhs=dz1_k_codes[:, pair, g, :].bitcast(E5M2), rhs_scale=dz1_k_scales[:, pair, g, :],
-                start=(pair == 0), stop=(pair == 1))
+                out=acc[:], lhsT=x_codes[:, cols].bitcast(E4M3), lhsT_scale=x_scales[:, cols],
+                rhs=dz1_m_codes[:, pair, g, :].bitcast(E5M2), rhs_scale=dz1_m_scales[:, pair, g, :],
+                start=True, stop=True)
+            banks["out_0", pair, g, row] = lambda: (
+                ring_tile("result", ("out_0", pair, g, half), [P, 2, N], F32)[:, t, :].rearrange(
+                    "p (i q u b) -> p i q u b", i=2, u=2, b=2),
+                acc[:].rearrange("p (i u q b) -> p i q u b", i=2, u=2, b=2))
 
-        def output_1_first(g, half):
-            for t in range(2):
-                out1_pass(g, 2 * half + t, 0)
+        def store_0(pair, g, half):
+            nc.sync.dma_start(
+                out=out0_rows[g, :, 2 * half : 2 * half + 2, N * pair : N * (pair + 1)],
+                in_=tiles["result", ("out_0", pair, g, half)][:])
 
-        def output_1_second(g, half, engines):
-            result = ring_tile("result", ("out_1", g, half), [P, 2, N], F32)
-            for t in range(2):
-                row = 2 * half + t
-                out1_pass(g, row, 1)
-                copy(engines[t],
-                     result[:, t, :].rearrange("p (m t) -> p m t", t=4),
-                     tiles["out_1", (g, row)][:].rearrange("p (t m) -> p m t", t=4))
-                if (g, half) == (G - 1, 1):
-                    nc.sync.dma_start(out=out1_rows[g, :, row, :], in_=result[:, t, :])
-            if (g, half) != (G - 1, 1):
-                nc.sync.dma_start(out=out1_rows[g, :, 2 * half : 2 * half + 2, :], in_=result[:])
+        def output_1(g, row):
+            acc = psum.tile([P, N], F32, tag="bank", name="acc1")
+            for pair in range(PAIRS):
+                cols = slice(256 * row + P * pair, 256 * row + P * (pair + 1))
+                nc.tensor.matmul_mx(
+                    out=acc[:],
+                    lhsT=mask_codes[:, g, cols].bitcast(E4M3), lhsT_scale=mask_scales[:, g, cols],
+                    rhs=dz1_k_codes[:, pair, g, :].bitcast(E5M2), rhs_scale=dz1_k_scales[:, pair, g, :],
+                    start=(pair == 0), stop=(pair == 1))
+            banks["out_1", g, row] = lambda: (
+                ring_tile("result_1", g, [P, 4, N], F32)[:, row, :].rearrange("p (m t) -> p m t", t=4),
+                acc[:].rearrange("p (t m) -> p m t", t=4))
+
+        def store_1(g, row, n):
+            nc.sync.dma_start(out=out1_rows[g, :, row : row + n, :], in_=tiles["result_1", g][:, row : row + n, :])
+
+
+        def rows(kind, index, first, n):
+            return [(kind, index, r) for r in range(first, first + n)]
+
+        def emptied(steps):
+            return [("empty", s) for s in steps]
+
+        def gives(step):
+            kind = step[0]
+            if kind in ("load_pre", "load_grad", "load_wi", "relu", "q_wi", "q_dz2"):
+                return rows(kind, step[1], step[2], step[3])
+            if kind == "interleave":
+                return rows(kind, step[1], step[2], step[3])
+            return [step]
+
+        def needs(step):
+            kind = step[0]
+            if kind == "empty":
+                return [step[1]] + reuse(step[1])
+            if kind == "load_pre":
+                e, j = step[1:3]
+                old = 2 * e + j // 2 - BUFS["pre"]
+                return rows("relu", old // 2, 2 * (old % 2), 2) if old >= 0 else []
+            if kind == "load_grad":
+                old = step[1] - BUFS["grad"]
+                return rows("relu", old, 0, 4) if old >= 0 else []
+            if kind == "load_wi":
+                old = step[1] - BUFS["weights"]
+                return rows("wi", old, 0, 4) if old >= 0 else []
+            if kind == "load_mask":
+                return rows("wi", E + step[1] - BUFS["weights"], 0, 4)
+            if kind == "load_x":
+                return []
+            if kind == "relu":
+                e, j, n = step[1:]
+                old = 2 * e + j // 2 - BUFS["dz2"]
+                return (rows("load_pre", e, j, n) + rows("load_grad", e, j, n)
+                        + (rows("dz2", old // 2, 2 * (old % 2), 2) if old >= 0 else []))
+            if kind == "wi":
+                return [("load_wi", step[1], step[2])]
+            if kind == "mask":
+                return [("load_mask", step[1])]
+            if kind == "x":
+                return [("load_x", step[1])]
+            if kind == "dz2":
+                return [("relu", step[1], step[2])]
+            if kind == "q_wi":
+                old = step[1] - BUFS["wi_codes"]
+                return emptied(rows("wi", *step[1:])) + (rows("dh", old, 0, 4) if old >= 0 else [])
+            if kind == "q_dz2":
+                old = step[1] - BUFS["dz2_codes"]
+                return emptied(rows("dz2", *step[1:])) + (rows("dh", old, 0, 4) if old >= 0 else [])
+            if kind == "q_x":
+                return emptied(rows("x", step[1], 0, 2))
+            if kind == "q_mask":
+                return emptied(rows("mask", step[1], 2 * step[2], 2))
+            if kind == "dh":
+                return rows("q_dz2", step[1], 0, 4) + [("q_wi", step[1], step[2])]
+            if kind == "interleave":
+                return emptied(rows("dh", step[1], 0, 4)) + ([("q_m", 0, 0), ("q_m", 0, 1)] if step[1] >= 2 else [])
+            if kind == "q_m":
+                return [("interleave", 2 * step[1] + i, step[2]) for i in range(2)]
+            if kind == "slots":
+                pair, g, h = step[1:]
+                return emptied(rows("dh", 2 * pair, 2 * h, 2) + rows("dh", 2 * pair + 1, 2 * h, 2))
+            if kind == "q_k":
+                return emptied([("slots", step[1], step[2], h) for h in range(2)])
+            if kind == "out_0":
+                return [("q_x", step[2]), ("q_m", step[1], step[2])]
+            if kind == "out_1":
+                return [("q_mask", step[1], step[2] // 2), ("q_k", 0, step[1]), ("q_k", 1, step[1])]
+            if kind == "store_0":
+                pair, g, half = step[1:]
+                return emptied([("out_0", pair, g, 2 * half + t) for t in range(2)])
+            return emptied(rows("out_1", *step[1:]))
+
+        def reuse(step):
+            if step[:3] == ("out_0", 1, 1):
+                return [("store_0", 0, 0, step[3] // 2)]
+            if step[:3] == ("slots", 1, 1):
+                return [("q_k", 0, 0)]
+            return []
+
+        calls = {
+            "load_pre": load_pre, "load_grad": load_grad, "load_wi": load_wi, "load_mask": load_mask, "load_x": load_x,
+            "relu": relu_backward, "x": turn_x, "dz2": turn_dz2, "slots": turn_dz1,
+            "wi": lambda e, row: turn_row("wi", e, row), "mask": lambda g, row: turn_row("mask", g, row),
+            "q_wi": quantize_wi, "q_dz2": quantize_dz2, "q_x": quantize_x, "q_mask": quantize_mask,
+            "q_m": quantize_dz1_m, "q_k": quantize_dz1_slots, "dh": dh,
+            "interleave": lambda e, g, n: interleave_dz1(e, slice(g, g + n)),
+            "out_0": output_0, "out_1": output_1, "store_0": store_0, "store_1": store_1,
+        }
+
+        def write_program(queues):
+            done = set()
+            filled = []
+            at = {name: 0 for name in queues}
+            left = sum(len(q) for q in queues.values())
+            while left:
+                before = left
+                for name, queue in queues.items():
+                    while at[name] < len(queue):
+                        step = queue[at[name]]
+                        wanted = needs(step)
+                        if name == "tensor" and len(filled) >= 8:
+                            wanted = wanted + [("empty", filled[-8])]
+                        if not all(w in done for w in wanted):
+                            break
+                        if step[0] == "empty":
+                            empty(step[1], name)
+                        else:
+                            calls[step[0]](*step[1:])
+                        if name == "tensor":
+                            filled.append(step)
+                        for w in gives(step):
+                            done.add(w)
+                        at[name] = at[name] + 1
+                        left = left - 1
+                assert left < before, [q[at[n]] for n, q in queues.items() if at[n] < len(q)]
 
         with tc.manual_schedule():
-            load_wi(0, 0, 2)
-            load_pre(0, 0, 1)
-            load_grad(0, 0, 1)
-            load_pre(0, 1, 1)
-            load_grad(0, 1, 1)
-            load_pre(0, 2, 2)
-            load_grad(0, 2, 2)
-            load_wi(0, 2, 2)
-            load_grad(1, 0, 4)
-            load_wi(1, 0, 4)
-            load_pre(1, 0, 2)
-            load_pre(1, 2, 2)
-            load_x()
-            turn_wi(0, 0, "ss")
-            relu_backward(0, 0)
-            relu_backward(0, 1)
-            load_grad(2, 0, 4)
-            load_pre(2, 0, 2)
-            load_wi(2, 0, 4)
-            load_pre(2, 2, 2)
-            turn_wi(0, 1, "sv")
-            load_wi(3, 0, 4)
-            turn_dz2(0, 0, "vv")
-            quantize_wi(0)
-            turn_dz2(0, 1, "ss")
-            quantize_dz2(0, 0)
-            turn_wi(1, 0, "ss")
-            dh_first(0, 0)
-            dh_first(0, 1)
-            quantize_dz2(0, 1)
-            dh_second(0, 0, "s")
-            dh_first(0, 2)
-            relu_backward(1, 0)
-            load_pre(3, 0, 2)
-            dh_second(0, 1, "s")
-            relu_backward(1, 1)
-            load_grad(3, 0, 4)
-            load_pre(3, 2, 2)
-            dh_first(0, 3)
-            dh_second(0, 2, "s")
-            turn_wi(1, 1, "ss")
-            load_mask(0)
-            quantize_wi(1)
-            dh_second(0, 3, "s")
-            turn_dz2(1, 0, "ss")
-            turn_dz2(1, 1, "ss")
-            turn_x(0, "ss")
-            turn_x(1, "ss")
-            quantize_dz2(1, 0)
-            dh_first(1, 0)
-            dh_first(1, 1)
-            quantize_dz2(1, 1)
-            interleave_dz1(0)
-            dh_second(1, 0, "s")
-            dh_second(1, 1, "v")
-            dh_first(1, 2)
-            dh_first(1, 3)
-            relu_backward(2, 0)
-            dh_second(1, 2, "s")
-            dh_second(1, 3, "s")
-            turn_dz1(0, 0, "ss")
-            interleave_dz1(1)
-            quantize_dz1_m(0, 0)
-            quantize_dz1_m(0, 1)
-            relu_backward(2, 1)
-            turn_wi(2, 0, "ss")
-            turn_dz2(2, 0, "ss")
-            quantize_x()
-            turn_dz1(0, 1, "ss")
-            turn_wi(2, 1, "ss")
-            load_mask(1)
-            turn_wi(3, 0, "ss")
-            turn_dz2(2, 1, "ss")
-            quantize_wi(2)
-            turn_wi(3, 1, "ss")
-            quantize_dz2(2, 0)
-            output_0(0, 0, 0, "ss")
-            dh_first(2, 0)
-            dh_first(2, 1)
-            quantize_dz2(2, 1)
-            dh_second(2, 0, "s")
-            dh_first(2, 2)
-            relu_backward(3, 0)
-            relu_backward(3, 1)
-            dh_second(2, 1, "s")
-            dh_second(2, 2, "s")
-            output_0(0, 0, 1, "ss")
-            dh_first(2, 3)
-            dh_second(2, 3, "s")
-            turn_dz2(3, 0, "vs")
-            turn_dz2(3, 1, "ss")
-            quantize_wi(3)
-            quantize_dz2(3, 0)
-            quantize_dz2(3, 1)
-            turn_mask(0, 0, "ss")
-            turn_mask(0, 1, "ss")
-            interleave_dz1(2)
-            quantize_dz1_slots(0, 0)
-            dh_first(3, 0)
-            dh_first(3, 1)
-            dh_first(3, 2)
-            dh_second(3, 0, "s")
-            dh_first(3, 3)
-            dh_second(3, 1, "v")
-            dh_second(3, 2, "s")
-            dh_second(3, 3, "v")
-            output_0(0, 1, 0, "ss")
-            output_0(0, 1, 1, "ss")
-            turn_mask(1, 0, "ss")
-            interleave_dz1(3)
-            quantize_dz1_m(1, 0)
-            turn_dz1(1, 0, "vv")
-            output_0(1, 0, 0, "sv")
-            output_0(1, 0, 1, "ss")
-            quantize_dz1_m(1, 1)
-            quantize_mask(0)
-            turn_mask(1, 1, "sv")
-            quantize_dz1_slots(0, 1)
-            output_0(1, 1, 0, "ss")
-            output_0(1, 1, 1, "ss")
-            quantize_dz1_slots(1, 0)
-            quantize_mask(1)
-            turn_dz1(1, 1, "ss")
-            output_1_first(0, 0)
-            output_1_second(0, 0, "sv")
-            output_1_first(0, 1)
-            quantize_dz1_slots(1, 1)
-            output_1_second(0, 1, "sv")
-            output_1_first(1, 0)
-            output_1_second(1, 0, "sv")
-            output_1_first(1, 1)
-            output_1_second(1, 1, "sv")
+            write_program({"sync": [("load_grad", 0, 0, 1), ("load_pre", 0, 0, 1), ("load_grad", 0, 1, 1), ("load_pre", 0, 1, 1), ("load_grad", 0, 2, 2), ("load_pre", 0, 2, 1), ("load_pre", 0, 3, 1), ("load_wi", 0, 0, 2), ("load_wi", 0, 2, 2), ("load_x", 0), ("load_x", 1), ("load_grad", 1, 0, 4), ("load_pre", 1, 0, 2), ("load_pre", 1, 2, 2), ("load_wi", 1, 0, 2), ("load_wi", 1, 2, 2), ("load_grad", 2, 0, 4), ("load_pre", 2, 0, 2), ("load_pre", 2, 2, 2), ("load_wi", 2, 0, 4), ("load_grad", 3, 0, 4), ("load_pre", 3, 0, 2), ("load_pre", 3, 2, 2), ("load_wi", 3, 0, 2), ("load_wi", 3, 2, 2), ("load_mask", 0), ("load_mask", 1), ("store_0", 0, 0, 0), ("store_0", 0, 0, 1), ("store_0", 0, 1, 0), ("store_0", 0, 1, 1), ("store_0", 1, 0, 0), ("store_0", 1, 0, 1), ("store_0", 1, 1, 0), ("store_0", 1, 1, 1), ("store_1", 0, 0, 2), ("store_1", 0, 2, 2), ("store_1", 1, 0, 2), ("store_1", 1, 2, 1), ("store_1", 1, 3, 1)],
+                "v": [("relu", 0, 0, 1), ("relu", 0, 1, 1), ("relu", 0, 2, 1), ("relu", 0, 3, 1), ("q_dz2", 0, 0, 2), ("q_dz2", 0, 2, 1), ("q_dz2", 0, 3, 1), ("q_wi", 0, 0, 2), ("q_wi", 0, 2, 2), ("q_x", 0), ("relu", 1, 0, 1), ("relu", 1, 1, 1), ("relu", 1, 2, 1), ("relu", 1, 3, 1), ("interleave", 0, 0, 2), ("q_dz2", 1, 0, 2), ("q_dz2", 1, 2, 1), ("q_wi", 1, 0, 2), ("q_dz2", 1, 3, 1), ("q_x", 1), ("q_wi", 1, 2, 2), ("relu", 2, 0, 1), ("relu", 2, 1, 1), ("relu", 2, 2, 1), ("interleave", 1, 0, 2), ("relu", 2, 3, 1), ("q_m", 0, 0), ("q_dz2", 2, 0, 2), ("q_dz2", 2, 2, 1), ("q_wi", 2, 0, 2), ("q_dz2", 2, 3, 1), ("q_wi", 2, 2, 2), ("relu", 3, 0, 1), ("relu", 3, 1, 1), ("relu", 3, 2, 1), ("relu", 3, 3, 1), ("q_dz2", 3, 0, 2), ("q_dz2", 3, 2, 1), ("q_wi", 3, 0, 2), ("q_dz2", 3, 3, 1), ("q_wi", 3, 2, 1), ("q_m", 0, 1), ("q_wi", 3, 3, 1), ("interleave", 2, 0, 2), ("empty", ("dh", 3, 1)), ("interleave", 3, 0, 1), ("q_k", 0, 0), ("q_m", 1, 0), ("interleave", 3, 1, 1), ("empty", ("out_0", 1, 0, 1)), ("q_m", 1, 1), ("empty", ("out_0", 1, 0, 3)), ("q_mask", 0, 0), ("q_mask", 0, 1), ("empty", ("slots", 1, 0, 1)), ("empty", ("out_0", 1, 1, 1)), ("empty", ("out_0", 1, 1, 3)), ("q_k", 1, 0), ("empty", ("slots", 0, 1, 1)), ("empty", ("slots", 1, 1, 1)), ("q_k", 0, 1), ("q_k", 1, 1), ("q_mask", 1, 0), ("q_mask", 1, 1), ("empty", ("out_1", 0, 3)), ("empty", ("out_1", 1, 1)), ("empty", ("out_1", 1, 3))],
+                "tensor": [("dz2", 0, 0), ("dz2", 0, 1), ("dz2", 0, 2), ("wi", 0, 0), ("dz2", 0, 3), ("wi", 0, 1), ("wi", 0, 2), ("wi", 0, 3), ("x", 0, 0), ("x", 0, 1), ("dh", 0, 0), ("x", 1, 0), ("dh", 0, 1), ("x", 1, 1), ("dh", 0, 2), ("dh", 0, 3), ("dz2", 1, 0), ("dz2", 1, 1), ("dz2", 1, 2), ("wi", 1, 0), ("wi", 1, 1), ("dz2", 1, 3), ("wi", 1, 2), ("wi", 1, 3), ("dh", 1, 0), ("dh", 1, 1), ("dh", 1, 2), ("dh", 1, 3), ("dz2", 2, 0), ("dz2", 2, 1), ("slots", 0, 0, 0), ("dz2", 2, 2), ("slots", 0, 0, 1), ("wi", 2, 0), ("wi", 2, 1), ("dz2", 2, 3), ("wi", 2, 2), ("wi", 2, 3), ("out_0", 0, 0, 0), ("out_0", 0, 0, 1), ("dh", 2, 0), ("dh", 2, 1), ("dz2", 3, 0), ("dh", 2, 2), ("dz2", 3, 1), ("dh", 2, 3), ("dz2", 3, 2), ("wi", 3, 0), ("wi", 3, 1), ("dz2", 3, 3), ("wi", 3, 2), ("wi", 3, 3), ("out_0", 0, 0, 2), ("out_0", 0, 0, 3), ("dh", 3, 0), ("dh", 3, 1), ("dh", 3, 2), ("dh", 3, 3), ("out_0", 0, 1, 0), ("out_0", 0, 1, 1), ("out_0", 0, 1, 2), ("out_0", 0, 1, 3), ("mask", 0, 0), ("mask", 0, 1), ("mask", 0, 2), ("out_0", 1, 0, 0), ("out_0", 1, 0, 1), ("out_0", 1, 0, 2), ("out_0", 1, 0, 3), ("mask", 0, 3), ("slots", 1, 0, 0), ("slots", 1, 0, 1), ("out_0", 1, 1, 0), ("out_0", 1, 1, 1), ("out_0", 1, 1, 2), ("out_0", 1, 1, 3), ("mask", 1, 0), ("mask", 1, 1), ("slots", 0, 1, 0), ("slots", 0, 1, 1), ("out_1", 0, 0), ("out_1", 0, 1), ("slots", 1, 1, 0), ("slots", 1, 1, 1), ("mask", 1, 2), ("mask", 1, 3), ("out_1", 0, 2), ("out_1", 0, 3), ("out_1", 1, 0), ("out_1", 1, 1), ("out_1", 1, 2), ("out_1", 1, 3)],
+                "s": [("empty", ("dz2", 0, 0)), ("empty", ("dz2", 0, 1)), ("empty", ("dz2", 0, 2)), ("empty", ("wi", 0, 0)), ("empty", ("dz2", 0, 3)), ("empty", ("wi", 0, 1)), ("empty", ("wi", 0, 2)), ("empty", ("wi", 0, 3)), ("empty", ("x", 0, 0)), ("empty", ("x", 0, 1)), ("empty", ("dh", 0, 0)), ("empty", ("x", 1, 0)), ("empty", ("dh", 0, 1)), ("empty", ("x", 1, 1)), ("empty", ("dh", 0, 2)), ("empty", ("dh", 0, 3)), ("empty", ("dz2", 1, 0)), ("empty", ("dz2", 1, 1)), ("empty", ("dz2", 1, 2)), ("empty", ("wi", 1, 0)), ("empty", ("wi", 1, 1)), ("empty", ("dz2", 1, 3)), ("empty", ("wi", 1, 2)), ("empty", ("wi", 1, 3)), ("empty", ("dh", 1, 0)), ("empty", ("dh", 1, 1)), ("empty", ("dh", 1, 2)), ("empty", ("dh", 1, 3)), ("empty", ("dz2", 2, 0)), ("empty", ("dz2", 2, 1)), ("empty", ("slots", 0, 0, 0)), ("empty", ("dz2", 2, 2)), ("empty", ("slots", 0, 0, 1)), ("empty", ("wi", 2, 0)), ("empty", ("wi", 2, 1)), ("empty", ("dz2", 2, 3)), ("empty", ("wi", 2, 2)), ("empty", ("wi", 2, 3)), ("empty", ("out_0", 0, 0, 0)), ("empty", ("out_0", 0, 0, 1)), ("empty", ("dh", 2, 0)), ("empty", ("dh", 2, 1)), ("empty", ("dz2", 3, 0)), ("empty", ("dh", 2, 2)), ("empty", ("dz2", 3, 1)), ("empty", ("dh", 2, 3)), ("empty", ("dz2", 3, 2)), ("empty", ("wi", 3, 0)), ("empty", ("wi", 3, 1)), ("empty", ("dz2", 3, 3)), ("empty", ("wi", 3, 2)), ("empty", ("wi", 3, 3)), ("empty", ("out_0", 0, 0, 2)), ("empty", ("out_0", 0, 0, 3)), ("empty", ("dh", 3, 0)), ("empty", ("dh", 3, 2)), ("empty", ("dh", 3, 3)), ("empty", ("out_0", 0, 1, 0)), ("empty", ("out_0", 0, 1, 1)), ("empty", ("out_0", 0, 1, 2)), ("empty", ("out_0", 0, 1, 3)), ("empty", ("mask", 0, 0)), ("empty", ("mask", 0, 1)), ("empty", ("mask", 0, 2)), ("empty", ("out_0", 1, 0, 0)), ("empty", ("out_0", 1, 0, 2)), ("empty", ("mask", 0, 3)), ("empty", ("slots", 1, 0, 0)), ("empty", ("out_0", 1, 1, 0)), ("empty", ("out_0", 1, 1, 2)), ("empty", ("mask", 1, 0)), ("empty", ("mask", 1, 1)), ("empty", ("slots", 0, 1, 0)), ("empty", ("out_1", 0, 0)), ("empty", ("out_1", 0, 1)), ("empty", ("slots", 1, 1, 0)), ("empty", ("mask", 1, 2)), ("empty", ("mask", 1, 3)), ("empty", ("out_1", 0, 2)), ("empty", ("out_1", 1, 0)), ("empty", ("out_1", 1, 2))]})

@@ -19,12 +19,12 @@ N = 512
 PAIRS = E // 2
 
 BUFS = {
-    "pre": 4, "grad": 2, "weights": 3,
+    "pre": 4, "grad": 3, "weights": 3,
     "dz2": 3, "grouped": 4,
     "wi_codes": 2, "wi_scales": 2, "dz2_codes": 2, "dz2_scales": 2,
-    "dz1": 2, "dz1_by_m": 1, "dz1_by_slot": 3, "result": 6,
+    "dz1": 2, "dz1_by_m": 1, "dz1_by_slot": 2, "result": 4,
 }
-SHARES = {"x": "dz1_by_slot", "result_1": "pre"}
+SHARES = {"x": "dz1_by_slot", "result_1": "pre", "wi": "weights", "mask": "weights"}
 
 
 def tile_flaxpositionwisemoelayer_pa_v_kernel(tc, dispatch_mask, x, wi, pre, grad_out, out_0, out_1):
@@ -70,26 +70,30 @@ def tile_flaxpositionwisemoelayer_pa_v_kernel(tc, dispatch_mask, x, wi, pre, gra
                 nc.vector.tensor_copy(out=out, in_=in_)
 
 
+        pieces = {}
+
+        def piece(kind, e, j, n, shape, dtype):
+            t = ring_tile(kind, (e, j), shape, dtype)
+            for r in range(j, j + n):
+                pieces[kind, e, r] = (t, r - j)
+            return t
+
         def load_pre(e, j, n):
-            half, first = divmod(j, 2)
-            t = ring_tile("pre", (e, half), [P, 2, H], F32)
-            nc.sync.dma_start(out=t[:, first : first + n, :], in_=pre_rows[e, :, j : j + n, :])
+            nc.sync.dma_start(out=piece("pre", e, j, n, [P, n, H], F32)[:], in_=pre_rows[e, :, j : j + n, :])
 
         def load_grad(e, j, n):
-            t = ring_tile("grad", e, [P, 4, H], BF16)
-            nc.sync.dma_start(out=t[:, j : j + n, :], in_=grad_rows[e, :, j : j + n, :])
+            nc.sync.dma_start(out=piece("grad", e, j, n, [P, n, H], BF16)[:], in_=grad_rows[e, :, j : j + n, :])
 
         def load_wi(e, j, n):
-            t = ring_tile("weights", ("wi", e), [P, 4, H], BF16)
-            nc.sync.dma_start(out=t[:, j : j + n, :], in_=wi_rows[e, :, j : j + n, :])
+            nc.sync.dma_start(out=piece("wi", e, j, n, [P, n, H], BF16)[:], in_=wi_rows[e, :, j : j + n, :])
 
         def load_mask(g):
-            t = ring_tile("weights", ("mask", g), [P, 4, E * C], BF16)
+            t = piece("mask", g, 0, 4, [P, 4, E * C], BF16)
             nc.sync.dma_start(out=t[:], in_=mask_rows[g])
 
-        def load_x(g):
-            t = ring_tile("x", g, [P, 4, M], BF16)
-            nc.sync.dma_start(out=t[:], in_=x_rows[:, g])
+        def load_x():
+            t = ring_tile("x", 0, [P, G, 4, M], BF16)
+            nc.sync.dma_start(out=t[:], in_=x_rows)
 
 
         banks = {}
@@ -108,21 +112,22 @@ def tile_flaxpositionwisemoelayer_pa_v_kernel(tc, dispatch_mask, x, wi, pre, gra
                 bank[:].rearrange("p i u r -> p i r u"))
 
         def turn_row(kind, index, row):
-            words = tiles["weights", (kind, index)][:, row, :].bitcast(F32)
+            tile, at = pieces[kind, index, row]
+            words = tile[:, at, :].bitcast(F32)
             turn((kind, index, row), lambda i, u: words[:, 256 * i + u : 256 * (i + 1) : 2],
                  lambda: ring_tile("grouped", (kind, index), [P, 4096], BF16), row)
 
         def turn_x(g, h):
-            rows = tiles["x", g]
+            rows = tiles["x", 0][:, g]
             turn(("x", g, h), lambda i, u: rows[:, 2 * h + i, :].bitcast(F32)[:, u::2],
                  lambda: ring_tile("grouped", "x", [P, 4096], BF16), 2 * g + h)
 
         def turn_dz2(e, j):
-            dz2 = tiles["dz2", (e, j // 2)]
+            dz2, at = pieces["dz2", e, j]
             bank = psum.tile([P, 2, 2, P], F32, tag="bank", name="bank")
             for a in range(2):
                 for u in range(2):
-                    nc.tensor.transpose(bank[:, a, u, :], dz2[:, u, j % 2, 256 * a : 256 * (a + 1)].bitcast(F32), ident[:])
+                    nc.tensor.transpose(bank[:, a, u, :], dz2[:, u, at, 256 * a : 256 * (a + 1)].bitcast(F32), ident[:])
             banks["dz2", e, j] = lambda: (
                 ring_tile("grouped", ("dz2", e), [P, 4096], BF16)[:].bitcast(F32).rearrange(
                     "p (a j r u) -> p a j r u", a=2, j=4, u=2)[:, :, j],
@@ -131,17 +136,18 @@ def tile_flaxpositionwisemoelayer_pa_v_kernel(tc, dispatch_mask, x, wi, pre, gra
         def turn_dz1(pair, g, h):
             dz1 = tiles["dz1", pair]
             turn(("slots", pair, g, h), lambda i, u: dz1[:, 2 * h + i, g, u, :].bitcast(F32),
-                 lambda: ring_tile("dz1_by_slot", (pair, g), [P, 2048], BF16), h)
+                 lambda: ring_tile("dz1_by_slot", pair, [P, 4096], BF16), 2 * g + h)
 
 
         def relu_backward(e, j, n):
-            half, first = divmod(j, 2)
-            dz2 = ring_tile("dz2", (e, half), [P, 2, 2, N], BF16)
-            pre_words = tiles["pre", (e, half)][:, first : first + n, :].rearrange("p j (k u b) -> p u j k b", u=2, b=2)
-            grad = tiles["grad", e][:, j : j + n, :].rearrange("p j (k u b) -> p u j k b", u=2, b=2)
+            dz2 = piece("dz2", e, j, n, [P, 2, n, N], BF16)
+            pre_tile, pre_at = pieces["pre", e, j]
+            grad_tile, grad_at = pieces["grad", e, j]
+            pre_words = pre_tile[:, pre_at : pre_at + n, :].rearrange("p j (k u b) -> p u j k b", u=2, b=2)
+            grad = grad_tile[:, grad_at : grad_at + n, :].rearrange("p j (k u b) -> p u j k b", u=2, b=2)
             for u in range(2):
                 nc.vector.scalar_tensor_tensor(
-                    out=dz2[:, u, first : first + n].rearrange("p j (k b) -> p j k b", b=2),
+                    out=dz2[:, u].rearrange("p j (k b) -> p j k b", b=2),
                     in0=pre_words[:, u], scalar=0.0, in1=grad[:, u], op0=ALU.is_gt, op1=ALU.mult)
 
         def quantize_wi(e, row, n):
@@ -155,33 +161,34 @@ def tile_flaxpositionwisemoelayer_pa_v_kernel(tc, dispatch_mask, x, wi, pre, gra
         def quantize_dz2(e, j, n):
             codes = ring_tile("dz2_codes", e, [P, 2 * N], U32)
             scales = ring_tile("dz2_scales", e, [P, 2 * N], U8)
-            for a in range(2):
-                cols = slice(N * a + P * j, N * a + P * (j + n))
+            for cols in [slice(0, 2 * N)] if n == 4 else [slice(N * a + P * j, N * a + P * (j + n)) for a in range(2)]:
                 nc.vector.quantize_mx(
                     out=codes[:, cols].bitcast(E5M2), scales=scales[:, cols],
                     in_=tiles["grouped", ("dz2", e)][:, 4 * cols.start : 4 * cols.stop])
 
-        def quantize_mask(g, half):
-            cols = slice(N * half, N * (half + 1))
+        def quantize_mask(g, half, n):
+            cols = slice(N * half, N * (half + n))
             nc.vector.quantize_mx(
                 out=mask_codes[:, g, cols].bitcast(E4M3), scales=mask_scales[:, g, cols],
                 in_=tiles["grouped", ("mask", g)][:, 4 * cols.start : 4 * cols.stop])
 
-        def quantize_x(g):
-            cols = slice(S * g, S * (g + 1))
+        def quantize_x(g, n):
+            cols = slice(S * g, S * (g + n))
             nc.vector.quantize_mx(
                 out=x_codes[:, cols].bitcast(E4M3), scales=x_scales[:, cols],
                 in_=tiles["grouped", "x"][:, 4 * cols.start : 4 * cols.stop])
 
-        def quantize_dz1_m(pair, g):
-            by_m = tiles["dz1_by_m", pair][:, g].rearrange("p i u s t -> p (i u s t)")
+        def quantize_dz1_m(pair, g, n):
             nc.vector.quantize_mx(
-                out=dz1_m_codes[:, pair, g, :].bitcast(E5M2), scales=dz1_m_scales[:, pair, g, :], in_=by_m)
+                out=dz1_m_codes[:, pair, g : g + n, :].rearrange("p g w -> p (g w)").bitcast(E5M2),
+                scales=dz1_m_scales[:, pair, g : g + n, :].rearrange("p g w -> p (g w)"),
+                in_=tiles["dz1_by_m", pair][:, g : g + n].rearrange("p g i u s t -> p (g i u s t)"))
 
-        def quantize_dz1_slots(pair, g):
+        def quantize_dz1_slots(pair, g, n):
             nc.vector.quantize_mx(
-                out=dz1_k_codes[:, pair, g, :].bitcast(E5M2), scales=dz1_k_scales[:, pair, g, :],
-                in_=tiles["dz1_by_slot", (pair, g)][:])
+                out=dz1_k_codes[:, pair, g : g + n, :].rearrange("p g w -> p (g w)").bitcast(E5M2),
+                scales=dz1_k_scales[:, pair, g : g + n, :].rearrange("p g w -> p (g w)"),
+                in_=tiles["dz1_by_slot", pair][:, 2048 * g : 2048 * (g + n)])
 
 
         def dh(e, t):
@@ -204,8 +211,8 @@ def tile_flaxpositionwisemoelayer_pa_v_kernel(tc, dispatch_mask, x, wi, pre, gra
             pair, i = divmod(e, 2)
             by_m = ring_tile("dz1_by_m", pair, [P, G, 2, 2, P, 4], BF16)
             nc.vector.tensor_copy(
-                out=by_m[:, groups, i],
-                in_=tiles["dz1", pair][:, :, groups, :, P * i : P * (i + 1)].rearrange("p t g u s -> p g u s t"))
+                out=by_m[:, groups, i].rearrange("p g u (c n) t -> p g u c t n", n=4),
+                in_=tiles["dz1", pair][:, :, groups, :, P * i : P * (i + 1)].rearrange("p t g u (c n) -> p g u c t n", n=4))
 
 
         def output_0(pair, g, row):
@@ -253,39 +260,31 @@ def tile_flaxpositionwisemoelayer_pa_v_kernel(tc, dispatch_mask, x, wi, pre, gra
             kind = step[0]
             if kind in ("load_pre", "load_grad", "load_wi", "relu", "q_wi", "q_dz2"):
                 return rows(kind, step[1], step[2], step[3])
-            if kind == "interleave":
+            if kind in ("interleave", "q_m", "q_mask", "q_k"):
                 return rows(kind, step[1], step[2], step[3])
+            if kind == "q_x":
+                return [(kind, g) for g in range(step[1], step[1] + step[2])]
+            if kind == "warm":
+                return [("empty", step)]
             return [step]
 
         def needs(step):
             kind = step[0]
             if kind == "empty":
                 return [step[1]] + reuse(step[1])
-            if kind == "load_pre":
-                e, j = step[1:3]
-                old = 2 * e + j // 2 - BUFS["pre"]
-                return rows("relu", old // 2, 2 * (old % 2), 2) if old >= 0 else []
-            if kind == "load_grad":
-                old = step[1] - BUFS["grad"]
-                return rows("relu", old, 0, 4) if old >= 0 else []
-            if kind == "load_wi":
-                old = step[1] - BUFS["weights"]
-                return rows("wi", old, 0, 4) if old >= 0 else []
-            if kind == "load_mask":
-                return rows("wi", E + step[1] - BUFS["weights"], 0, 4)
-            if kind == "load_x":
+            if kind in ("load_pre", "load_grad", "load_wi", "load_mask"):
+                return readers_of_replaced(step)
+            if kind in ("load_x", "warm"):
                 return []
             if kind == "relu":
                 e, j, n = step[1:]
-                old = 2 * e + j // 2 - BUFS["dz2"]
-                return (rows("load_pre", e, j, n) + rows("load_grad", e, j, n)
-                        + (rows("dz2", old // 2, 2 * (old % 2), 2) if old >= 0 else []))
+                return rows("load_pre", e, j, n) + rows("load_grad", e, j, n) + readers_of_replaced(step)
             if kind == "wi":
                 return [("load_wi", step[1], step[2])]
             if kind == "mask":
                 return [("load_mask", step[1])]
             if kind == "x":
-                return [("load_x", step[1])]
+                return [("load_x",)]
             if kind == "dz2":
                 return [("relu", step[1], step[2])]
             if kind == "q_wi":
@@ -295,20 +294,20 @@ def tile_flaxpositionwisemoelayer_pa_v_kernel(tc, dispatch_mask, x, wi, pre, gra
                 old = step[1] - BUFS["dz2_codes"]
                 return emptied(rows("dz2", *step[1:])) + (rows("dh", old, 0, 4) if old >= 0 else [])
             if kind == "q_x":
-                return emptied(rows("x", step[1], 0, 2))
+                return emptied([("x", g, h) for g in range(step[1], step[1] + step[2]) for h in range(2)])
             if kind == "q_mask":
-                return emptied(rows("mask", step[1], 2 * step[2], 2))
+                return emptied(rows("mask", step[1], 2 * step[2], 2 * step[3]))
             if kind == "dh":
                 return rows("q_dz2", step[1], 0, 4) + [("q_wi", step[1], step[2])]
             if kind == "interleave":
                 return emptied(rows("dh", step[1], 0, 4)) + ([("q_m", 0, 0), ("q_m", 0, 1)] if step[1] >= 2 else [])
             if kind == "q_m":
-                return [("interleave", 2 * step[1] + i, step[2]) for i in range(2)]
+                return rows("interleave", 2 * step[1], step[2], step[3]) + rows("interleave", 2 * step[1] + 1, step[2], step[3])
             if kind == "slots":
                 pair, g, h = step[1:]
                 return emptied(rows("dh", 2 * pair, 2 * h, 2) + rows("dh", 2 * pair + 1, 2 * h, 2))
             if kind == "q_k":
-                return emptied([("slots", step[1], step[2], h) for h in range(2)])
+                return emptied([("slots", step[1], g, h) for g in range(step[2], step[2] + step[3]) for h in range(2)])
             if kind == "out_0":
                 return [("q_x", step[2]), ("q_m", step[1], step[2])]
             if kind == "out_1":
@@ -318,14 +317,29 @@ def tile_flaxpositionwisemoelayer_pa_v_kernel(tc, dispatch_mask, x, wi, pre, gra
                 return emptied([("out_0", pair, g, 2 * half + t) for t in range(2)])
             return emptied(rows("out_1", *step[1:]))
 
+        def readers_of_replaced(step):
+            tag, reader = {"load_pre": ("pre", "relu"), "load_grad": ("grad", "relu"), "load_wi": ("weights", "wi"),
+                           "load_mask": ("weights", "wi"), "relu": ("dz2", "dz2")}[step[0]]
+            line = lines.setdefault(tag, [])
+            if step not in line:
+                line.append(step)
+            back = line.index(step) - BUFS[tag]
+            return rows(reader, *line[back][1:]) if back >= 0 else []
+
+        lines = {}
+
         def reuse(step):
-            if step[:3] == ("out_0", 1, 1):
-                return [("store_0", 0, 0, step[3] // 2)]
-            if step[:3] == ("slots", 1, 1):
-                return [("q_k", 0, 0)]
+            if step[0] == "out_0":
+                back = 4 * step[1] + 2 * step[2] + step[3] // 2 - BUFS["result"]
+                return [("store_0", back // 4, back // 2 % 2, back % 2)] if back >= 0 else []
             return []
 
+        def warm(n):
+            bank = psum.tile([P, P], F32, tag="bank", name="warm")
+            nc.tensor.matmul(out=bank[:], lhsT=ident[:], rhs=ident[:], start=True, stop=True)
+
         calls = {
+            "warm": warm,
             "load_pre": load_pre, "load_grad": load_grad, "load_wi": load_wi, "load_mask": load_mask, "load_x": load_x,
             "relu": relu_backward, "x": turn_x, "dz2": turn_dz2, "slots": turn_dz1,
             "wi": lambda e, row: turn_row("wi", e, row), "mask": lambda g, row: turn_row("mask", g, row),
@@ -363,7 +377,7 @@ def tile_flaxpositionwisemoelayer_pa_v_kernel(tc, dispatch_mask, x, wi, pre, gra
                 assert left < before, [q[at[n]] for n, q in queues.items() if at[n] < len(q)]
 
         with tc.manual_schedule():
-            write_program({"sync": [("load_grad", 0, 0, 1), ("load_pre", 0, 0, 1), ("load_grad", 0, 1, 1), ("load_pre", 0, 1, 1), ("load_grad", 0, 2, 2), ("load_pre", 0, 2, 1), ("load_pre", 0, 3, 1), ("load_wi", 0, 0, 2), ("load_wi", 0, 2, 2), ("load_x", 0), ("load_x", 1), ("load_grad", 1, 0, 4), ("load_pre", 1, 0, 2), ("load_pre", 1, 2, 2), ("load_wi", 1, 0, 2), ("load_wi", 1, 2, 2), ("load_grad", 2, 0, 4), ("load_pre", 2, 0, 2), ("load_pre", 2, 2, 2), ("load_wi", 2, 0, 4), ("load_grad", 3, 0, 4), ("load_pre", 3, 0, 2), ("load_pre", 3, 2, 2), ("load_wi", 3, 0, 2), ("load_wi", 3, 2, 2), ("load_mask", 0), ("load_mask", 1), ("store_0", 0, 0, 0), ("store_0", 0, 0, 1), ("store_0", 0, 1, 0), ("store_0", 0, 1, 1), ("store_0", 1, 0, 0), ("store_0", 1, 0, 1), ("store_0", 1, 1, 0), ("store_0", 1, 1, 1), ("store_1", 0, 0, 2), ("store_1", 0, 2, 2), ("store_1", 1, 0, 2), ("store_1", 1, 2, 1), ("store_1", 1, 3, 1)],
-                "v": [("relu", 0, 0, 1), ("relu", 0, 1, 1), ("relu", 0, 2, 1), ("relu", 0, 3, 1), ("q_dz2", 0, 0, 2), ("q_dz2", 0, 2, 1), ("q_dz2", 0, 3, 1), ("q_wi", 0, 0, 2), ("q_wi", 0, 2, 2), ("q_x", 0), ("relu", 1, 0, 1), ("relu", 1, 1, 1), ("relu", 1, 2, 1), ("relu", 1, 3, 1), ("interleave", 0, 0, 2), ("q_dz2", 1, 0, 2), ("q_dz2", 1, 2, 1), ("q_wi", 1, 0, 2), ("q_dz2", 1, 3, 1), ("q_x", 1), ("q_wi", 1, 2, 2), ("relu", 2, 0, 1), ("relu", 2, 1, 1), ("relu", 2, 2, 1), ("interleave", 1, 0, 2), ("relu", 2, 3, 1), ("q_m", 0, 0), ("q_dz2", 2, 0, 2), ("q_dz2", 2, 2, 1), ("q_wi", 2, 0, 2), ("q_dz2", 2, 3, 1), ("q_wi", 2, 2, 2), ("relu", 3, 0, 1), ("relu", 3, 1, 1), ("relu", 3, 2, 1), ("relu", 3, 3, 1), ("q_dz2", 3, 0, 2), ("q_dz2", 3, 2, 1), ("q_wi", 3, 0, 2), ("q_dz2", 3, 3, 1), ("q_wi", 3, 2, 1), ("q_m", 0, 1), ("q_wi", 3, 3, 1), ("interleave", 2, 0, 2), ("empty", ("dh", 3, 1)), ("interleave", 3, 0, 1), ("q_k", 0, 0), ("q_m", 1, 0), ("interleave", 3, 1, 1), ("empty", ("out_0", 1, 0, 1)), ("q_m", 1, 1), ("empty", ("out_0", 1, 0, 3)), ("q_mask", 0, 0), ("q_mask", 0, 1), ("empty", ("slots", 1, 0, 1)), ("empty", ("out_0", 1, 1, 1)), ("empty", ("out_0", 1, 1, 3)), ("q_k", 1, 0), ("empty", ("slots", 0, 1, 1)), ("empty", ("slots", 1, 1, 1)), ("q_k", 0, 1), ("q_k", 1, 1), ("q_mask", 1, 0), ("q_mask", 1, 1), ("empty", ("out_1", 0, 3)), ("empty", ("out_1", 1, 1)), ("empty", ("out_1", 1, 3))],
-                "tensor": [("dz2", 0, 0), ("dz2", 0, 1), ("dz2", 0, 2), ("wi", 0, 0), ("dz2", 0, 3), ("wi", 0, 1), ("wi", 0, 2), ("wi", 0, 3), ("x", 0, 0), ("x", 0, 1), ("dh", 0, 0), ("x", 1, 0), ("dh", 0, 1), ("x", 1, 1), ("dh", 0, 2), ("dh", 0, 3), ("dz2", 1, 0), ("dz2", 1, 1), ("dz2", 1, 2), ("wi", 1, 0), ("wi", 1, 1), ("dz2", 1, 3), ("wi", 1, 2), ("wi", 1, 3), ("dh", 1, 0), ("dh", 1, 1), ("dh", 1, 2), ("dh", 1, 3), ("dz2", 2, 0), ("dz2", 2, 1), ("slots", 0, 0, 0), ("dz2", 2, 2), ("slots", 0, 0, 1), ("wi", 2, 0), ("wi", 2, 1), ("dz2", 2, 3), ("wi", 2, 2), ("wi", 2, 3), ("out_0", 0, 0, 0), ("out_0", 0, 0, 1), ("dh", 2, 0), ("dh", 2, 1), ("dz2", 3, 0), ("dh", 2, 2), ("dz2", 3, 1), ("dh", 2, 3), ("dz2", 3, 2), ("wi", 3, 0), ("wi", 3, 1), ("dz2", 3, 3), ("wi", 3, 2), ("wi", 3, 3), ("out_0", 0, 0, 2), ("out_0", 0, 0, 3), ("dh", 3, 0), ("dh", 3, 1), ("dh", 3, 2), ("dh", 3, 3), ("out_0", 0, 1, 0), ("out_0", 0, 1, 1), ("out_0", 0, 1, 2), ("out_0", 0, 1, 3), ("mask", 0, 0), ("mask", 0, 1), ("mask", 0, 2), ("out_0", 1, 0, 0), ("out_0", 1, 0, 1), ("out_0", 1, 0, 2), ("out_0", 1, 0, 3), ("mask", 0, 3), ("slots", 1, 0, 0), ("slots", 1, 0, 1), ("out_0", 1, 1, 0), ("out_0", 1, 1, 1), ("out_0", 1, 1, 2), ("out_0", 1, 1, 3), ("mask", 1, 0), ("mask", 1, 1), ("slots", 0, 1, 0), ("slots", 0, 1, 1), ("out_1", 0, 0), ("out_1", 0, 1), ("slots", 1, 1, 0), ("slots", 1, 1, 1), ("mask", 1, 2), ("mask", 1, 3), ("out_1", 0, 2), ("out_1", 0, 3), ("out_1", 1, 0), ("out_1", 1, 1), ("out_1", 1, 2), ("out_1", 1, 3)],
-                "s": [("empty", ("dz2", 0, 0)), ("empty", ("dz2", 0, 1)), ("empty", ("dz2", 0, 2)), ("empty", ("wi", 0, 0)), ("empty", ("dz2", 0, 3)), ("empty", ("wi", 0, 1)), ("empty", ("wi", 0, 2)), ("empty", ("wi", 0, 3)), ("empty", ("x", 0, 0)), ("empty", ("x", 0, 1)), ("empty", ("dh", 0, 0)), ("empty", ("x", 1, 0)), ("empty", ("dh", 0, 1)), ("empty", ("x", 1, 1)), ("empty", ("dh", 0, 2)), ("empty", ("dh", 0, 3)), ("empty", ("dz2", 1, 0)), ("empty", ("dz2", 1, 1)), ("empty", ("dz2", 1, 2)), ("empty", ("wi", 1, 0)), ("empty", ("wi", 1, 1)), ("empty", ("dz2", 1, 3)), ("empty", ("wi", 1, 2)), ("empty", ("wi", 1, 3)), ("empty", ("dh", 1, 0)), ("empty", ("dh", 1, 1)), ("empty", ("dh", 1, 2)), ("empty", ("dh", 1, 3)), ("empty", ("dz2", 2, 0)), ("empty", ("dz2", 2, 1)), ("empty", ("slots", 0, 0, 0)), ("empty", ("dz2", 2, 2)), ("empty", ("slots", 0, 0, 1)), ("empty", ("wi", 2, 0)), ("empty", ("wi", 2, 1)), ("empty", ("dz2", 2, 3)), ("empty", ("wi", 2, 2)), ("empty", ("wi", 2, 3)), ("empty", ("out_0", 0, 0, 0)), ("empty", ("out_0", 0, 0, 1)), ("empty", ("dh", 2, 0)), ("empty", ("dh", 2, 1)), ("empty", ("dz2", 3, 0)), ("empty", ("dh", 2, 2)), ("empty", ("dz2", 3, 1)), ("empty", ("dh", 2, 3)), ("empty", ("dz2", 3, 2)), ("empty", ("wi", 3, 0)), ("empty", ("wi", 3, 1)), ("empty", ("dz2", 3, 3)), ("empty", ("wi", 3, 2)), ("empty", ("wi", 3, 3)), ("empty", ("out_0", 0, 0, 2)), ("empty", ("out_0", 0, 0, 3)), ("empty", ("dh", 3, 0)), ("empty", ("dh", 3, 2)), ("empty", ("dh", 3, 3)), ("empty", ("out_0", 0, 1, 0)), ("empty", ("out_0", 0, 1, 1)), ("empty", ("out_0", 0, 1, 2)), ("empty", ("out_0", 0, 1, 3)), ("empty", ("mask", 0, 0)), ("empty", ("mask", 0, 1)), ("empty", ("mask", 0, 2)), ("empty", ("out_0", 1, 0, 0)), ("empty", ("out_0", 1, 0, 2)), ("empty", ("mask", 0, 3)), ("empty", ("slots", 1, 0, 0)), ("empty", ("out_0", 1, 1, 0)), ("empty", ("out_0", 1, 1, 2)), ("empty", ("mask", 1, 0)), ("empty", ("mask", 1, 1)), ("empty", ("slots", 0, 1, 0)), ("empty", ("out_1", 0, 0)), ("empty", ("out_1", 0, 1)), ("empty", ("slots", 1, 1, 0)), ("empty", ("mask", 1, 2)), ("empty", ("mask", 1, 3)), ("empty", ("out_1", 0, 2)), ("empty", ("out_1", 1, 0)), ("empty", ("out_1", 1, 2))]})
+            write_program({"sync": [("load_wi", 0, 0, 2), ("load_grad", 0, 0, 1), ("load_pre", 0, 0, 1), ("load_grad", 0, 1, 1), ("load_pre", 0, 1, 1), ("load_wi", 0, 2, 2), ("load_grad", 0, 2, 2), ("load_pre", 0, 2, 1), ("load_pre", 0, 3, 1), ("load_grad", 1, 0, 4), ("load_pre", 1, 0, 2), ("load_wi", 1, 0, 4), ("load_pre", 1, 2, 2), ("load_x",), ("load_grad", 2, 0, 4), ("load_pre", 2, 0, 2), ("load_wi", 2, 0, 4), ("load_pre", 2, 2, 2), ("load_grad", 3, 0, 4), ("load_pre", 3, 0, 2), ("load_wi", 3, 0, 4), ("load_pre", 3, 2, 1), ("load_pre", 3, 3, 1), ("load_mask", 0), ("load_mask", 1), ("store_0", 0, 0, 0), ("store_0", 0, 0, 1), ("store_0", 0, 1, 0), ("store_0", 0, 1, 1), ("store_0", 1, 0, 0), ("store_0", 1, 0, 1), ("store_0", 1, 1, 0), ("store_0", 1, 1, 1), ("store_1", 0, 0, 2), ("store_1", 0, 2, 2), ("store_1", 1, 0, 2), ("store_1", 1, 2, 1), ("store_1", 1, 3, 1)],
+                "v": [("relu", 0, 0, 1), ("relu", 0, 1, 1), ("relu", 0, 2, 1), ("relu", 0, 3, 1), ("q_dz2", 0, 0, 2), ("q_wi", 0, 0, 4), ("q_dz2", 0, 2, 2), ("relu", 1, 0, 2), ("empty", ("dh", 0, 1)), ("empty", ("dh", 0, 3)), ("relu", 1, 2, 2), ("interleave", 0, 0, 2), ("q_wi", 1, 0, 4), ("q_dz2", 1, 0, 4), ("empty", ("x", 1, 1)), ("relu", 2, 0, 2), ("q_x", 0, 2), ("interleave", 1, 0, 2), ("relu", 2, 2, 2), ("q_m", 0, 0, 2), ("q_wi", 2, 0, 4), ("q_dz2", 2, 0, 4), ("relu", 3, 0, 2), ("relu", 3, 2, 1), ("relu", 3, 3, 1), ("q_wi", 3, 0, 4), ("q_dz2", 3, 0, 2), ("q_dz2", 3, 2, 2), ("q_k", 0, 0, 2), ("empty", ("dh", 2, 3)), ("interleave", 2, 0, 2), ("empty", ("dh", 3, 1)), ("empty", ("dh", 3, 3)), ("interleave", 3, 0, 1), ("empty", ("mask", 0, 0)), ("q_m", 1, 0, 1), ("interleave", 3, 1, 1), ("empty", ("mask", 0, 2)), ("q_m", 1, 1, 1), ("empty", ("out_0", 1, 0, 3)), ("q_mask", 0, 0, 2), ("empty", ("mask", 1, 1)), ("empty", ("out_0", 1, 1, 1)), ("q_k", 1, 0, 2), ("empty", ("out_0", 1, 1, 3)), ("empty", ("mask", 1, 3)), ("q_mask", 1, 0, 1), ("q_mask", 1, 1, 1), ("empty", ("out_1", 0, 3)), ("empty", ("out_1", 1, 1)), ("empty", ("out_1", 1, 3))],
+                "tensor": [("wi", 0, 0), ("wi", 0, 1), ("dz2", 0, 0), ("dz2", 0, 1), ("wi", 0, 2), ("wi", 0, 3), ("dz2", 0, 2), ("dz2", 0, 3), ("dh", 0, 0), ("dh", 0, 1), ("dh", 0, 2), ("dh", 0, 3), ("dz2", 1, 0), ("dz2", 1, 1), ("wi", 1, 0), ("wi", 1, 1), ("wi", 1, 2), ("wi", 1, 3), ("dz2", 1, 2), ("dz2", 1, 3), ("x", 0, 0), ("x", 0, 1), ("x", 1, 0), ("x", 1, 1), ("dh", 1, 0), ("dh", 1, 1), ("dh", 1, 2), ("dh", 1, 3), ("dz2", 2, 0), ("dz2", 2, 1), ("wi", 2, 0), ("wi", 2, 1), ("wi", 2, 2), ("wi", 2, 3), ("slots", 0, 0, 0), ("slots", 0, 0, 1), ("dz2", 2, 2), ("dz2", 2, 3), ("slots", 0, 1, 0), ("slots", 0, 1, 1), ("out_0", 0, 0, 0), ("out_0", 0, 0, 1), ("out_0", 0, 0, 2), ("out_0", 0, 0, 3), ("wi", 3, 0), ("wi", 3, 1), ("wi", 3, 2), ("wi", 3, 3), ("dz2", 3, 0), ("dz2", 3, 1), ("dh", 2, 0), ("dz2", 3, 2), ("dz2", 3, 3), ("dh", 2, 1), ("dh", 2, 2), ("dh", 2, 3), ("out_0", 0, 1, 0), ("out_0", 0, 1, 1), ("dh", 3, 0), ("dh", 3, 1), ("dh", 3, 2), ("dh", 3, 3), ("out_0", 0, 1, 2), ("out_0", 0, 1, 3), ("mask", 0, 0), ("mask", 0, 1), ("mask", 0, 2), ("mask", 0, 3), ("slots", 1, 0, 0), ("slots", 1, 0, 1), ("slots", 1, 1, 0), ("slots", 1, 1, 1), ("out_0", 1, 0, 0), ("out_0", 1, 0, 1), ("out_0", 1, 0, 2), ("out_0", 1, 0, 3), ("mask", 1, 0), ("mask", 1, 1), ("out_0", 1, 1, 0), ("out_0", 1, 1, 1), ("out_0", 1, 1, 2), ("out_0", 1, 1, 3), ("mask", 1, 2), ("mask", 1, 3), ("out_1", 0, 0), ("out_1", 0, 1), ("out_1", 0, 2), ("out_1", 0, 3), ("out_1", 1, 0), ("out_1", 1, 1), ("out_1", 1, 2), ("out_1", 1, 3)],
+                "s": [("empty", ("wi", 0, 0)), ("empty", ("wi", 0, 1)), ("empty", ("dz2", 0, 0)), ("empty", ("dz2", 0, 1)), ("empty", ("wi", 0, 2)), ("empty", ("wi", 0, 3)), ("empty", ("dz2", 0, 2)), ("empty", ("dz2", 0, 3)), ("empty", ("dh", 0, 0)), ("empty", ("dh", 0, 2)), ("empty", ("dz2", 1, 0)), ("empty", ("dz2", 1, 1)), ("empty", ("wi", 1, 0)), ("empty", ("wi", 1, 1)), ("empty", ("wi", 1, 2)), ("empty", ("wi", 1, 3)), ("empty", ("dz2", 1, 2)), ("empty", ("dz2", 1, 3)), ("empty", ("x", 0, 0)), ("empty", ("x", 0, 1)), ("empty", ("x", 1, 0)), ("empty", ("dh", 1, 0)), ("empty", ("dh", 1, 1)), ("empty", ("dh", 1, 2)), ("empty", ("dh", 1, 3)), ("empty", ("dz2", 2, 0)), ("empty", ("dz2", 2, 1)), ("empty", ("wi", 2, 0)), ("empty", ("wi", 2, 1)), ("empty", ("wi", 2, 2)), ("empty", ("wi", 2, 3)), ("empty", ("slots", 0, 0, 0)), ("empty", ("slots", 0, 0, 1)), ("empty", ("dz2", 2, 2)), ("empty", ("dz2", 2, 3)), ("empty", ("slots", 0, 1, 0)), ("empty", ("slots", 0, 1, 1)), ("empty", ("out_0", 0, 0, 0)), ("empty", ("out_0", 0, 0, 1)), ("empty", ("out_0", 0, 0, 2)), ("empty", ("out_0", 0, 0, 3)), ("empty", ("wi", 3, 0)), ("empty", ("wi", 3, 1)), ("empty", ("wi", 3, 2)), ("empty", ("wi", 3, 3)), ("empty", ("dz2", 3, 0)), ("empty", ("dz2", 3, 1)), ("empty", ("dz2", 3, 2)), ("empty", ("dz2", 3, 3)), ("empty", ("dh", 2, 0)), ("empty", ("dh", 2, 1)), ("empty", ("dh", 2, 2)), ("empty", ("out_0", 0, 1, 0)), ("empty", ("out_0", 0, 1, 1)), ("empty", ("dh", 3, 0)), ("empty", ("dh", 3, 2)), ("empty", ("out_0", 0, 1, 2)), ("empty", ("out_0", 0, 1, 3)), ("empty", ("mask", 0, 1)), ("empty", ("mask", 0, 3)), ("empty", ("slots", 1, 0, 0)), ("empty", ("slots", 1, 0, 1)), ("empty", ("out_0", 1, 0, 0)), ("empty", ("out_0", 1, 0, 1)), ("empty", ("slots", 1, 1, 0)), ("empty", ("out_0", 1, 0, 2)), ("empty", ("slots", 1, 1, 1)), ("empty", ("mask", 1, 0)), ("empty", ("out_0", 1, 1, 0)), ("empty", ("out_0", 1, 1, 2)), ("empty", ("mask", 1, 2)), ("empty", ("out_1", 0, 0)), ("empty", ("out_1", 0, 1)), ("empty", ("out_1", 0, 2)), ("empty", ("out_1", 1, 0)), ("empty", ("out_1", 1, 2))]})

@@ -25,6 +25,7 @@ BUFS = {
     "dz1": 2, "dz1_by_m": 1, "dz1_by_slot": 2, "result": 4,
 }
 SHARES = {"x": "dz1_by_slot", "result_1": "pre", "wi": "weights", "mask": "weights"}
+DZ2_ROWS = (2, 4, 4, 2)
 
 
 def tile_flaxpositionwisemoelayer_pa_v_kernel(tc, dispatch_mask, x, wi, pre, grad_out, out_0, out_1):
@@ -96,31 +97,26 @@ def tile_flaxpositionwisemoelayer_pa_v_kernel(tc, dispatch_mask, x, wi, pre, gra
             nc.sync.dma_start(out=t[:], in_=x_rows)
 
 
-        banks = {}
-
-        def empty(key, engine):
-            out, in_ = banks[key]()
-            copy(engine, out, in_)
-
-        def turn(key, source, grouped, block):
+        def turn(source, grouped, block):
             bank = psum.tile([P, 2, 2, P], F32, tag="bank", name="bank")
             for i in range(2):
                 for u in range(2):
                     nc.tensor.transpose(bank[:, i, u, :], source(i, u), ident[:])
-            banks[key] = lambda: (
+            return lambda engine: copy(
+                engine,
                 grouped()[:].bitcast(F32)[:, N * block : N * (block + 1)].rearrange("p (i r u) -> p i r u", i=2, u=2),
                 bank[:].rearrange("p i u r -> p i r u"))
 
         def turn_row(kind, index, row):
             tile, at = pieces[kind, index, row]
             words = tile[:, at, :].bitcast(F32)
-            turn((kind, index, row), lambda i, u: words[:, 256 * i + u : 256 * (i + 1) : 2],
-                 lambda: ring_tile("grouped", (kind, index), [P, 4096], BF16), row)
+            return turn(lambda i, u: words[:, 256 * i + u : 256 * (i + 1) : 2],
+                        lambda: ring_tile("grouped", (kind, index), [P, 4096], BF16), row)
 
         def turn_x(g, h):
             rows = tiles["x", 0][:, g]
-            turn(("x", g, h), lambda i, u: rows[:, 2 * h + i, :].bitcast(F32)[:, u::2],
-                 lambda: ring_tile("grouped", "x", [P, 4096], BF16), 2 * g + h)
+            return turn(lambda i, u: rows[:, 2 * h + i, :].bitcast(F32)[:, u::2],
+                        lambda: ring_tile("grouped", "x", [P, 4096], BF16), 2 * g + h)
 
         def turn_dz2(e, j):
             dz2, at = pieces["dz2", e, j]
@@ -128,15 +124,17 @@ def tile_flaxpositionwisemoelayer_pa_v_kernel(tc, dispatch_mask, x, wi, pre, gra
             for a in range(2):
                 for u in range(2):
                     nc.tensor.transpose(bank[:, a, u, :], dz2[:, u, at, 256 * a : 256 * (a + 1)].bitcast(F32), ident[:])
-            banks["dz2", e, j] = lambda: (
-                ring_tile("grouped", ("dz2", e), [P, 4096], BF16)[:].bitcast(F32).rearrange(
-                    "p (a j r u) -> p a j r u", a=2, j=4, u=2)[:, :, j],
+            n = DZ2_ROWS[e]
+            return lambda engine: copy(
+                engine,
+                ring_tile("grouped", ("dz2", e, j // n), [P, 1024 * n], BF16)[:].bitcast(F32).rearrange(
+                    "p (a j r u) -> p a j r u", a=2, j=n, u=2)[:, :, j % n],
                 bank[:].rearrange("p a u r -> p a r u"))
 
         def turn_dz1(pair, g, h):
             dz1 = tiles["dz1", pair]
-            turn(("slots", pair, g, h), lambda i, u: dz1[:, 2 * h + i, g, u, :].bitcast(F32),
-                 lambda: ring_tile("dz1_by_slot", pair, [P, 4096], BF16), 2 * g + h)
+            return turn(lambda i, u: dz1[:, 2 * h + i, g, u, :].bitcast(F32),
+                        lambda: ring_tile("dz1_by_slot", pair, [P, 4096], BF16), 2 * g + h)
 
 
         def relu_backward(e, j, n):
@@ -150,21 +148,22 @@ def tile_flaxpositionwisemoelayer_pa_v_kernel(tc, dispatch_mask, x, wi, pre, gra
                     out=dz2[:, u].rearrange("p j (k b) -> p j k b", b=2),
                     in0=pre_words[:, u], scalar=0.0, in1=grad[:, u], op0=ALU.is_gt, op1=ALU.mult)
 
-        def quantize_wi(e, row, n):
+        def quantize_wi(e):
             codes = ring_tile("wi_codes", e, [P, 2 * M], U32)
             scales = ring_tile("wi_scales", e, [P, 2 * M], U8)
-            cols = slice(256 * row, 256 * (row + n))
-            nc.vector.quantize_mx(
-                out=codes[:, cols].bitcast(E4M3), scales=scales[:, cols],
-                in_=tiles["grouped", ("wi", e)][:, 1024 * row : 1024 * (row + n)])
+            nc.vector.quantize_mx(out=codes[:].bitcast(E4M3), scales=scales[:], in_=tiles["grouped", ("wi", e)][:])
 
-        def quantize_dz2(e, j, n):
+        def quantize_dz2(e, part):
             codes = ring_tile("dz2_codes", e, [P, 2 * N], U32)
             scales = ring_tile("dz2_scales", e, [P, 2 * N], U8)
-            for cols in [slice(0, 2 * N)] if n == 4 else [slice(N * a + P * j, N * a + P * (j + n)) for a in range(2)]:
+            grouped = tiles["grouped", ("dz2", e, part)]
+            if DZ2_ROWS[e] == 4:
+                nc.vector.quantize_mx(out=codes[:].bitcast(E5M2), scales=scales[:], in_=grouped[:])
+                return
+            for a in range(2):
+                cols = slice(N * a + 256 * part, N * a + 256 * (part + 1))
                 nc.vector.quantize_mx(
-                    out=codes[:, cols].bitcast(E5M2), scales=scales[:, cols],
-                    in_=tiles["grouped", ("dz2", e)][:, 4 * cols.start : 4 * cols.stop])
+                    out=codes[:, cols].bitcast(E5M2), scales=scales[:, cols], in_=grouped[:, 1024 * a : 1024 * (a + 1)])
 
         def quantize_mask(g, half, n):
             cols = slice(N * half, N * (half + n))
@@ -172,11 +171,8 @@ def tile_flaxpositionwisemoelayer_pa_v_kernel(tc, dispatch_mask, x, wi, pre, gra
                 out=mask_codes[:, g, cols].bitcast(E4M3), scales=mask_scales[:, g, cols],
                 in_=tiles["grouped", ("mask", g)][:, 4 * cols.start : 4 * cols.stop])
 
-        def quantize_x(g, n):
-            cols = slice(S * g, S * (g + n))
-            nc.vector.quantize_mx(
-                out=x_codes[:, cols].bitcast(E4M3), scales=x_scales[:, cols],
-                in_=tiles["grouped", "x"][:, 4 * cols.start : 4 * cols.stop])
+        def quantize_x():
+            nc.vector.quantize_mx(out=x_codes[:].bitcast(E4M3), scales=x_scales[:], in_=tiles["grouped", "x"][:])
 
         def quantize_dz1_m(pair, g, n):
             nc.vector.quantize_mx(
@@ -184,11 +180,11 @@ def tile_flaxpositionwisemoelayer_pa_v_kernel(tc, dispatch_mask, x, wi, pre, gra
                 scales=dz1_m_scales[:, pair, g : g + n, :].rearrange("p g w -> p (g w)"),
                 in_=tiles["dz1_by_m", pair][:, g : g + n].rearrange("p g i u s t -> p (g i u s t)"))
 
-        def quantize_dz1_slots(pair, g, n):
+        def quantize_dz1_slots(pair):
             nc.vector.quantize_mx(
-                out=dz1_k_codes[:, pair, g : g + n, :].rearrange("p g w -> p (g w)").bitcast(E5M2),
-                scales=dz1_k_scales[:, pair, g : g + n, :].rearrange("p g w -> p (g w)"),
-                in_=tiles["dz1_by_slot", pair][:, 2048 * g : 2048 * (g + n)])
+                out=dz1_k_codes[:, pair].rearrange("p g w -> p (g w)").bitcast(E5M2),
+                scales=dz1_k_scales[:, pair].rearrange("p g w -> p (g w)"),
+                in_=tiles["dz1_by_slot", pair][:])
 
 
         def dh(e, t):
@@ -202,7 +198,8 @@ def tile_flaxpositionwisemoelayer_pa_v_kernel(tc, dispatch_mask, x, wi, pre, gra
                     rhs=tiles["dz2_codes", e][:, d_cols].bitcast(E5M2), rhs_scale=tiles["dz2_scales", e][:, d_cols],
                     start=(a == 0), stop=(a == 1))
             pair, i = divmod(e, 2)
-            banks["dh", e, t] = lambda: (
+            return lambda engine: copy(
+                engine,
                 ring_tile("dz1", pair, [P, 4, G, 2, 256], BF16)[:, t, :, :, P * i : P * (i + 1)].rearrange(
                     "p g u (q b) -> p g u q b", b=2),
                 sums[:].rearrange("p (u b g q) -> p g u q b", u=2, b=2, g=2))
@@ -223,7 +220,8 @@ def tile_flaxpositionwisemoelayer_pa_v_kernel(tc, dispatch_mask, x, wi, pre, gra
                 out=acc[:], lhsT=x_codes[:, cols].bitcast(E4M3), lhsT_scale=x_scales[:, cols],
                 rhs=dz1_m_codes[:, pair, g, :].bitcast(E5M2), rhs_scale=dz1_m_scales[:, pair, g, :],
                 start=True, stop=True)
-            banks["out_0", pair, g, row] = lambda: (
+            return lambda engine: copy(
+                engine,
                 ring_tile("result", ("out_0", pair, g, half), [P, 2, N], F32)[:, t, :].rearrange(
                     "p (i q u b) -> p i q u b", i=2, u=2, b=2),
                 acc[:].rearrange("p (i u q b) -> p i q u b", i=2, u=2, b=2))
@@ -242,7 +240,8 @@ def tile_flaxpositionwisemoelayer_pa_v_kernel(tc, dispatch_mask, x, wi, pre, gra
                     lhsT=mask_codes[:, g, cols].bitcast(E4M3), lhsT_scale=mask_scales[:, g, cols],
                     rhs=dz1_k_codes[:, pair, g, :].bitcast(E5M2), rhs_scale=dz1_k_scales[:, pair, g, :],
                     start=(pair == 0), stop=(pair == 1))
-            banks["out_1", g, row] = lambda: (
+            return lambda engine: copy(
+                engine,
                 ring_tile("result_1", g, [P, 4, N], F32)[:, row, :].rearrange("p (m t) -> p m t", t=4),
                 acc[:].rearrange("p (t m) -> p m t", t=4))
 
@@ -250,134 +249,141 @@ def tile_flaxpositionwisemoelayer_pa_v_kernel(tc, dispatch_mask, x, wi, pre, gra
             nc.sync.dma_start(out=out1_rows[g, :, row : row + n, :], in_=tiles["result_1", g][:, row : row + n, :])
 
 
-        def rows(kind, index, first, n):
-            return [(kind, index, r) for r in range(first, first + n)]
+        both = slice(0, G)
 
-        def emptied(steps):
-            return [("empty", s) for s in steps]
+        def load_expert(e):
+            load_grad(e, 0, 4)
+            load_pre(e, 0, 2)
+            load_wi(e, 0, 4)
+            for j, n in [(2, 2)] if e < E - 1 else [(2, 1), (3, 1)]:
+                load_pre(e, j, n)
 
-        def gives(step):
-            kind = step[0]
-            if kind in ("load_pre", "load_grad", "load_wi", "relu", "q_wi", "q_dz2"):
-                return rows(kind, step[1], step[2], step[3])
-            if kind in ("interleave", "q_m", "q_mask", "q_k"):
-                return rows(kind, step[1], step[2], step[3])
-            if kind == "q_x":
-                return [(kind, g) for g in range(step[1], step[1] + step[2])]
-            if kind == "warm":
-                return [("empty", step)]
-            return [step]
+        def turn_wi(e, rows):
+            for row in rows:
+                turn_row("wi", e, row)("s")
 
-        def needs(step):
-            kind = step[0]
-            if kind == "empty":
-                return [step[1]] + reuse(step[1])
-            if kind in ("load_pre", "load_grad", "load_wi", "load_mask"):
-                return readers_of_replaced(step)
-            if kind in ("load_x", "warm"):
-                return []
-            if kind == "relu":
-                e, j, n = step[1:]
-                return rows("load_pre", e, j, n) + rows("load_grad", e, j, n) + readers_of_replaced(step)
-            if kind == "wi":
-                return [("load_wi", step[1], step[2])]
-            if kind == "mask":
-                return [("load_mask", step[1])]
-            if kind == "x":
-                return [("load_x",)]
-            if kind == "dz2":
-                return [("relu", step[1], step[2])]
-            if kind == "q_wi":
-                old = step[1] - BUFS["wi_codes"]
-                return emptied(rows("wi", *step[1:])) + (rows("dh", old, 0, 4) if old >= 0 else [])
-            if kind == "q_dz2":
-                old = step[1] - BUFS["dz2_codes"]
-                return emptied(rows("dz2", *step[1:])) + (rows("dh", old, 0, 4) if old >= 0 else [])
-            if kind == "q_x":
-                return emptied([("x", g, h) for g in range(step[1], step[1] + step[2]) for h in range(2)])
-            if kind == "q_mask":
-                return emptied(rows("mask", step[1], 2 * step[2], 2 * step[3]))
-            if kind == "dh":
-                return rows("q_dz2", step[1], 0, 4) + [("q_wi", step[1], step[2])]
-            if kind == "interleave":
-                return emptied(rows("dh", step[1], 0, 4)) + ([("q_m", 0, 0), ("q_m", 0, 1)] if step[1] >= 2 else [])
-            if kind == "q_m":
-                return rows("interleave", 2 * step[1], step[2], step[3]) + rows("interleave", 2 * step[1] + 1, step[2], step[3])
-            if kind == "slots":
-                pair, g, h = step[1:]
-                return emptied(rows("dh", 2 * pair, 2 * h, 2) + rows("dh", 2 * pair + 1, 2 * h, 2))
-            if kind == "q_k":
-                return emptied([("slots", step[1], g, h) for g in range(step[2], step[2] + step[3]) for h in range(2)])
-            if kind == "out_0":
-                return [("q_x", step[2]), ("q_m", step[1], step[2])]
-            if kind == "out_1":
-                return [("q_mask", step[1], step[2] // 2), ("q_k", 0, step[1]), ("q_k", 1, step[1])]
-            if kind == "store_0":
-                pair, g, half = step[1:]
-                return emptied([("out_0", pair, g, 2 * half + t) for t in range(2)])
-            return emptied(rows("out_1", *step[1:]))
-
-        def readers_of_replaced(step):
-            tag, reader = {"load_pre": ("pre", "relu"), "load_grad": ("grad", "relu"), "load_wi": ("weights", "wi"),
-                           "load_mask": ("weights", "wi"), "relu": ("dz2", "dz2")}[step[0]]
-            line = lines.setdefault(tag, [])
-            if step not in line:
-                line.append(step)
-            back = line.index(step) - BUFS[tag]
-            return rows(reader, *line[back][1:]) if back >= 0 else []
-
-        lines = {}
-
-        def reuse(step):
-            if step[0] == "out_0":
-                back = 4 * step[1] + 2 * step[2] + step[3] // 2 - BUFS["result"]
-                return [("store_0", back // 4, back // 2 % 2, back % 2)] if back >= 0 else []
-            return []
-
-        def warm(n):
-            bank = psum.tile([P, P], F32, tag="bank", name="warm")
-            nc.tensor.matmul(out=bank[:], lhsT=ident[:], rhs=ident[:], start=True, stop=True)
-
-        calls = {
-            "warm": warm,
-            "load_pre": load_pre, "load_grad": load_grad, "load_wi": load_wi, "load_mask": load_mask, "load_x": load_x,
-            "relu": relu_backward, "x": turn_x, "dz2": turn_dz2, "slots": turn_dz1,
-            "wi": lambda e, row: turn_row("wi", e, row), "mask": lambda g, row: turn_row("mask", g, row),
-            "q_wi": quantize_wi, "q_dz2": quantize_dz2, "q_x": quantize_x, "q_mask": quantize_mask,
-            "q_m": quantize_dz1_m, "q_k": quantize_dz1_slots, "dh": dh,
-            "interleave": lambda e, g, n: interleave_dz1(e, slice(g, g + n)),
-            "out_0": output_0, "out_1": output_1, "store_0": store_0, "store_1": store_1,
-        }
-
-        def write_program(queues):
-            done = set()
-            filled = []
-            at = {name: 0 for name in queues}
-            left = sum(len(q) for q in queues.values())
-            while left:
-                before = left
-                for name, queue in queues.items():
-                    while at[name] < len(queue):
-                        step = queue[at[name]]
-                        wanted = needs(step)
-                        if name == "tensor" and len(filled) >= 8:
-                            wanted = wanted + [("empty", filled[-8])]
-                        if not all(w in done for w in wanted):
-                            break
-                        if step[0] == "empty":
-                            empty(step[1], name)
-                        else:
-                            calls[step[0]](*step[1:])
-                        if name == "tensor":
-                            filled.append(step)
-                        for w in gives(step):
-                            done.add(w)
-                        at[name] = at[name] + 1
-                        left = left - 1
-                assert left < before, [q[at[n]] for n, q in queues.items() if at[n] < len(q)]
+        def turn_dz2_rows(e, rows):
+            for j in rows:
+                turn_dz2(e, j)("s")
 
         with tc.manual_schedule():
-            write_program({"sync": [("load_wi", 0, 0, 2), ("load_grad", 0, 0, 1), ("load_pre", 0, 0, 1), ("load_grad", 0, 1, 1), ("load_pre", 0, 1, 1), ("load_wi", 0, 2, 2), ("load_grad", 0, 2, 2), ("load_pre", 0, 2, 1), ("load_pre", 0, 3, 1), ("load_grad", 1, 0, 4), ("load_pre", 1, 0, 2), ("load_wi", 1, 0, 4), ("load_pre", 1, 2, 2), ("load_x",), ("load_grad", 2, 0, 4), ("load_pre", 2, 0, 2), ("load_wi", 2, 0, 4), ("load_pre", 2, 2, 2), ("load_grad", 3, 0, 4), ("load_pre", 3, 0, 2), ("load_wi", 3, 0, 4), ("load_pre", 3, 2, 1), ("load_pre", 3, 3, 1), ("load_mask", 0), ("load_mask", 1), ("store_0", 0, 0, 0), ("store_0", 0, 0, 1), ("store_0", 0, 1, 0), ("store_0", 0, 1, 1), ("store_0", 1, 0, 0), ("store_0", 1, 0, 1), ("store_0", 1, 1, 0), ("store_0", 1, 1, 1), ("store_1", 0, 0, 2), ("store_1", 0, 2, 2), ("store_1", 1, 0, 2), ("store_1", 1, 2, 1), ("store_1", 1, 3, 1)],
-                "v": [("relu", 0, 0, 1), ("relu", 0, 1, 1), ("relu", 0, 2, 1), ("relu", 0, 3, 1), ("q_dz2", 0, 0, 2), ("q_wi", 0, 0, 4), ("q_dz2", 0, 2, 2), ("relu", 1, 0, 2), ("empty", ("dh", 0, 1)), ("empty", ("dh", 0, 3)), ("relu", 1, 2, 2), ("interleave", 0, 0, 2), ("q_wi", 1, 0, 4), ("q_dz2", 1, 0, 4), ("empty", ("x", 1, 1)), ("relu", 2, 0, 2), ("q_x", 0, 2), ("interleave", 1, 0, 2), ("relu", 2, 2, 2), ("q_m", 0, 0, 2), ("q_wi", 2, 0, 4), ("q_dz2", 2, 0, 4), ("relu", 3, 0, 2), ("relu", 3, 2, 1), ("relu", 3, 3, 1), ("q_wi", 3, 0, 4), ("q_dz2", 3, 0, 2), ("q_dz2", 3, 2, 2), ("q_k", 0, 0, 2), ("empty", ("dh", 2, 3)), ("interleave", 2, 0, 2), ("empty", ("dh", 3, 1)), ("empty", ("dh", 3, 3)), ("interleave", 3, 0, 1), ("empty", ("mask", 0, 0)), ("q_m", 1, 0, 1), ("interleave", 3, 1, 1), ("empty", ("mask", 0, 2)), ("q_m", 1, 1, 1), ("empty", ("out_0", 1, 0, 3)), ("q_mask", 0, 0, 2), ("empty", ("mask", 1, 1)), ("empty", ("out_0", 1, 1, 1)), ("q_k", 1, 0, 2), ("empty", ("out_0", 1, 1, 3)), ("empty", ("mask", 1, 3)), ("q_mask", 1, 0, 1), ("q_mask", 1, 1, 1), ("empty", ("out_1", 0, 3)), ("empty", ("out_1", 1, 1)), ("empty", ("out_1", 1, 3))],
-                "tensor": [("wi", 0, 0), ("wi", 0, 1), ("dz2", 0, 0), ("dz2", 0, 1), ("wi", 0, 2), ("wi", 0, 3), ("dz2", 0, 2), ("dz2", 0, 3), ("dh", 0, 0), ("dh", 0, 1), ("dh", 0, 2), ("dh", 0, 3), ("dz2", 1, 0), ("dz2", 1, 1), ("wi", 1, 0), ("wi", 1, 1), ("wi", 1, 2), ("wi", 1, 3), ("dz2", 1, 2), ("dz2", 1, 3), ("x", 0, 0), ("x", 0, 1), ("x", 1, 0), ("x", 1, 1), ("dh", 1, 0), ("dh", 1, 1), ("dh", 1, 2), ("dh", 1, 3), ("dz2", 2, 0), ("dz2", 2, 1), ("wi", 2, 0), ("wi", 2, 1), ("wi", 2, 2), ("wi", 2, 3), ("slots", 0, 0, 0), ("slots", 0, 0, 1), ("dz2", 2, 2), ("dz2", 2, 3), ("slots", 0, 1, 0), ("slots", 0, 1, 1), ("out_0", 0, 0, 0), ("out_0", 0, 0, 1), ("out_0", 0, 0, 2), ("out_0", 0, 0, 3), ("wi", 3, 0), ("wi", 3, 1), ("wi", 3, 2), ("wi", 3, 3), ("dz2", 3, 0), ("dz2", 3, 1), ("dh", 2, 0), ("dz2", 3, 2), ("dz2", 3, 3), ("dh", 2, 1), ("dh", 2, 2), ("dh", 2, 3), ("out_0", 0, 1, 0), ("out_0", 0, 1, 1), ("dh", 3, 0), ("dh", 3, 1), ("dh", 3, 2), ("dh", 3, 3), ("out_0", 0, 1, 2), ("out_0", 0, 1, 3), ("mask", 0, 0), ("mask", 0, 1), ("mask", 0, 2), ("mask", 0, 3), ("slots", 1, 0, 0), ("slots", 1, 0, 1), ("slots", 1, 1, 0), ("slots", 1, 1, 1), ("out_0", 1, 0, 0), ("out_0", 1, 0, 1), ("out_0", 1, 0, 2), ("out_0", 1, 0, 3), ("mask", 1, 0), ("mask", 1, 1), ("out_0", 1, 1, 0), ("out_0", 1, 1, 1), ("out_0", 1, 1, 2), ("out_0", 1, 1, 3), ("mask", 1, 2), ("mask", 1, 3), ("out_1", 0, 0), ("out_1", 0, 1), ("out_1", 0, 2), ("out_1", 0, 3), ("out_1", 1, 0), ("out_1", 1, 1), ("out_1", 1, 2), ("out_1", 1, 3)],
-                "s": [("empty", ("wi", 0, 0)), ("empty", ("wi", 0, 1)), ("empty", ("dz2", 0, 0)), ("empty", ("dz2", 0, 1)), ("empty", ("wi", 0, 2)), ("empty", ("wi", 0, 3)), ("empty", ("dz2", 0, 2)), ("empty", ("dz2", 0, 3)), ("empty", ("dh", 0, 0)), ("empty", ("dh", 0, 2)), ("empty", ("dz2", 1, 0)), ("empty", ("dz2", 1, 1)), ("empty", ("wi", 1, 0)), ("empty", ("wi", 1, 1)), ("empty", ("wi", 1, 2)), ("empty", ("wi", 1, 3)), ("empty", ("dz2", 1, 2)), ("empty", ("dz2", 1, 3)), ("empty", ("x", 0, 0)), ("empty", ("x", 0, 1)), ("empty", ("x", 1, 0)), ("empty", ("dh", 1, 0)), ("empty", ("dh", 1, 1)), ("empty", ("dh", 1, 2)), ("empty", ("dh", 1, 3)), ("empty", ("dz2", 2, 0)), ("empty", ("dz2", 2, 1)), ("empty", ("wi", 2, 0)), ("empty", ("wi", 2, 1)), ("empty", ("wi", 2, 2)), ("empty", ("wi", 2, 3)), ("empty", ("slots", 0, 0, 0)), ("empty", ("slots", 0, 0, 1)), ("empty", ("dz2", 2, 2)), ("empty", ("dz2", 2, 3)), ("empty", ("slots", 0, 1, 0)), ("empty", ("slots", 0, 1, 1)), ("empty", ("out_0", 0, 0, 0)), ("empty", ("out_0", 0, 0, 1)), ("empty", ("out_0", 0, 0, 2)), ("empty", ("out_0", 0, 0, 3)), ("empty", ("wi", 3, 0)), ("empty", ("wi", 3, 1)), ("empty", ("wi", 3, 2)), ("empty", ("wi", 3, 3)), ("empty", ("dz2", 3, 0)), ("empty", ("dz2", 3, 1)), ("empty", ("dz2", 3, 2)), ("empty", ("dz2", 3, 3)), ("empty", ("dh", 2, 0)), ("empty", ("dh", 2, 1)), ("empty", ("dh", 2, 2)), ("empty", ("out_0", 0, 1, 0)), ("empty", ("out_0", 0, 1, 1)), ("empty", ("dh", 3, 0)), ("empty", ("dh", 3, 2)), ("empty", ("out_0", 0, 1, 2)), ("empty", ("out_0", 0, 1, 3)), ("empty", ("mask", 0, 1)), ("empty", ("mask", 0, 3)), ("empty", ("slots", 1, 0, 0)), ("empty", ("slots", 1, 0, 1)), ("empty", ("out_0", 1, 0, 0)), ("empty", ("out_0", 1, 0, 1)), ("empty", ("slots", 1, 1, 0)), ("empty", ("out_0", 1, 0, 2)), ("empty", ("slots", 1, 1, 1)), ("empty", ("mask", 1, 0)), ("empty", ("out_0", 1, 1, 0)), ("empty", ("out_0", 1, 1, 2)), ("empty", ("mask", 1, 2)), ("empty", ("out_1", 0, 0)), ("empty", ("out_1", 0, 1)), ("empty", ("out_1", 0, 2)), ("empty", ("out_1", 1, 0)), ("empty", ("out_1", 1, 2))]})
+            load_wi(0, 0, 2)
+            for j in range(2):
+                load_grad(0, j, 1)
+                load_pre(0, j, 1)
+            load_wi(0, 2, 2)
+            load_grad(0, 2, 2)
+            for j in range(2, 4):
+                load_pre(0, j, 1)
+            for half in range(2):
+                turn_wi(0, range(2 * half, 2 * half + 2))
+                for j in range(2 * half, 2 * half + 2):
+                    relu_backward(0, j, 1)
+                    turn_dz2(0, j)("s")
+            load_expert(1)
+            load_x()
+            load_expert(2)
+            quantize_dz2(0, 0)
+            quantize_wi(0)
+            quantize_dz2(0, 1)
+
+            relu_backward(1, 0, 2)
+            for t in range(4):
+                dh(0, t)("sv"[t % 2])
+            turn_dz2_rows(1, range(2))
+            turn_wi(1, range(4))
+            relu_backward(1, 2, 2)
+            turn_dz2_rows(1, range(2, 4))
+            interleave_dz1(0, both)
+            quantize_wi(1)
+            quantize_dz2(1, 0)
+            for g in range(G):
+                for h in range(2):
+                    turn_x(g, h)("sv"[g + h == 2])
+
+            for t in range(4):
+                dh(1, t)("s")
+            relu_backward(2, 0, 2)
+            load_expert(3)
+            quantize_x()
+            interleave_dz1(1, both)
+            turn_dz2_rows(2, range(2))
+            turn_wi(2, range(4))
+            for g in range(G):
+                load_mask(g)
+            relu_backward(2, 2, 2)
+            for g in range(G):
+                for h in range(2):
+                    turn_dz1(0, g, h)("s")
+                if g == 0:
+                    turn_dz2_rows(2, range(2, 4))
+            quantize_dz1_m(0, 0, G)
+            for row in range(4):
+                output_0(0, 0, row)("s")
+            quantize_wi(2)
+            quantize_dz2(2, 0)
+            for half in range(2):
+                store_0(0, 0, half)
+
+            relu_backward(3, 0, 2)
+            turn_wi(3, range(4))
+            turn_dz2_rows(3, range(2))
+            empty_first_tile = dh(2, 0)
+            for j in range(2, 4):
+                relu_backward(3, j, 1)
+                turn_dz2(3, j)("s")
+            quantize_wi(3)
+            for half in range(2):
+                quantize_dz2(3, half)
+            quantize_dz1_slots(0)
+            empty_first_tile("s")
+            for t in range(1, 4):
+                dh(2, t)("sv"[t == 3])
+            interleave_dz1(2, both)
+
+            for half in range(2):
+                for row in range(2 * half, 2 * half + 2):
+                    output_0(0, 1, row)("s")
+                store_0(0, 1, half)
+                if half == 0:
+                    for t in range(4):
+                        dh(3, t)("sv"[t % 2])
+
+            for g in range(G):
+                interleave_dz1(3, slice(g, g + 1))
+                for row in range(2 * g, 2 * g + 2):
+                    turn_row("mask", 0, row)("vs"[row % 2])
+                quantize_dz1_m(1, g, 1)
+            for h in range(2):
+                turn_dz1(1, 0, h)("s")
+            empty_slots = [turn_dz1(1, 1, h) for h in range(2)]
+            for row in range(4):
+                output_0(1, 0, row)("sv"[row == 3])
+                if row % 2:
+                    store_0(1, 0, row // 2)
+                if row in (1, 2):
+                    empty_slots[row - 1]("s")
+            quantize_mask(0, 0, 2)
+
+            for row in range(2):
+                turn_row("mask", 1, row)("sv"[row % 2])
+            for row in range(4):
+                output_0(1, 1, row)("sv"[row % 2])
+                if row == 1:
+                    quantize_dz1_slots(1)
+                if row % 2:
+                    store_0(1, 1, row // 2)
+            for row in range(2, 4):
+                turn_row("mask", 1, row)("sv"[row % 2])
+            for half in range(2):
+                quantize_mask(1, half, 1)
+            for row in range(4):
+                output_1(0, row)("sv"[row == 3])
+                if row % 2:
+                    store_1(0, row - 1, 2)
+            for row in range(4):
+                output_1(1, row)("sv"[row % 2])
+                if row == 1:
+                    store_1(1, 0, 2)
+                if row >= 2:
+                    store_1(1, row, 1)

@@ -19,10 +19,15 @@ N = 512
 PAIRS = E // 2
 
 BUFS = {
-    "pre": 4, "grad": 3, "weights": 3,
-    "dz2": 3, "grouped": 4,
+    "pre": 4,
+    "grad": 3,
+    "weights": 3,
+    "dz2": 3,
+    "grouped": 4,
     "wi_codes": 2, "wi_scales": 2, "dz2_codes": 2, "dz2_scales": 2,
-    "dz1": 2, "dz1_by_m": 1, "dz1_by_slot": 2, "result": 4,
+    "dz1": 2, "dz1_by_slot": 2,
+    "dz1_by_m": 1,
+    "result": 4,
 }
 SHARES = {"x": "dz1_by_slot", "result_1": "pre", "wi": "weights", "mask": "weights"}
 DZ2_ROWS = (2, 4, 4, 2)
@@ -178,7 +183,7 @@ def tile_flaxpositionwisemoelayer_pa_v_kernel(tc, dispatch_mask, x, wi, pre, gra
             nc.vector.quantize_mx(
                 out=dz1_m_codes[:, pair, g : g + n, :].rearrange("p g w -> p (g w)").bitcast(E5M2),
                 scales=dz1_m_scales[:, pair, g : g + n, :].rearrange("p g w -> p (g w)"),
-                in_=tiles["dz1_by_m", pair][:, g : g + n].rearrange("p g i u s t -> p (g i u s t)"))
+                in_=tiles["dz1_by_m", pair][:, g : g + n].rearrange("p g u i s t -> p (g u i s t)"))
 
         def quantize_dz1_slots(pair):
             nc.vector.quantize_mx(
@@ -204,12 +209,11 @@ def tile_flaxpositionwisemoelayer_pa_v_kernel(tc, dispatch_mask, x, wi, pre, gra
                     "p g u (q b) -> p g u q b", b=2),
                 sums[:].rearrange("p (u b g q) -> p g u q b", u=2, b=2, g=2))
 
-        def interleave_dz1(e, groups):
-            pair, i = divmod(e, 2)
+        def interleave_dz1(pair, groups, experts):
             by_m = ring_tile("dz1_by_m", pair, [P, G, 2, 2, P, 4], BF16)
             nc.vector.tensor_copy(
-                out=by_m[:, groups, i].rearrange("p g u (c n) t -> p g u c t n", n=4),
-                in_=tiles["dz1", pair][:, :, groups, :, P * i : P * (i + 1)].rearrange("p t g u (c n) -> p g u c t n", n=4))
+                out=by_m[:].rearrange("p g u i (c n) t -> p g u i c t n", n=4)[:, groups, :, experts],
+                in_=tiles["dz1", pair][:].rearrange("p t g u (i c n) -> p g u i c t n", i=2, n=4)[:, groups, :, experts])
 
 
         def output_0(pair, g, row):
@@ -224,7 +228,7 @@ def tile_flaxpositionwisemoelayer_pa_v_kernel(tc, dispatch_mask, x, wi, pre, gra
                 engine,
                 ring_tile("result", ("out_0", pair, g, half), [P, 2, N], F32)[:, t, :].rearrange(
                     "p (i q u b) -> p i q u b", i=2, u=2, b=2),
-                acc[:].rearrange("p (i u q b) -> p i q u b", i=2, u=2, b=2))
+                acc[:].rearrange("p (u i q b) -> p i q u b", i=2, u=2, b=2))
 
         def store_0(pair, g, half):
             nc.sync.dma_start(
@@ -294,7 +298,7 @@ def tile_flaxpositionwisemoelayer_pa_v_kernel(tc, dispatch_mask, x, wi, pre, gra
             turn_wi(1, range(4))
             relu_backward(1, 2, 2)
             turn_dz2_rows(1, range(2, 4))
-            interleave_dz1(0, both)
+            interleave_dz1(0, both, 0)
             quantize_wi(1)
             quantize_dz2(1, 0)
             for g in range(G):
@@ -306,7 +310,7 @@ def tile_flaxpositionwisemoelayer_pa_v_kernel(tc, dispatch_mask, x, wi, pre, gra
             relu_backward(2, 0, 2)
             load_expert(3)
             quantize_x()
-            interleave_dz1(1, both)
+            interleave_dz1(0, both, 1)
             turn_dz2_rows(2, range(2))
             turn_wi(2, range(4))
             for g in range(G):
@@ -339,7 +343,6 @@ def tile_flaxpositionwisemoelayer_pa_v_kernel(tc, dispatch_mask, x, wi, pre, gra
             empty_first_tile("s")
             for t in range(1, 4):
                 dh(2, t)("sv"[t == 3])
-            interleave_dz1(2, both)
 
             for half in range(2):
                 for row in range(2 * half, 2 * half + 2):
@@ -350,7 +353,7 @@ def tile_flaxpositionwisemoelayer_pa_v_kernel(tc, dispatch_mask, x, wi, pre, gra
                         dh(3, t)("sv"[t % 2])
 
             for g in range(G):
-                interleave_dz1(3, slice(g, g + 1))
+                interleave_dz1(1, g, both)
                 for row in range(2 * g, 2 * g + 2):
                     turn_row("mask", 0, row)("vs"[row % 2])
                 quantize_dz1_m(1, g, 1)

@@ -20,7 +20,7 @@ PAIRS = E // 2
 
 BUFS = {
     "pre": 4,
-    "grad": 3,
+    "grad": 5,
     "weights": 3,
     "dz2": 3,
     "grouped": 4,
@@ -153,10 +153,13 @@ def tile_flaxpositionwisemoelayer_pa_v_kernel(tc, dispatch_mask, x, wi, pre, gra
                     out=dz2[:, u].rearrange("p j (k b) -> p j k b", b=2),
                     in0=pre_words[:, u], scalar=0.0, in1=grad[:, u], op0=ALU.is_gt, op1=ALU.mult)
 
-        def quantize_wi(e):
+        def quantize_wi(e, row=0, n=4):
             codes = ring_tile("wi_codes", e, [P, 2 * M], U32)
             scales = ring_tile("wi_scales", e, [P, 2 * M], U8)
-            nc.vector.quantize_mx(out=codes[:].bitcast(E4M3), scales=scales[:], in_=tiles["grouped", ("wi", e)][:])
+            cols = slice(256 * row, 256 * (row + n))
+            nc.vector.quantize_mx(
+                out=codes[:, cols].bitcast(E4M3), scales=scales[:, cols],
+                in_=tiles["grouped", ("wi", e)][:, 4 * cols.start : 4 * cols.stop])
 
         def quantize_dz2(e, part):
             codes = ring_tile("dz2_codes", e, [P, 2 * N], U32)
@@ -256,10 +259,11 @@ def tile_flaxpositionwisemoelayer_pa_v_kernel(tc, dispatch_mask, x, wi, pre, gra
         both = slice(0, G)
 
         def load_expert(e):
-            load_grad(e, 0, 4)
-            load_pre(e, 0, 2)
             load_wi(e, 0, 4)
-            for j, n in [(2, 2)] if e < E - 1 else [(2, 1), (3, 1)]:
+            load_grad(e, 0, 2)
+            load_pre(e, 0, 2)
+            load_grad(e, 2, 2)
+            for j, n in [(2, 2)] if e == 2 else [(2, 1), (3, 1)]:
                 load_pre(e, j, n)
 
         def turn_wi(e, rows):
@@ -291,97 +295,94 @@ def tile_flaxpositionwisemoelayer_pa_v_kernel(tc, dispatch_mask, x, wi, pre, gra
             quantize_wi(0)
             quantize_dz2(0, 1)
 
+            turn_wi(1, range(1))
+            for t in range(3):
+                dh(0, t)("s")
             relu_backward(1, 0, 2)
-            for t in range(4):
-                dh(0, t)("sv"[t % 2])
+            turn_wi(1, range(1, 4))
+            relu_backward(1, 2, 1)
+            relu_backward(1, 3, 1)
             turn_dz2_rows(1, range(2))
-            turn_wi(1, range(4))
-            relu_backward(1, 2, 2)
-            turn_dz2_rows(1, range(2, 4))
-            interleave_dz1(0, both, 0)
+            last = dh(0, 3)
             quantize_wi(1)
+            last("v")
+            turn_dz2_rows(1, range(2, 4))
             quantize_dz2(1, 0)
+            interleave_dz1(0, both, 0)
             for g in range(G):
                 for h in range(2):
-                    turn_x(g, h)("sv"[g + h == 2])
-
-            for t in range(4):
-                dh(1, t)("s")
-            relu_backward(2, 0, 2)
+                    turn_x(g, h)("s")
             load_expert(3)
+            for t in range(4):
+                dh(1, t)("vsss"[t])
             quantize_x()
-            interleave_dz1(0, both, 1)
-            turn_dz2_rows(2, range(2))
+            relu_backward(2, 0, 2)
             turn_wi(2, range(4))
+            interleave_dz1(0, both, 1)
+            for h in range(2):
+                for g in range(G):
+                    turn_dz1(0, g, h)("s")
             for g in range(G):
                 load_mask(g)
+            turn_dz2_rows(2, range(2))
             relu_backward(2, 2, 2)
-            for g in range(G):
-                for h in range(2):
-                    turn_dz1(0, g, h)("s")
-                if g == 0:
-                    turn_dz2_rows(2, range(2, 4))
             quantize_dz1_m(0, 0, G)
+            quantize_wi(2)
+            turn_dz2_rows(2, range(2, 4))
             for row in range(4):
                 output_0(0, 0, row)("s")
-            quantize_wi(2)
             quantize_dz2(2, 0)
-            for half in range(2):
-                store_0(0, 0, half)
-
             relu_backward(3, 0, 2)
             turn_wi(3, range(4))
+            late = [dh(2, t) for t in range(2)]
             turn_dz2_rows(3, range(2))
-            empty_first_tile = dh(2, 0)
-            for j in range(2, 4):
-                relu_backward(3, j, 1)
-                turn_dz2(3, j)("s")
+            relu_backward(3, 2, 1)
+            relu_backward(3, 3, 1)
             quantize_wi(3)
-            for half in range(2):
-                quantize_dz2(3, half)
+            turn_dz2_rows(3, range(2, 4))
+            quantize_dz2(3, 0)
+            quantize_dz2(3, 1)
+            late += [dh(2, t) for t in range(2, 4)]
+            for c in late:
+                c("s")
             quantize_dz1_slots(0)
-            empty_first_tile("s")
-            for t in range(1, 4):
-                dh(2, t)("sv"[t == 3])
-
             for half in range(2):
-                for row in range(2 * half, 2 * half + 2):
-                    output_0(0, 1, row)("s")
-                store_0(0, 1, half)
-                if half == 0:
-                    for t in range(4):
-                        dh(3, t)("sv"[t % 2])
+                store_0(0, 0, half)
+            for t in range(4):
+                dh(3, t)("vs"[t % 2])
+            for row in range(4):
+                output_0(0, 1, row)("s")
+                if row % 2:
+                    store_0(0, 1, row // 2)
 
             for g in range(G):
                 interleave_dz1(1, g, both)
-                for row in range(2 * g, 2 * g + 2):
-                    turn_row("mask", 0, row)("vs"[row % 2])
+            for g in range(G):
                 quantize_dz1_m(1, g, 1)
-            for h in range(2):
-                turn_dz1(1, 0, h)("s")
-            empty_slots = [turn_dz1(1, 1, h) for h in range(2)]
+            slots = [turn_dz1(1, g, h) for g in range(G) for h in range(2)]
             for row in range(4):
-                output_0(1, 0, row)("sv"[row == 3])
+                turn_row("mask", 0, row)("s")
+            for c in slots:
+                c("v")
+            for row in range(4):
+                output_0(1, 0, row)("s")
                 if row % 2:
                     store_0(1, 0, row // 2)
-                if row in (1, 2):
-                    empty_slots[row - 1]("s")
+            quantize_dz1_slots(1)
             quantize_mask(0, 0, 2)
-
             for row in range(2):
-                turn_row("mask", 1, row)("sv"[row % 2])
+                turn_row("mask", 1, row)("v")
             for row in range(4):
-                output_0(1, 1, row)("sv"[row % 2])
-                if row == 1:
-                    quantize_dz1_slots(1)
+                output_0(1, 1, row)("s")
                 if row % 2:
                     store_0(1, 1, row // 2)
             for row in range(2, 4):
-                turn_row("mask", 1, row)("sv"[row % 2])
-            for half in range(2):
-                quantize_mask(1, half, 1)
+                turn_row("mask", 1, row)("vs"[row % 2])
+            quantize_mask(1, 0, 1)
             for row in range(4):
                 output_1(0, row)("sv"[row == 3])
+                if row == 0:
+                    quantize_mask(1, 1, 1)
                 if row % 2:
                     store_1(0, row - 1, 2)
             for row in range(4):

@@ -275,37 +275,31 @@ def tile_flaxpositionwisemoelayer_pa_v_kernel(tc, dispatch_mask, x, wi, pre, gra
                 turn_dz2(e, j)("s")
 
         with tc.manual_schedule():
-            load_wi(0, 0, 2)
-            for j in range(2):
-                load_grad(0, j, 1)
-                load_pre(0, j, 1)
-            load_wi(0, 2, 2)
-            load_grad(0, 2, 2)
+            load_expert(0)
+            turn_wi(0, range(4))
+            relu_backward(0, 0, 2)
+            turn_dz2_rows(0, range(2))
             for j in range(2, 4):
-                load_pre(0, j, 1)
-            for half in range(2):
-                turn_wi(0, range(2 * half, 2 * half + 2))
-                for j in range(2 * half, 2 * half + 2):
-                    relu_backward(0, j, 1)
-                    turn_dz2(0, j)("s")
+                relu_backward(0, j, 1)
+                turn_dz2(0, j)("s")
             load_expert(1)
             load_x()
             load_expert(2)
-            quantize_dz2(0, 0)
             quantize_wi(0)
+            quantize_dz2(0, 0)
             quantize_dz2(0, 1)
 
-            turn_wi(1, range(1))
+            turn_wi(1, range(2))
             for t in range(3):
-                dh(0, t)("s")
+                dh(0, t)("vsv"[t])
             relu_backward(1, 0, 2)
-            turn_wi(1, range(1, 4))
+            turn_wi(1, range(2, 4))
             relu_backward(1, 2, 1)
             relu_backward(1, 3, 1)
             turn_dz2_rows(1, range(2))
             last = dh(0, 3)
             quantize_wi(1)
-            last("v")
+            last("s")
             turn_dz2_rows(1, range(2, 4))
             quantize_dz2(1, 0)
             interleave_dz1(0, both, 0)
@@ -329,12 +323,16 @@ def tile_flaxpositionwisemoelayer_pa_v_kernel(tc, dispatch_mask, x, wi, pre, gra
             quantize_dz1_m(0, 0, G)
             quantize_wi(2)
             turn_dz2_rows(2, range(2, 4))
-            for row in range(4):
-                output_0(0, 0, row)("s")
             quantize_dz2(2, 0)
             relu_backward(3, 0, 2)
-            turn_wi(3, range(4))
-            late = [dh(2, t) for t in range(2)]
+            for half in range(2):
+                turn_wi(3, range(2 * half, 2 * half + 2))
+                for row in range(2 * half, 2 * half + 2):
+                    output_0(0, 0, row)("s")
+                store_0(0, 0, half)
+            late = [output_0(0, 1, row) for row in range(2)]
+            dh(2, 0)("s")
+            late += [dh(2, 1)]
             turn_dz2_rows(3, range(2))
             relu_backward(3, 2, 1)
             relu_backward(3, 3, 1)
@@ -342,51 +340,47 @@ def tile_flaxpositionwisemoelayer_pa_v_kernel(tc, dispatch_mask, x, wi, pre, gra
             turn_dz2_rows(3, range(2, 4))
             quantize_dz2(3, 0)
             quantize_dz2(3, 1)
-            late += [dh(2, t) for t in range(2, 4)]
             for c in late:
                 c("s")
+            store_0(0, 1, 0)
+            for t in range(2, 4):
+                dh(2, t)("sv"[t % 2])
+            late = [output_0(0, 1, row) for row in range(2, 4)]
+            late[0]("v")
+            interleave_dz1(1, both, 0)
             quantize_dz1_slots(0)
-            for half in range(2):
-                store_0(0, 0, half)
             for t in range(4):
-                dh(3, t)("vs"[t % 2])
-            for row in range(4):
-                output_0(0, 1, row)("s")
-                if row % 2:
-                    store_0(0, 1, row // 2)
+                dh(3, t)("s")
+            late[1]("s")
+            store_0(0, 1, 1)
 
             for g in range(G):
-                interleave_dz1(1, g, both)
+                interleave_dz1(1, g, 1)
             for g in range(G):
                 quantize_dz1_m(1, g, 1)
-            slots = [turn_dz1(1, g, h) for g in range(G) for h in range(2)]
             for row in range(4):
                 turn_row("mask", 0, row)("s")
+            slots = [turn_dz1(1, g, h) for g in range(G) for h in range(2)]
             for c in slots:
                 c("v")
-            for row in range(4):
-                output_0(1, 0, row)("s")
-                if row % 2:
-                    store_0(1, 0, row // 2)
-            quantize_dz1_slots(1)
             quantize_mask(0, 0, 2)
-            for row in range(2):
-                turn_row("mask", 1, row)("v")
+            quantize_dz1_slots(1)
+            for g in range(G):
+                for row in range(4):
+                    output_0(1, g, row)("s")
+                    if row % 2:
+                        store_0(1, g, row // 2)
             for row in range(4):
-                output_0(1, 1, row)("s")
-                if row % 2:
-                    store_0(1, 1, row // 2)
-            for row in range(2, 4):
-                turn_row("mask", 1, row)("vs"[row % 2])
-            quantize_mask(1, 0, 1)
+                turn_row("mask", 1, row)("vvsv"[row])
+                if row == 1:
+                    quantize_mask(1, 0, 1)
+            quantize_mask(1, 1, 1)
             for row in range(4):
-                output_1(0, row)("sv"[row == 3])
-                if row == 0:
-                    quantize_mask(1, 1, 1)
+                output_1(0, row)("s")
                 if row % 2:
                     store_1(0, row - 1, 2)
             for row in range(4):
-                output_1(1, row)("sv"[row % 2])
+                output_1(1, row)("vs"[row % 2])
                 if row == 1:
                     store_1(1, 0, 2)
                 if row >= 2:

@@ -259,12 +259,16 @@ def tile_flaxpositionwisemoelayer_pa_v_kernel(tc, dispatch_mask, x, wi, pre, gra
         both = slice(0, G)
 
         def load_expert(e):
-            load_wi(e, 0, 4)
+            if e > 0:
+                load_wi(e, 0, 4)
             load_grad(e, 0, 2)
             load_pre(e, 0, 2)
             load_grad(e, 2, 2)
             for j, n in [(2, 2)] if e == 2 else [(2, 1), (3, 1)]:
                 load_pre(e, j, n)
+            if e == 0:
+                for half in range(2):
+                    load_wi(e, 2 * half, 2)
 
         def turn_wi(e, rows):
             for row in rows:
@@ -276,7 +280,6 @@ def tile_flaxpositionwisemoelayer_pa_v_kernel(tc, dispatch_mask, x, wi, pre, gra
 
         with tc.manual_schedule():
             load_expert(0)
-            turn_wi(0, range(4))
             relu_backward(0, 0, 2)
             turn_dz2_rows(0, range(2))
             for j in range(2, 4):
@@ -285,21 +288,20 @@ def tile_flaxpositionwisemoelayer_pa_v_kernel(tc, dispatch_mask, x, wi, pre, gra
             load_expert(1)
             load_x()
             load_expert(2)
-            quantize_wi(0)
             quantize_dz2(0, 0)
             quantize_dz2(0, 1)
-
-            turn_wi(1, range(2))
-            for t in range(3):
-                dh(0, t)("vsv"[t])
+            for half in range(2):
+                for row in range(2 * half, 2 * half + 2):
+                    turn_row("wi", 0, row)("s")
+                quantize_wi(0, 2 * half, 2)
+            for t in range(4):
+                dh(0, t)("s")
             relu_backward(1, 0, 2)
-            turn_wi(1, range(2, 4))
+            turn_wi(1, range(4))
             relu_backward(1, 2, 1)
             relu_backward(1, 3, 1)
             turn_dz2_rows(1, range(2))
-            last = dh(0, 3)
             quantize_wi(1)
-            last("s")
             turn_dz2_rows(1, range(2, 4))
             quantize_dz2(1, 0)
             interleave_dz1(0, both, 0)

@@ -259,10 +259,12 @@ def tile_flaxpositionwisemoelayer_pa_v_kernel(tc, dispatch_mask, x, wi, pre, gra
         both = slice(0, G)
 
         def load_expert(e):
-            if e > 0:
+            if e == 3:
                 load_wi(e, 0, 4)
             load_grad(e, 0, 2)
             load_pre(e, 0, 2)
+            if e in (1, 2):
+                load_wi(e, 0, 4)
             load_grad(e, 2, 2)
             for j, n in [(2, 2)] if e == 2 else [(2, 1), (3, 1)]:
                 load_pre(e, j, n)
@@ -297,34 +299,35 @@ def tile_flaxpositionwisemoelayer_pa_v_kernel(tc, dispatch_mask, x, wi, pre, gra
             for t in range(4):
                 dh(0, t)("s")
             relu_backward(1, 0, 2)
+            turn_dz2_rows(1, range(2))
             turn_wi(1, range(4))
+            interleave_dz1(0, both, 0)
             relu_backward(1, 2, 1)
             relu_backward(1, 3, 1)
-            turn_dz2_rows(1, range(2))
             quantize_wi(1)
             turn_dz2_rows(1, range(2, 4))
             quantize_dz2(1, 0)
-            interleave_dz1(0, both, 0)
             for g in range(G):
                 for h in range(2):
                     turn_x(g, h)("s")
             load_expert(3)
             for t in range(4):
-                dh(1, t)("vsss"[t])
-            quantize_x()
+                dh(1, t)("s")
             relu_backward(2, 0, 2)
-            turn_wi(2, range(4))
+            quantize_x()
             interleave_dz1(0, both, 1)
+            turn_dz2_rows(2, range(2))
+            turn_wi(2, range(4))
+            for g in range(G):
+                load_mask(g)
+            quantize_dz1_m(0, 0, G)
+            relu_backward(2, 2, 2)
+            quantize_wi(2)
             for h in range(2):
                 for g in range(G):
                     turn_dz1(0, g, h)("s")
-            for g in range(G):
-                load_mask(g)
-            turn_dz2_rows(2, range(2))
-            relu_backward(2, 2, 2)
-            quantize_dz1_m(0, 0, G)
-            quantize_wi(2)
             turn_dz2_rows(2, range(2, 4))
+            quantize_dz1_slots(0)
             quantize_dz2(2, 0)
             relu_backward(3, 0, 2)
             for half in range(2):
@@ -346,13 +349,12 @@ def tile_flaxpositionwisemoelayer_pa_v_kernel(tc, dispatch_mask, x, wi, pre, gra
                 c("s")
             store_0(0, 1, 0)
             for t in range(2, 4):
-                dh(2, t)("sv"[t % 2])
+                dh(2, t)("v")
             late = [output_0(0, 1, row) for row in range(2, 4)]
-            late[0]("v")
+            late[0]("s")
             interleave_dz1(1, both, 0)
-            quantize_dz1_slots(0)
             for t in range(4):
-                dh(3, t)("s")
+                dh(3, t)("sssv"[t])
             late[1]("s")
             store_0(0, 1, 1)
 
@@ -363,8 +365,8 @@ def tile_flaxpositionwisemoelayer_pa_v_kernel(tc, dispatch_mask, x, wi, pre, gra
             for row in range(4):
                 turn_row("mask", 0, row)("s")
             slots = [turn_dz1(1, g, h) for g in range(G) for h in range(2)]
-            for c in slots:
-                c("v")
+            for i in range(4):
+                slots[i]("svvv"[i])
             quantize_mask(0, 0, 2)
             quantize_dz1_slots(1)
             for g in range(G):

@@ -19,28 +19,22 @@ N = 512
 PAIRS = E // 2
 
 BUFS = {
-    "pre": 4,
-    "grad": 5,
-    "weights": 3,
-    "dz2": 3,
-    "grouped": 4,
-    "wi_codes": 2, "wi_scales": 2, "dz2_codes": 2, "dz2_scales": 2,
-    "dz1": 2, "dz1_by_slot": 2,
-    "dz1_by_m": 1,
-    "result": 4,
+    "pre": 5, "grad": 4, "rows": 3, "x": 2, "dz2": 3, "narrow": 6,
+    "wi_codes": 2, "wi_scales": 2, "dz2_codes": 2, "dz2_scales": 2, "dz1": 4, "dz1_by_m": 3,
+    "x_codes": 2, "x_scales": 2, "mask_codes": 2, "mask_scales": 2,
+    "dz1_m_codes": 3, "dz1_m_scales": 3, "dz1_k_codes": 4, "dz1_k_scales": 4, "result": 4,
 }
-SHARES = {"x": "dz1_by_slot", "result_1": "pre", "wi": "weights", "mask": "weights"}
-DZ2_ROWS = (2, 4, 4, 2)
+SHARES = {"wi": "rows", "mask": "rows"}
 
 
 def tile_flaxpositionwisemoelayer_pa_v_kernel(tc, dispatch_mask, x, wi, pre, grad_out, out_0, out_1):
     nc = tc.nc
 
     mask_rows = dispatch_mask.rearrange("g (p t) e c -> g p t (e c)", t=4)
-    x_rows = x.rearrange("g (p t) m -> p g t m", t=4)
+    x_rows = x.rearrange("g (p t) m -> g p t m", t=4)
     wi_rows = wi.rearrange("e (p t) h -> e p t h", t=4)
-    pre_rows = pre.rearrange("e g c h -> e (g c) h").rearrange("e (p j) h -> e p j h", j=4)
-    grad_rows = grad_out.rearrange("e g c h -> e (g c) h").rearrange("e (p j) h -> e p j h", j=4)
+    pre_rows = pre.rearrange("e g (p j) h -> e g p j h", j=2)
+    grad_rows = grad_out.rearrange("e g (p j) h -> e g p j h", j=2)
     out0_rows = out_0.rearrange("g (p t) e c -> g p t (e c)", t=4)
     out1_rows = out_1.rearrange("g (p t) m -> g p t m", t=4)
 
@@ -51,15 +45,6 @@ def tile_flaxpositionwisemoelayer_pa_v_kernel(tc, dispatch_mask, x, wi, pre, gra
 
         ident = keep.tile([P, P], F32, name="ident")
         make_identity(nc, ident[:])
-
-        x_codes = keep.tile([P, G * S], U32, align_bytes=64, name="x_codes")
-        x_scales = keep.tile([P, G * S], U8, align_bytes=64, name="x_scales")
-        mask_codes = keep.tile([P, G, PAIRS * S], U32, align_bytes=64, name="mask_codes")
-        mask_scales = keep.tile([P, G, PAIRS * S], U8, align_bytes=64, name="mask_scales")
-        dz1_m_codes = keep.tile([P, PAIRS, G, N], U32, align_bytes=64, name="dz1_m_codes")
-        dz1_m_scales = keep.tile([P, PAIRS, G, N], U8, align_bytes=64, name="dz1_m_scales")
-        dz1_k_codes = keep.tile([P, PAIRS, G, N], U32, align_bytes=64, name="dz1_k_codes")
-        dz1_k_scales = keep.tile([P, PAIRS, G, N], U8, align_bytes=64, name="dz1_k_scales")
 
         tiles = {}
 
@@ -78,28 +63,26 @@ def tile_flaxpositionwisemoelayer_pa_v_kernel(tc, dispatch_mask, x, wi, pre, gra
 
         pieces = {}
 
-        def piece(kind, e, j, n, shape, dtype):
-            t = ring_tile(kind, (e, j), shape, dtype)
+        def piece(kind, index, j, n, shape, dtype):
+            t = ring_tile(kind, (index, j), shape, dtype)
             for r in range(j, j + n):
-                pieces[kind, e, r] = (t, r - j)
+                pieces[kind, index, r] = (t, r - j)
             return t
 
-        def load_pre(e, j, n):
-            nc.sync.dma_start(out=piece("pre", e, j, n, [P, n, H], F32)[:], in_=pre_rows[e, :, j : j + n, :])
+        def load_pre(e, g, j=0, n=2):
+            nc.sync.dma_start(out=piece("pre", (e, g), j, n, [P, n, H], F32)[:], in_=pre_rows[e, g, :, j : j + n, :])
 
-        def load_grad(e, j, n):
-            nc.sync.dma_start(out=piece("grad", e, j, n, [P, n, H], BF16)[:], in_=grad_rows[e, :, j : j + n, :])
+        def load_grad(e, g):
+            nc.sync.dma_start(out=piece("grad", (e, g), 0, 2, [P, 2, H], BF16)[:], in_=grad_rows[e, g])
 
-        def load_wi(e, j, n):
+        def load_wi(e, j=0, n=4):
             nc.sync.dma_start(out=piece("wi", e, j, n, [P, n, H], BF16)[:], in_=wi_rows[e, :, j : j + n, :])
 
-        def load_mask(g):
-            t = piece("mask", g, 0, 4, [P, 4, E * C], BF16)
-            nc.sync.dma_start(out=t[:], in_=mask_rows[g])
+        def load_mask(g, j=0, n=4):
+            nc.sync.dma_start(out=piece("mask", g, j, n, [P, n, E * C], BF16)[:], in_=mask_rows[g, :, j : j + n, :])
 
-        def load_x():
-            t = ring_tile("x", 0, [P, G, 4, M], BF16)
-            nc.sync.dma_start(out=t[:], in_=x_rows)
+        def load_x(g):
+            nc.sync.dma_start(out=ring_tile("x", g, [P, 4, M], BF16)[:], in_=x_rows[g])
 
 
         def turn(source, grouped, block):
@@ -112,280 +95,425 @@ def tile_flaxpositionwisemoelayer_pa_v_kernel(tc, dispatch_mask, x, wi, pre, gra
                 grouped()[:].bitcast(F32)[:, N * block : N * (block + 1)].rearrange("p (i r u) -> p i r u", i=2, u=2),
                 bank[:].rearrange("p i u r -> p i r u"))
 
+        parts = {("wi", 0): 2, ("wi", 1): 2, ("wi", 2): 2, ("wi", 3): 2, ("mask", 0): 2, ("mask", 1): 2}
+
+        def grouped_rows(kind, index, row):
+            n = parts.get((kind, index), 4)
+            return ring_tile("narrow" if n == 2 else "wide", (kind, index, row // n), [P, 1024 * n], BF16)
+
         def turn_row(kind, index, row):
             tile, at = pieces[kind, index, row]
             words = tile[:, at, :].bitcast(F32)
             return turn(lambda i, u: words[:, 256 * i + u : 256 * (i + 1) : 2],
-                        lambda: ring_tile("grouped", (kind, index), [P, 4096], BF16), row)
+                        lambda: grouped_rows(kind, index, row), row % parts.get((kind, index), 4))
 
         def turn_x(g, h):
-            rows = tiles["x", 0][:, g]
+            rows = tiles["x", g]
             return turn(lambda i, u: rows[:, 2 * h + i, :].bitcast(F32)[:, u::2],
-                        lambda: ring_tile("grouped", "x", [P, 4096], BF16), 2 * g + h)
+                        lambda: ring_tile("narrow", ("x", g), [P, 2048], BF16), h)
 
-        def turn_dz2(e, j):
-            dz2, at = pieces["dz2", e, j]
+        def turn_dz2(e, g, j):
+            dz2, at = pieces["dz2", (e, g), j]
             bank = psum.tile([P, 2, 2, P], F32, tag="bank", name="bank")
-            for a in range(2):
-                for u in range(2):
+            for u in range(2):
+                for a in range(2):
                     nc.tensor.transpose(bank[:, a, u, :], dz2[:, u, at, 256 * a : 256 * (a + 1)].bitcast(F32), ident[:])
-            n = DZ2_ROWS[e]
             return lambda engine: copy(
                 engine,
-                ring_tile("grouped", ("dz2", e, j // n), [P, 1024 * n], BF16)[:].bitcast(F32).rearrange(
-                    "p (a j r u) -> p a j r u", a=2, j=n, u=2)[:, :, j % n],
+                ring_tile("narrow", ("dz2", e, g), [P, 2048], BF16)[:].bitcast(F32).rearrange(
+                    "p (a j r u) -> p a j r u", a=2, j=2, u=2)[:, :, j],
                 bank[:].rearrange("p a u r -> p a r u"))
 
         def turn_dz1(pair, g, h):
-            dz1 = tiles["dz1", pair]
-            return turn(lambda i, u: dz1[:, 2 * h + i, g, u, :].bitcast(F32),
-                        lambda: ring_tile("dz1_by_slot", pair, [P, 4096], BF16), 2 * g + h)
+            dz1 = tiles["dz1", (pair, g)]
+            return turn(lambda i, u: dz1[:, 2 * h + i, u, :].bitcast(F32),
+                        lambda: ring_tile("narrow", ("dz1", pair, g), [P, 2048], BF16), h)
 
 
-        def relu_backward(e, j, n):
-            dz2 = piece("dz2", e, j, n, [P, 2, n, N], BF16)
-            pre_tile, pre_at = pieces["pre", e, j]
-            grad_tile, grad_at = pieces["grad", e, j]
+        def relu_backward(e, g, j=0, n=2):
+            dz2 = piece("dz2", (e, g), j, n, [P, 2, n, N], BF16)
+            pre_tile, pre_at = pieces["pre", (e, g), j]
+            grad_tile, grad_at = pieces["grad", (e, g), j]
             pre_words = pre_tile[:, pre_at : pre_at + n, :].rearrange("p j (k u b) -> p u j k b", u=2, b=2)
             grad = grad_tile[:, grad_at : grad_at + n, :].rearrange("p j (k u b) -> p u j k b", u=2, b=2)
-            for u in range(2):
+            for u, rows in [(0, slice(0, n))] + [(1, slice(r, r + 1)) for r in range(n)]:
                 nc.vector.scalar_tensor_tensor(
-                    out=dz2[:, u].rearrange("p j (k b) -> p j k b", b=2),
-                    in0=pre_words[:, u], scalar=0.0, in1=grad[:, u], op0=ALU.is_gt, op1=ALU.mult)
+                    out=dz2[:, u, rows].rearrange("p j (k b) -> p j k b", b=2),
+                    in0=pre_words[:, u, rows], scalar=0.0, in1=grad[:, u, rows], op0=ALU.is_gt, op1=ALU.mult)
 
-        def quantize_wi(e, row=0, n=4):
-            codes = ring_tile("wi_codes", e, [P, 2 * M], U32)
-            scales = ring_tile("wi_scales", e, [P, 2 * M], U8)
-            cols = slice(256 * row, 256 * (row + n))
-            nc.vector.quantize_mx(
-                out=codes[:, cols].bitcast(E4M3), scales=scales[:, cols],
-                in_=tiles["grouped", ("wi", e)][:, 4 * cols.start : 4 * cols.stop])
+        def quantize(kind, key, words, first, grouped, fmt):
+            codes = ring_tile(kind + "_codes", key, [P, words], U32)
+            scales = ring_tile(kind + "_scales", key, [P, words], U8)
+            cols = slice(first, first + grouped.shape[1] // 4)
+            nc.vector.quantize_mx(out=codes[:, cols].bitcast(fmt), scales=scales[:, cols], in_=grouped)
 
-        def quantize_dz2(e, part):
-            codes = ring_tile("dz2_codes", e, [P, 2 * N], U32)
-            scales = ring_tile("dz2_scales", e, [P, 2 * N], U8)
-            grouped = tiles["grouped", ("dz2", e, part)]
-            if DZ2_ROWS[e] == 4:
-                nc.vector.quantize_mx(out=codes[:].bitcast(E5M2), scales=scales[:], in_=grouped[:])
-                return
-            for a in range(2):
-                cols = slice(N * a + 256 * part, N * a + 256 * (part + 1))
-                nc.vector.quantize_mx(
-                    out=codes[:, cols].bitcast(E5M2), scales=scales[:, cols], in_=grouped[:, 1024 * a : 1024 * (a + 1)])
+        def operand(kind, key, first, n, fmt):
+            cols = slice(first, first + n)
+            return tiles[kind + "_codes", key][:, cols].bitcast(fmt), tiles[kind + "_scales", key][:, cols]
 
-        def quantize_mask(g, half, n):
-            cols = slice(N * half, N * (half + n))
-            nc.vector.quantize_mx(
-                out=mask_codes[:, g, cols].bitcast(E4M3), scales=mask_scales[:, g, cols],
-                in_=tiles["grouped", ("mask", g)][:, 4 * cols.start : 4 * cols.stop])
+        def quantize_rows(kind, index, row=0):
+            quantize(kind, index, 1024, 256 * row, grouped_rows(kind, index, row)[:], E4M3)
 
-        def quantize_x():
-            nc.vector.quantize_mx(out=x_codes[:].bitcast(E4M3), scales=x_scales[:], in_=tiles["grouped", "x"][:])
+        def quantize_x(g):
+            quantize("x", g, N, 0, tiles["narrow", ("x", g)][:], E4M3)
 
-        def quantize_dz1_m(pair, g, n):
-            nc.vector.quantize_mx(
-                out=dz1_m_codes[:, pair, g : g + n, :].rearrange("p g w -> p (g w)").bitcast(E5M2),
-                scales=dz1_m_scales[:, pair, g : g + n, :].rearrange("p g w -> p (g w)"),
-                in_=tiles["dz1_by_m", pair][:, g : g + n].rearrange("p g u i s t -> p (g u i s t)"))
+        def quantize_dz2(e, g):
+            quantize("dz2", (e, g), N, 0, tiles["narrow", ("dz2", e, g)][:], E5M2)
 
-        def quantize_dz1_slots(pair):
-            nc.vector.quantize_mx(
-                out=dz1_k_codes[:, pair].rearrange("p g w -> p (g w)").bitcast(E5M2),
-                scales=dz1_k_scales[:, pair].rearrange("p g w -> p (g w)"),
-                in_=tiles["dz1_by_slot", pair][:])
+        def quantize_dz1_m(e, g):
+            quantize("dz1_m", (e, g), C, 0, tiles["dz1_by_m", (e, g)][:].rearrange("p u s t -> p (u s t)"), E5M2)
+
+        def quantize_dz1_slots(pair, g):
+            quantize("dz1_k", (pair, g), N, 0, tiles["narrow", ("dz1", pair, g)][:], E5M2)
+
+        def product(out, lhs, rhs, start, stop):
+            nc.tensor.matmul_mx(out=out, lhsT=lhs[0], lhsT_scale=lhs[1], rhs=rhs[0], rhs_scale=rhs[1],
+                                start=start, stop=stop)
 
 
-        def dh(e, t):
-            sums = psum.tile([P, N], F32, tag="bank", name="dh")
-            for a in range(2):
-                w_cols = slice(256 * t + P * a, 256 * t + P * (a + 1))
-                d_cols = slice(N * a, N * (a + 1))
-                nc.tensor.matmul_mx(
-                    out=sums[:],
-                    lhsT=tiles["wi_codes", e][:, w_cols].bitcast(E4M3), lhsT_scale=tiles["wi_scales", e][:, w_cols],
-                    rhs=tiles["dz2_codes", e][:, d_cols].bitcast(E5M2), rhs_scale=tiles["dz2_scales", e][:, d_cols],
-                    start=(a == 0), stop=(a == 1))
+        def dh(e, g, h):
+            sums = psum.tile([P, 2, C], F32, tag="bank", name="dh")
+            for t in range(2):
+                for a in range(2):
+                    product(sums[:, t, :], operand("wi", e, 256 * (2 * h + t) + P * a, P, E4M3),
+                            operand("dz2", (e, g), C * a, C, E5M2), a == 0, a == 1)
             pair, i = divmod(e, 2)
             return lambda engine: copy(
                 engine,
-                ring_tile("dz1", pair, [P, 4, G, 2, 256], BF16)[:, t, :, :, P * i : P * (i + 1)].rearrange(
-                    "p g u (q b) -> p g u q b", b=2),
-                sums[:].rearrange("p (u b g q) -> p g u q b", u=2, b=2, g=2))
+                ring_tile("dz1", (pair, g), [P, 4, 2, 256], BF16)[:, 2 * h : 2 * h + 2, :, P * i : P * (i + 1)].rearrange(
+                    "p t u (q b) -> p t u q b", b=2),
+                sums[:].rearrange("p t (b q u) -> p t u q b", b=2, u=2))
 
-        def interleave_dz1(pair, groups, experts):
-            by_m = ring_tile("dz1_by_m", pair, [P, G, 2, 2, P, 4], BF16)
+        def interleave_dz1(e, g):
+            pair, i = divmod(e, 2)
+            by_m = ring_tile("dz1_by_m", (e, g), [P, 2, P, 4], BF16)
             nc.vector.tensor_copy(
-                out=by_m[:].rearrange("p g u i (c n) t -> p g u i c t n", n=4)[:, groups, :, experts],
-                in_=tiles["dz1", pair][:].rearrange("p t g u (i c n) -> p g u i c t n", i=2, n=4)[:, groups, :, experts])
+                out=by_m[:].rearrange("p u (c n) t -> p u c t n", n=4),
+                in_=tiles["dz1", (pair, g)][:, :, :, P * i : P * (i + 1)].rearrange("p t u (c n) -> p u c t n", n=4))
 
 
-        def output_0(pair, g, row):
-            half, t = divmod(row, 2)
-            acc = psum.tile([P, N], F32, tag="bank", name="acc")
-            cols = slice(S * g + P * row, S * g + P * (row + 1))
-            nc.tensor.matmul_mx(
-                out=acc[:], lhsT=x_codes[:, cols].bitcast(E4M3), lhsT_scale=x_scales[:, cols],
-                rhs=dz1_m_codes[:, pair, g, :].bitcast(E5M2), rhs_scale=dz1_m_scales[:, pair, g, :],
-                start=True, stop=True)
+        def result_0(e, g, h):
+            if g == 0:
+                return ring_tile("result", (0, h), [P, 2, E * C], F32)[:, :, C * e : C * (e + 1)]
+            pair, i = divmod(e, 2)
+            if pair == 0:
+                return ring_tile("result", (1, pair), [P, 4, N], F32)[:, 2 * h : 2 * h + 2, C * i : C * (i + 1)]
+            return ring_tile("result", (1, pair, i), [P, 4, C], F32)[:, 2 * h : 2 * h + 2, :]
+
+        def output_0(e, g, h):
+            acc = psum.tile([P, 2, C], F32, tag="bank", name="acc")
+            for t in range(2):
+                product(acc[:, t, :], operand("x", g, P * (2 * h + t), P, E4M3), operand("dz1_m", (e, g), 0, C, E5M2),
+                        True, True)
+            return lambda engine: copy(
+                engine, result_0(e, g, h).rearrange("p t (q u b) -> p t q u b", u=2, b=2),
+                acc[:].rearrange("p t (u q b) -> p t q u b", u=2, b=2))
+
+        def store_0(key, g, rows, cols):
+            nc.sync.dma_start(out=out0_rows[g, :, rows, cols], in_=tiles["result", key][:])
+
+        def output_1(g, row, pairs=range(PAIRS)):
+            if ("acc1", g, row) not in tiles:
+                tiles["acc1", g, row] = psum.tile([P, N], F32, tag="bank", name="acc1")
+            acc = tiles["acc1", g, row]
+            for pair in pairs:
+                product(acc[:], operand("mask", g, 256 * row + P * pair, P, E4M3),
+                        operand("dz1_k", (pair, g), 0, N, E5M2), pair == 0, pair == 1)
             return lambda engine: copy(
                 engine,
-                ring_tile("result", ("out_0", pair, g, half), [P, 2, N], F32)[:, t, :].rearrange(
-                    "p (i q u b) -> p i q u b", i=2, u=2, b=2),
-                acc[:].rearrange("p (u i q b) -> p i q u b", i=2, u=2, b=2))
-
-        def store_0(pair, g, half):
-            nc.sync.dma_start(
-                out=out0_rows[g, :, 2 * half : 2 * half + 2, N * pair : N * (pair + 1)],
-                in_=tiles["result", ("out_0", pair, g, half)][:])
-
-        def output_1(g, row):
-            acc = psum.tile([P, N], F32, tag="bank", name="acc1")
-            for pair in range(PAIRS):
-                cols = slice(256 * row + P * pair, 256 * row + P * (pair + 1))
-                nc.tensor.matmul_mx(
-                    out=acc[:],
-                    lhsT=mask_codes[:, g, cols].bitcast(E4M3), lhsT_scale=mask_scales[:, g, cols],
-                    rhs=dz1_k_codes[:, pair, g, :].bitcast(E5M2), rhs_scale=dz1_k_scales[:, pair, g, :],
-                    start=(pair == 0), stop=(pair == 1))
-            return lambda engine: copy(
-                engine,
-                ring_tile("result_1", g, [P, 4, N], F32)[:, row, :].rearrange("p (m t) -> p m t", t=4),
+                ring_tile("pre", ("out_1", g), [P, 4, N], F32)[:, row, :].rearrange("p (m t) -> p m t", t=4),
                 acc[:].rearrange("p (t m) -> p m t", t=4))
 
         def store_1(g, row, n):
-            nc.sync.dma_start(out=out1_rows[g, :, row : row + n, :], in_=tiles["result_1", g][:, row : row + n, :])
+            nc.sync.dma_start(out=out1_rows[g, :, row : row + n, :], in_=tiles["pre", ("out_1", g)][:, row : row + n, :])
 
 
-        both = slice(0, G)
-
-        def load_expert(e):
-            if e == 3:
-                load_wi(e, 0, 4)
-            load_grad(e, 0, 2)
-            load_pre(e, 0, 2)
-            if e in (1, 2):
-                load_wi(e, 0, 4)
-            load_grad(e, 2, 2)
-            for j, n in [(2, 2)] if e == 2 else [(2, 1), (3, 1)]:
-                load_pre(e, j, n)
-            if e == 0:
-                for half in range(2):
-                    load_wi(e, 2 * half, 2)
-
-        def turn_wi(e, rows):
-            for row in rows:
-                turn_row("wi", e, row)("s")
-
-        def turn_dz2_rows(e, rows):
-            for j in rows:
-                turn_dz2(e, j)("s")
-
+        banks = {}
         with tc.manual_schedule():
-            load_expert(0)
-            relu_backward(0, 0, 2)
-            turn_dz2_rows(0, range(2))
-            for j in range(2, 4):
-                relu_backward(0, j, 1)
-                turn_dz2(0, j)("s")
-            load_expert(1)
-            load_x()
-            load_expert(2)
+            load_x(0)
+            load_grad(0, 0)
+            load_pre(0, 0, 0, 1)
+            relu_backward(0, 0, 0, 1)
+            load_pre(0, 0, 1, 1)
+            relu_backward(0, 0, 1, 1)
+            banks["Tx0.0"] = turn_x(0, 0)
+            banks["Tx0.0"]("s")
+            banks["Tx0.1"] = turn_x(0, 1)
+            banks["Tx0.1"]("s")
+            quantize_x(0)
+            banks["T20.0"] = turn_dz2(0, 0, 0)
+            banks["T20.1"] = turn_dz2(0, 0, 1)
+            load_wi(0, 0, 2)
+            banks["Tw0.0"] = turn_row("wi", 0, 0)
+            banks["Tw0.0"]("v")
+            banks["T20.0"]("s")
+            banks["T20.1"]("s")
             quantize_dz2(0, 0)
+            banks["Tw0.1"] = turn_row("wi", 0, 1)
+            banks["Tw0.1"]("s")
+            quantize_rows("wi", 0, 0)
+            load_wi(0, 2, 2)
+            banks["Tw0.2"] = turn_row("wi", 0, 2)
+            banks["Tw0.2"]("s")
+            banks["Tw0.3"] = turn_row("wi", 0, 3)
+            banks["Tw0.3"]("s")
+            quantize_rows("wi", 0, 2)
+            load_grad(0, 1)
+            load_pre(0, 1, 0, 1)
+            relu_backward(0, 1, 0, 1)
+            load_pre(0, 1, 1, 1)
+            relu_backward(0, 1, 1, 1)
+            banks["D0.0"] = dh(0, 0, 0)
+            banks["D0.0"]("s")
+            banks["D0.1"] = dh(0, 0, 1)
+            banks["D0.1"]("s")
+            interleave_dz1(0, 0)
+            banks["T21.0"] = turn_dz2(0, 1, 0)
+            banks["T21.1"] = turn_dz2(0, 1, 1)
+            load_wi(1, 0, 4)
+            banks["Tw1.0"] = turn_row("wi", 1, 0)
+            banks["Tw1.0"]("v")
+            banks["T21.0"]("s")
+            banks["T21.1"]("s")
             quantize_dz2(0, 1)
-            for half in range(2):
-                for row in range(2 * half, 2 * half + 2):
-                    turn_row("wi", 0, row)("s")
-                quantize_wi(0, 2 * half, 2)
-            for t in range(4):
-                dh(0, t)("s")
-            relu_backward(1, 0, 2)
-            turn_dz2_rows(1, range(2))
-            turn_wi(1, range(4))
-            interleave_dz1(0, both, 0)
-            relu_backward(1, 2, 1)
-            relu_backward(1, 3, 1)
-            quantize_wi(1)
-            turn_dz2_rows(1, range(2, 4))
+            quantize_dz1_m(0, 0)
+            banks["Tw1.1"] = turn_row("wi", 1, 1)
+            banks["Tw1.1"]("s")
+            quantize_rows("wi", 1, 0)
+            load_grad(1, 0)
+            load_pre(1, 0, 0, 1)
+            relu_backward(1, 0, 0, 1)
+            load_pre(1, 0, 1, 1)
+            relu_backward(1, 0, 1, 1)
+            banks["Tw1.2"] = turn_row("wi", 1, 2)
+            banks["Tw1.2"]("s")
+            banks["Tw1.3"] = turn_row("wi", 1, 3)
+            banks["Tw1.3"]("s")
+            quantize_rows("wi", 1, 2)
+            banks["O00.0"] = output_0(0, 0, 0)
+            banks["O00.0"]("s")
+            banks["O00.1"] = output_0(0, 0, 1)
+            banks["O00.1"]("s")
+            banks["D1.0"] = dh(0, 1, 0)
+            banks["D1.0"]("s")
+            banks["D1.1"] = dh(0, 1, 1)
+            banks["D1.1"]("s")
+            interleave_dz1(0, 1)
+            banks["T22.0"] = turn_dz2(1, 0, 0)
+            banks["T22.1"] = turn_dz2(1, 0, 1)
+            load_x(1)
+            banks["Tx1.0"] = turn_x(1, 0)
+            banks["Tx1.0"]("v")
+            banks["T22.0"]("s")
+            banks["T22.1"]("s")
             quantize_dz2(1, 0)
-            for g in range(G):
-                for h in range(2):
-                    turn_x(g, h)("s")
-            load_expert(3)
-            for t in range(4):
-                dh(1, t)("s")
-            relu_backward(2, 0, 2)
-            quantize_x()
-            interleave_dz1(0, both, 1)
-            turn_dz2_rows(2, range(2))
-            turn_wi(2, range(4))
-            for g in range(G):
-                load_mask(g)
-            quantize_dz1_m(0, 0, G)
-            relu_backward(2, 2, 2)
-            quantize_wi(2)
-            for h in range(2):
-                for g in range(G):
-                    turn_dz1(0, g, h)("s")
-            turn_dz2_rows(2, range(2, 4))
-            quantize_dz1_slots(0)
+            load_grad(1, 1)
+            load_pre(1, 1, 0, 1)
+            relu_backward(1, 1, 0, 1)
+            load_pre(1, 1, 1, 1)
+            relu_backward(1, 1, 1, 1)
+            banks["Tx1.1"] = turn_x(1, 1)
+            banks["Tx1.1"]("s")
+            quantize_x(1)
+            banks["D2.0"] = dh(1, 0, 0)
+            banks["D2.0"]("s")
+            banks["D2.1"] = dh(1, 0, 1)
+            banks["D2.1"]("s")
+            interleave_dz1(1, 0)
+            quantize_dz1_m(0, 1)
+            banks["T23.0"] = turn_dz2(1, 1, 0)
+            banks["Ts00.0"] = turn_dz1(0, 0, 0)
+            banks["T23.1"] = turn_dz2(1, 1, 1)
+            load_wi(2, 0, 4)
+            banks["Tw2.0"] = turn_row("wi", 2, 0)
+            banks["Tw2.0"]("v")
+            banks["T23.0"]("s")
+            banks["T23.1"]("s")
+            quantize_dz2(1, 1)
+            banks["Ts00.0"]("s")
+            banks["Tw2.1"] = turn_row("wi", 2, 1)
+            banks["Tw2.1"]("s")
+            quantize_rows("wi", 2, 0)
+            load_grad(2, 0)
+            load_pre(2, 0, 0, 1)
+            relu_backward(2, 0, 0, 1)
+            load_pre(2, 0, 1, 1)
+            relu_backward(2, 0, 1, 1)
+            banks["Tw2.2"] = turn_row("wi", 2, 2)
+            banks["Tw2.2"]("s")
+            banks["Tw2.3"] = turn_row("wi", 2, 3)
+            banks["Tw2.3"]("s")
+            quantize_rows("wi", 2, 2)
+            banks["O01.0"] = output_0(0, 1, 0)
+            banks["O01.0"]("s")
+            banks["O01.1"] = output_0(0, 1, 1)
+            banks["O01.1"]("s")
+            banks["D3.0"] = dh(1, 1, 0)
+            banks["D3.0"]("s")
+            banks["D3.1"] = dh(1, 1, 1)
+            banks["D3.1"]("s")
+            interleave_dz1(1, 1)
+            quantize_dz1_m(1, 0)
+            banks["T24.0"] = turn_dz2(2, 0, 0)
+            banks["Ts00.1"] = turn_dz1(0, 0, 1)
+            banks["T24.1"] = turn_dz2(2, 0, 1)
+            load_wi(3, 0, 4)
+            banks["Tw3.0"] = turn_row("wi", 3, 0)
+            banks["Tw3.0"]("v")
+            banks["T24.0"]("s")
+            banks["T24.1"]("s")
             quantize_dz2(2, 0)
-            relu_backward(3, 0, 2)
-            for half in range(2):
-                turn_wi(3, range(2 * half, 2 * half + 2))
-                for row in range(2 * half, 2 * half + 2):
-                    output_0(0, 0, row)("s")
-                store_0(0, 0, half)
-            late = [output_0(0, 1, row) for row in range(2)]
-            dh(2, 0)("s")
-            late += [dh(2, 1)]
-            turn_dz2_rows(3, range(2))
-            relu_backward(3, 2, 1)
-            relu_backward(3, 3, 1)
-            quantize_wi(3)
-            turn_dz2_rows(3, range(2, 4))
+            banks["Ts00.1"]("s")
+            banks["Tw3.1"] = turn_row("wi", 3, 1)
+            banks["Tw3.1"]("s")
+            quantize_rows("wi", 3, 0)
+            load_grad(3, 0)
+            load_pre(3, 0, 0, 1)
+            relu_backward(3, 0, 0, 1)
+            load_pre(3, 0, 1, 1)
+            relu_backward(3, 0, 1, 1)
+            banks["Tw3.2"] = turn_row("wi", 3, 2)
+            banks["Tw3.2"]("s")
+            banks["Tw3.3"] = turn_row("wi", 3, 3)
+            banks["Tw3.3"]("s")
+            quantize_rows("wi", 3, 2)
+            banks["O02.0"] = output_0(1, 0, 0)
+            banks["O02.0"]("s")
+            banks["O02.1"] = output_0(1, 0, 1)
+            banks["O02.1"]("s")
+            banks["D4.0"] = dh(2, 0, 0)
+            banks["D4.0"]("s")
+            banks["D4.1"] = dh(2, 0, 1)
+            banks["D4.1"]("s")
+            interleave_dz1(2, 0)
+            quantize_dz1_m(1, 1)
+            quantize_dz1_slots(0, 0)
+            banks["T25.0"] = turn_dz2(3, 0, 0)
+            banks["T25.0"]("s")
+            banks["T25.1"] = turn_dz2(3, 0, 1)
+            banks["T25.1"]("s")
             quantize_dz2(3, 0)
+            quantize_dz1_m(2, 0)
+            load_mask(0, 0, 4)
+            banks["Tm0.0"] = turn_row("mask", 0, 0)
+            banks["Tm0.0"]("s")
+            banks["Tm0.1"] = turn_row("mask", 0, 1)
+            banks["Tm0.1"]("s")
+            quantize_rows("mask", 0, 0)
+            load_grad(2, 1)
+            load_pre(2, 1, 0, 1)
+            relu_backward(2, 1, 0, 1)
+            load_pre(2, 1, 1, 1)
+            relu_backward(2, 1, 1, 1)
+            banks["Tm0.2"] = turn_row("mask", 0, 2)
+            banks["Tm0.2"]("s")
+            banks["Tm0.3"] = turn_row("mask", 0, 3)
+            banks["Tm0.3"]("s")
+            quantize_rows("mask", 0, 2)
+            banks["O03.0"] = output_0(1, 1, 0)
+            banks["O03.0"]("s")
+            banks["O03.1"] = output_0(1, 1, 1)
+            banks["O03.1"]("s")
+            banks["D5.0"] = dh(3, 0, 0)
+            banks["D5.0"]("s")
+            banks["D5.1"] = dh(3, 0, 1)
+            banks["D5.1"]("s")
+            interleave_dz1(3, 0)
+            banks["O04.0"] = output_0(2, 0, 0)
+            banks["O04.1"] = output_0(2, 0, 1)
+            banks["T26.0"] = turn_dz2(2, 1, 0)
+            banks["T26.1"] = turn_dz2(2, 1, 1)
+            banks["Ts10.0"] = turn_dz1(1, 0, 0)
+            banks["Ts10.0"]("v")
+            banks["T26.0"]("s")
+            banks["T26.1"]("s")
+            quantize_dz2(2, 1)
+            quantize_dz1_m(3, 0)
+            banks["Ts10.1"] = turn_dz1(1, 0, 1)
+            banks["Ts10.1"]("s")
+            quantize_dz1_slots(1, 0)
+            load_mask(1, 0, 4)
+            load_grad(3, 1)
+            load_pre(3, 1, 0, 1)
+            relu_backward(3, 1, 0, 1)
+            load_pre(3, 1, 1, 1)
+            relu_backward(3, 1, 1, 1)
+            banks["Tm1.0"] = turn_row("mask", 1, 0)
+            banks["Tm1.1"] = turn_row("mask", 1, 1)
+            banks["Tm1.1"]("v")
+            banks["O04.0"]("s")
+            banks["O04.1"]("s")
+            banks["Tm1.0"]("s")
+            banks["Ts01.0"] = turn_dz1(0, 1, 0)
+            banks["Ts01.1"] = turn_dz1(0, 1, 1)
+            banks["O05.0"] = output_0(3, 0, 0)
+            banks["O05.0"]("s")
+            banks["O05.1"] = output_0(3, 0, 1)
+            banks["O05.1"]("s")
+            banks["D6.0"] = dh(2, 1, 0)
+            banks["D6.0"]("s")
+            banks["D6.1"] = dh(2, 1, 1)
+            banks["D6.1"]("s")
+            interleave_dz1(2, 1)
+            banks["T27.0"] = turn_dz2(3, 1, 0)
+            banks["Tm1.2"] = turn_row("mask", 1, 2)
+            banks["T27.1"] = turn_dz2(3, 1, 1)
+            banks["T27.1"]("v")
+            quantize_dz1_m(2, 1)
+            banks["T27.0"]("s")
             quantize_dz2(3, 1)
-            for c in late:
-                c("s")
-            store_0(0, 1, 0)
-            for t in range(2, 4):
-                dh(2, t)("v")
-            late = [output_0(0, 1, row) for row in range(2, 4)]
-            late[0]("s")
-            interleave_dz1(1, both, 0)
-            for t in range(4):
-                dh(3, t)("sssv"[t])
-            late[1]("s")
-            store_0(0, 1, 1)
-
-            for g in range(G):
-                interleave_dz1(1, g, 1)
-            for g in range(G):
-                quantize_dz1_m(1, g, 1)
-            for row in range(4):
-                turn_row("mask", 0, row)("s")
-            slots = [turn_dz1(1, g, h) for g in range(G) for h in range(2)]
-            for i in range(4):
-                slots[i]("svvv"[i])
-            quantize_mask(0, 0, 2)
-            quantize_dz1_slots(1)
-            for g in range(G):
-                for row in range(4):
-                    output_0(1, g, row)("s")
-                    if row % 2:
-                        store_0(1, g, row // 2)
-            for row in range(4):
-                turn_row("mask", 1, row)("vvsv"[row])
-                if row == 1:
-                    quantize_mask(1, 0, 1)
-            quantize_mask(1, 1, 1)
-            for row in range(4):
-                output_1(0, row)("s")
-                if row % 2:
-                    store_1(0, row - 1, 2)
-            for row in range(4):
-                output_1(1, row)("vs"[row % 2])
-                if row == 1:
-                    store_1(1, 0, 2)
-                if row >= 2:
-                    store_1(1, row, 1)
+            banks["Tm1.3"] = turn_row("mask", 1, 3)
+            banks["O10.0"] = output_1(0, 0)
+            banks["O10.1"] = output_1(0, 1)
+            banks["O10.1"]("v")
+            quantize_rows("mask", 1, 0)
+            banks["O06.0"] = output_0(2, 1, 0)
+            banks["O06.1"] = output_0(2, 1, 1)
+            banks["D7.0"] = dh(3, 1, 0)
+            banks["D7.0"]("v")
+            banks["Ts01.0"]("s")
+            banks["Ts01.1"]("s")
+            quantize_dz1_slots(0, 1)
+            banks["O10.0"]("s")
+            banks["Tm1.2"]("s")
+            banks["O06.0"]("s")
+            banks["O06.1"]("s")
+            banks["D7.1"] = dh(3, 1, 1)
+            banks["D7.1"]("s")
+            interleave_dz1(3, 1)
+            banks["O10.2"] = output_1(0, 2)
+            banks["O10.3"] = output_1(0, 3)
+            banks["Ts11.0"] = turn_dz1(1, 1, 0)
+            banks["Ts11.0"]("v")
+            quantize_dz1_m(3, 1)
+            banks["O10.2"]("s")
+            banks["O10.3"]("s")
+            banks["Ts11.1"] = turn_dz1(1, 1, 1)
+            banks["Ts11.1"]("s")
+            quantize_dz1_slots(1, 1)
+            banks["Tm1.3"]("s")
+            quantize_rows("mask", 1, 2)
+            output_1(1, 0, [0])
+            output_1(1, 1, [0])
+            banks["O07.0"] = output_0(3, 1, 0)
+            banks["O07.1"] = output_0(3, 1, 1)
+            banks["O07.1"]("v")
+            banks["O11.0"] = output_1(1, 0, [1])
+            banks["O11.0"]("v")
+            banks["O11.1"] = output_1(1, 1, [1])
+            banks["O11.2"] = output_1(1, 2)
+            banks["O11.2"]("v")
+            banks["O07.0"]("s")
+            banks["O11.1"]("s")
+            banks["O11.3"] = output_1(1, 3)
+            banks["O11.3"]("s")
+            store_0((1, 0), 1, slice(0, 4), slice(0, N))
+            store_0((0, 0), 0, slice(0, 2), slice(0, E * C))
+            store_0((0, 1), 0, slice(2, 4), slice(0, E * C))
+            store_1(0, 0, 2)
+            store_0((1, 1, 0), 1, slice(0, 4), slice(2 * C, 3 * C))
+            store_1(0, 2, 2)
+            store_0((1, 1, 1), 1, slice(0, 4), slice(3 * C, 4 * C))
+            store_1(1, 0, 2)
+            store_1(1, 2, 1)
+            store_1(1, 3, 1)

@@ -19,10 +19,10 @@ N = 512
 PAIRS = E // 2
 
 BUFS = {
-    "pre": 5, "grad": 4, "rows": 3, "x": 2, "dz2": 3, "narrow": 6,
+    "pre": 5, "grad": 4, "rows": 3, "x": 2, "dz2": 3, "wide": 1, "narrow": 5,
     "wi_codes": 2, "wi_scales": 2, "dz2_codes": 2, "dz2_scales": 2, "dz1": 4, "dz1_by_m": 3,
     "x_codes": 2, "x_scales": 2, "mask_codes": 2, "mask_scales": 2,
-    "dz1_m_codes": 3, "dz1_m_scales": 3, "dz1_k_codes": 4, "dz1_k_scales": 4, "result": 4,
+    "dz1_m_codes": 3, "dz1_m_scales": 3, "dz1_k_codes": 4, "dz1_k_scales": 4, "result": 5,
 }
 SHARES = {"wi": "rows", "mask": "rows"}
 
@@ -95,7 +95,7 @@ def tile_flaxpositionwisemoelayer_pa_v_kernel(tc, dispatch_mask, x, wi, pre, gra
                 grouped()[:].bitcast(F32)[:, N * block : N * (block + 1)].rearrange("p (i r u) -> p i r u", i=2, u=2),
                 bank[:].rearrange("p i u r -> p i r u"))
 
-        parts = {("wi", 0): 2, ("wi", 1): 2, ("wi", 2): 2, ("wi", 3): 2, ("mask", 0): 2, ("mask", 1): 2}
+        parts = {("wi", 0): 2, ("mask", 1): 2}
 
         def grouped_rows(kind, index, row):
             n = parts.get((kind, index), 4)
@@ -198,6 +198,8 @@ def tile_flaxpositionwisemoelayer_pa_v_kernel(tc, dispatch_mask, x, wi, pre, gra
             pair, i = divmod(e, 2)
             if pair == 0:
                 return ring_tile("result", (1, pair), [P, 4, N], F32)[:, 2 * h : 2 * h + 2, C * i : C * (i + 1)]
+            if i == 1:
+                return ring_tile("result", (1, pair, i, h), [P, 2, C], F32)[:]
             return ring_tile("result", (1, pair, i), [P, 4, C], F32)[:, 2 * h : 2 * h + 2, :]
 
         def output_0(e, g, h):
@@ -224,97 +226,101 @@ def tile_flaxpositionwisemoelayer_pa_v_kernel(tc, dispatch_mask, x, wi, pre, gra
                 ring_tile("pre", ("out_1", g), [P, 4, N], F32)[:, row, :].rearrange("p (m t) -> p m t", t=4),
                 acc[:].rearrange("p (t m) -> p m t", t=4))
 
+        def warm_up(n):
+            unread = psum.tile([P, n, P], F32, tag="bank", name="unread")
+            for i in range(n):
+                nc.tensor.matmul(out=unread[:, i, :], lhsT=ident[:], rhs=ident[:], start=True, stop=True)
+
         def store_1(g, row, n):
             nc.sync.dma_start(out=out1_rows[g, :, row : row + n, :], in_=tiles["pre", ("out_1", g)][:, row : row + n, :])
 
 
         banks = {}
         with tc.manual_schedule():
-            load_x(0)
+            load_wi(0, 0, 2)
             load_grad(0, 0)
             load_pre(0, 0, 0, 1)
             relu_backward(0, 0, 0, 1)
             load_pre(0, 0, 1, 1)
             relu_backward(0, 0, 1, 1)
-            banks["Tx0.0"] = turn_x(0, 0)
-            banks["Tx0.0"]("s")
-            banks["Tx0.1"] = turn_x(0, 1)
-            banks["Tx0.1"]("s")
-            quantize_x(0)
-            banks["T20.0"] = turn_dz2(0, 0, 0)
-            banks["T20.1"] = turn_dz2(0, 0, 1)
-            load_wi(0, 0, 2)
             banks["Tw0.0"] = turn_row("wi", 0, 0)
-            banks["Tw0.0"]("v")
-            banks["T20.0"]("s")
-            banks["T20.1"]("s")
-            quantize_dz2(0, 0)
+            banks["Tw0.0"]("s")
             banks["Tw0.1"] = turn_row("wi", 0, 1)
             banks["Tw0.1"]("s")
             quantize_rows("wi", 0, 0)
+            banks["T20.0"] = turn_dz2(0, 0, 0)
+            banks["T20.0"]("s")
+            banks["T20.1"] = turn_dz2(0, 0, 1)
+            banks["T20.1"]("s")
+            quantize_dz2(0, 0)
             load_wi(0, 2, 2)
             banks["Tw0.2"] = turn_row("wi", 0, 2)
             banks["Tw0.2"]("s")
             banks["Tw0.3"] = turn_row("wi", 0, 3)
             banks["Tw0.3"]("s")
             quantize_rows("wi", 0, 2)
+            load_x(0)
             load_grad(0, 1)
             load_pre(0, 1, 0, 1)
             relu_backward(0, 1, 0, 1)
             load_pre(0, 1, 1, 1)
             relu_backward(0, 1, 1, 1)
+            banks["Tx0.0"] = turn_x(0, 0)
+            banks["Tx0.0"]("s")
+            banks["Tx0.1"] = turn_x(0, 1)
+            banks["Tx0.1"]("s")
+            quantize_x(0)
             banks["D0.0"] = dh(0, 0, 0)
             banks["D0.0"]("s")
             banks["D0.1"] = dh(0, 0, 1)
             banks["D0.1"]("s")
             interleave_dz1(0, 0)
             banks["T21.0"] = turn_dz2(0, 1, 0)
-            banks["T21.1"] = turn_dz2(0, 1, 1)
-            load_wi(1, 0, 4)
-            banks["Tw1.0"] = turn_row("wi", 1, 0)
-            banks["Tw1.0"]("v")
             banks["T21.0"]("s")
+            banks["T21.1"] = turn_dz2(0, 1, 1)
             banks["T21.1"]("s")
             quantize_dz2(0, 1)
             quantize_dz1_m(0, 0)
-            banks["Tw1.1"] = turn_row("wi", 1, 1)
-            banks["Tw1.1"]("s")
-            quantize_rows("wi", 1, 0)
+            load_wi(1, 0, 4)
             load_grad(1, 0)
             load_pre(1, 0, 0, 1)
             relu_backward(1, 0, 0, 1)
             load_pre(1, 0, 1, 1)
             relu_backward(1, 0, 1, 1)
+            banks["Tw1.0"] = turn_row("wi", 1, 0)
+            banks["Tw1.0"]("s")
+            banks["Tw1.1"] = turn_row("wi", 1, 1)
+            banks["Tw1.1"]("s")
             banks["Tw1.2"] = turn_row("wi", 1, 2)
             banks["Tw1.2"]("s")
             banks["Tw1.3"] = turn_row("wi", 1, 3)
             banks["Tw1.3"]("s")
-            quantize_rows("wi", 1, 2)
-            banks["O00.0"] = output_0(0, 0, 0)
-            banks["O00.0"]("s")
-            banks["O00.1"] = output_0(0, 0, 1)
-            banks["O00.1"]("s")
+            quantize_rows("wi", 1, 0)
             banks["D1.0"] = dh(0, 1, 0)
             banks["D1.0"]("s")
             banks["D1.1"] = dh(0, 1, 1)
             banks["D1.1"]("s")
             interleave_dz1(0, 1)
             banks["T22.0"] = turn_dz2(1, 0, 0)
-            banks["T22.1"] = turn_dz2(1, 0, 1)
-            load_x(1)
-            banks["Tx1.0"] = turn_x(1, 0)
-            banks["Tx1.0"]("v")
             banks["T22.0"]("s")
+            banks["T22.1"] = turn_dz2(1, 0, 1)
             banks["T22.1"]("s")
             quantize_dz2(1, 0)
+            load_x(1)
             load_grad(1, 1)
             load_pre(1, 1, 0, 1)
             relu_backward(1, 1, 0, 1)
             load_pre(1, 1, 1, 1)
             relu_backward(1, 1, 1, 1)
+            banks["Tx1.0"] = turn_x(1, 0)
+            banks["Tx1.0"]("s")
             banks["Tx1.1"] = turn_x(1, 1)
             banks["Tx1.1"]("s")
             quantize_x(1)
+            banks["O00.0"] = output_0(0, 0, 0)
+            banks["O00.0"]("s")
+            banks["O00.1"] = output_0(0, 0, 1)
+            banks["O00.1"]("s")
             banks["D2.0"] = dh(1, 0, 0)
             banks["D2.0"]("s")
             banks["D2.1"] = dh(1, 0, 1)
@@ -330,20 +336,19 @@ def tile_flaxpositionwisemoelayer_pa_v_kernel(tc, dispatch_mask, x, wi, pre, gra
             banks["T23.0"]("s")
             banks["T23.1"]("s")
             quantize_dz2(1, 1)
-            banks["Ts00.0"]("s")
-            banks["Tw2.1"] = turn_row("wi", 2, 1)
-            banks["Tw2.1"]("s")
-            quantize_rows("wi", 2, 0)
             load_grad(2, 0)
             load_pre(2, 0, 0, 1)
             relu_backward(2, 0, 0, 1)
             load_pre(2, 0, 1, 1)
             relu_backward(2, 0, 1, 1)
+            banks["Ts00.0"]("s")
+            banks["Tw2.1"] = turn_row("wi", 2, 1)
+            banks["Tw2.1"]("s")
             banks["Tw2.2"] = turn_row("wi", 2, 2)
             banks["Tw2.2"]("s")
             banks["Tw2.3"] = turn_row("wi", 2, 3)
             banks["Tw2.3"]("s")
-            quantize_rows("wi", 2, 2)
+            quantize_rows("wi", 2, 0)
             banks["O01.0"] = output_0(0, 1, 0)
             banks["O01.0"]("s")
             banks["O01.1"] = output_0(0, 1, 1)
@@ -363,20 +368,19 @@ def tile_flaxpositionwisemoelayer_pa_v_kernel(tc, dispatch_mask, x, wi, pre, gra
             banks["T24.0"]("s")
             banks["T24.1"]("s")
             quantize_dz2(2, 0)
-            banks["Ts00.1"]("s")
-            banks["Tw3.1"] = turn_row("wi", 3, 1)
-            banks["Tw3.1"]("s")
-            quantize_rows("wi", 3, 0)
             load_grad(3, 0)
             load_pre(3, 0, 0, 1)
             relu_backward(3, 0, 0, 1)
             load_pre(3, 0, 1, 1)
             relu_backward(3, 0, 1, 1)
+            banks["Ts00.1"]("s")
+            banks["Tw3.1"] = turn_row("wi", 3, 1)
+            banks["Tw3.1"]("s")
             banks["Tw3.2"] = turn_row("wi", 3, 2)
             banks["Tw3.2"]("s")
             banks["Tw3.3"] = turn_row("wi", 3, 3)
             banks["Tw3.3"]("s")
-            quantize_rows("wi", 3, 2)
+            quantize_rows("wi", 3, 0)
             banks["O02.0"] = output_0(1, 0, 0)
             banks["O02.0"]("s")
             banks["O02.1"] = output_0(1, 0, 1)
@@ -395,21 +399,20 @@ def tile_flaxpositionwisemoelayer_pa_v_kernel(tc, dispatch_mask, x, wi, pre, gra
             quantize_dz2(3, 0)
             quantize_dz1_m(2, 0)
             load_mask(0, 0, 4)
-            banks["Tm0.0"] = turn_row("mask", 0, 0)
-            banks["Tm0.0"]("s")
-            banks["Tm0.1"] = turn_row("mask", 0, 1)
-            banks["Tm0.1"]("s")
-            quantize_rows("mask", 0, 0)
             load_grad(2, 1)
             load_pre(2, 1, 0, 1)
             relu_backward(2, 1, 0, 1)
             load_pre(2, 1, 1, 1)
             relu_backward(2, 1, 1, 1)
+            banks["Tm0.0"] = turn_row("mask", 0, 0)
+            banks["Tm0.0"]("s")
+            banks["Tm0.1"] = turn_row("mask", 0, 1)
+            banks["Tm0.1"]("s")
             banks["Tm0.2"] = turn_row("mask", 0, 2)
             banks["Tm0.2"]("s")
             banks["Tm0.3"] = turn_row("mask", 0, 3)
             banks["Tm0.3"]("s")
-            quantize_rows("mask", 0, 2)
+            quantize_rows("mask", 0, 0)
             banks["O03.0"] = output_0(1, 1, 0)
             banks["O03.0"]("s")
             banks["O03.1"] = output_0(1, 1, 1)
@@ -432,7 +435,7 @@ def tile_flaxpositionwisemoelayer_pa_v_kernel(tc, dispatch_mask, x, wi, pre, gra
             banks["Ts10.1"] = turn_dz1(1, 0, 1)
             banks["Ts10.1"]("s")
             quantize_dz1_slots(1, 0)
-            load_mask(1, 0, 4)
+            load_mask(1, 0, 2)
             load_grad(3, 1)
             load_pre(3, 1, 0, 1)
             relu_backward(3, 1, 0, 1)
@@ -456,6 +459,7 @@ def tile_flaxpositionwisemoelayer_pa_v_kernel(tc, dispatch_mask, x, wi, pre, gra
             banks["D6.1"]("s")
             interleave_dz1(2, 1)
             banks["T27.0"] = turn_dz2(3, 1, 0)
+            load_mask(1, 2, 2)
             banks["Tm1.2"] = turn_row("mask", 1, 2)
             banks["T27.1"] = turn_dz2(3, 1, 1)
             banks["T27.1"]("v")
@@ -513,7 +517,8 @@ def tile_flaxpositionwisemoelayer_pa_v_kernel(tc, dispatch_mask, x, wi, pre, gra
             store_1(0, 0, 2)
             store_0((1, 1, 0), 1, slice(0, 4), slice(2 * C, 3 * C))
             store_1(0, 2, 2)
-            store_0((1, 1, 1), 1, slice(0, 4), slice(3 * C, 4 * C))
+            store_0((1, 1, 1, 0), 1, slice(0, 2), slice(3 * C, 4 * C))
+            store_0((1, 1, 1, 1), 1, slice(2, 4), slice(3 * C, 4 * C))
             store_1(1, 0, 2)
             store_1(1, 2, 1)
             store_1(1, 3, 1)

@@ -22,7 +22,7 @@ BUFS = {
     "pre": 5, "grad": 4, "rows": 3, "x": 2, "dz2": 3, "wide": 1, "narrow": 5,
     "wi_codes": 2, "wi_scales": 2, "dz2_codes": 2, "dz2_scales": 2, "dz1": 4, "dz1_by_m": 3,
     "x_codes": 2, "x_scales": 2, "mask_codes": 2, "mask_scales": 2,
-    "dz1_m_codes": 3, "dz1_m_scales": 3, "dz1_k_codes": 4, "dz1_k_scales": 4, "result": 5,
+    "dz1_m_codes": 3, "dz1_m_scales": 3, "dz1_k_codes": 4, "dz1_k_scales": 4, "result": 3, "result_all": 1,
 }
 SHARES = {"wi": "rows", "mask": "rows"}
 
@@ -194,7 +194,7 @@ def tile_flaxpositionwisemoelayer_pa_v_kernel(tc, dispatch_mask, x, wi, pre, gra
 
         def result_0(e, g, h):
             if g == 0:
-                return ring_tile("result", (0, h), [P, 2, E * C], F32)[:, :, C * e : C * (e + 1)]
+                return ring_tile("result_all", 0, [P, 4, E * C], F32)[:, 2 * h : 2 * h + 2, C * e : C * (e + 1)]
             pair, i = divmod(e, 2)
             if pair == 0:
                 return ring_tile("result", (1, pair), [P, 4, N], F32)[:, 2 * h : 2 * h + 2, C * i : C * (i + 1)]
@@ -212,7 +212,7 @@ def tile_flaxpositionwisemoelayer_pa_v_kernel(tc, dispatch_mask, x, wi, pre, gra
                 acc[:].rearrange("p t (u q b) -> p t q u b", u=2, b=2))
 
         def store_0(key, g, rows, cols):
-            nc.sync.dma_start(out=out0_rows[g, :, rows, cols], in_=tiles["result", key][:])
+            nc.sync.dma_start(out=out0_rows[g, :, rows, cols], in_=tiles["result_all" if g == 0 else "result", key][:])
 
         def output_1(g, row, pairs=range(PAIRS)):
             if ("acc1", g, row) not in tiles:
@@ -425,98 +425,96 @@ def tile_flaxpositionwisemoelayer_pa_v_kernel(tc, dispatch_mask, x, wi, pre, gra
             banks["O04.0"] = output_0(2, 0, 0)
             banks["O04.1"] = output_0(2, 0, 1)
             banks["T26.0"] = turn_dz2(2, 1, 0)
-            banks["T26.1"] = turn_dz2(2, 1, 1)
-            banks["Ts10.0"] = turn_dz1(1, 0, 0)
-            banks["Ts10.0"]("v")
             banks["T26.0"]("s")
+            banks["T26.1"] = turn_dz2(2, 1, 1)
             banks["T26.1"]("s")
             quantize_dz2(2, 1)
             quantize_dz1_m(3, 0)
-            banks["Ts10.1"] = turn_dz1(1, 0, 1)
-            banks["Ts10.1"]("s")
-            quantize_dz1_slots(1, 0)
             load_mask(1, 0, 2)
             load_grad(3, 1)
             load_pre(3, 1, 0, 1)
             relu_backward(3, 1, 0, 1)
             load_pre(3, 1, 1, 1)
             relu_backward(3, 1, 1, 1)
-            banks["Tm1.0"] = turn_row("mask", 1, 0)
-            banks["Tm1.1"] = turn_row("mask", 1, 1)
-            banks["Tm1.1"]("v")
+            banks["Ts10.0"] = turn_dz1(1, 0, 0)
+            banks["Ts10.0"]("s")
             banks["O04.0"]("s")
             banks["O04.1"]("s")
-            banks["Tm1.0"]("s")
+            banks["Ts10.1"] = turn_dz1(1, 0, 1)
+            banks["Ts10.1"]("s")
+            quantize_dz1_slots(1, 0)
+            banks["Tm1.0"] = turn_row("mask", 1, 0)
+            banks["Tm1.1"] = turn_row("mask", 1, 1)
             banks["Ts01.0"] = turn_dz1(0, 1, 0)
             banks["Ts01.1"] = turn_dz1(0, 1, 1)
             banks["O05.0"] = output_0(3, 0, 0)
-            banks["O05.0"]("s")
             banks["O05.1"] = output_0(3, 0, 1)
-            banks["O05.1"]("s")
             banks["D6.0"] = dh(2, 1, 0)
-            banks["D6.0"]("s")
             banks["D6.1"] = dh(2, 1, 1)
-            banks["D6.1"]("s")
-            interleave_dz1(2, 1)
+            banks["D6.1"]("v")
             banks["T27.0"] = turn_dz2(3, 1, 0)
-            load_mask(1, 2, 2)
-            banks["Tm1.2"] = turn_row("mask", 1, 2)
             banks["T27.1"] = turn_dz2(3, 1, 1)
             banks["T27.1"]("v")
-            quantize_dz1_m(2, 1)
+            banks["O05.0"]("s")
+            banks["O05.1"]("s")
+            banks["D6.0"]("s")
+            interleave_dz1(2, 1)
             banks["T27.0"]("s")
             quantize_dz2(3, 1)
-            banks["Tm1.3"] = turn_row("mask", 1, 3)
+            quantize_dz1_m(2, 1)
             banks["O10.0"] = output_1(0, 0)
             banks["O10.1"] = output_1(0, 1)
             banks["O10.1"]("v")
-            quantize_rows("mask", 1, 0)
-            banks["O06.0"] = output_0(2, 1, 0)
-            banks["O06.1"] = output_0(2, 1, 1)
+            banks["O10.2"] = output_1(0, 2)
+            banks["O10.3"] = output_1(0, 3)
+            banks["O10.3"]("v")
             banks["D7.0"] = dh(3, 1, 0)
             banks["D7.0"]("v")
+            banks["Tm1.0"]("s")
+            banks["O10.0"]("s")
+            banks["Tm1.1"]("s")
+            quantize_rows("mask", 1, 0)
+            banks["O10.2"]("s")
             banks["Ts01.0"]("s")
             banks["Ts01.1"]("s")
-            quantize_dz1_slots(0, 1)
-            banks["O10.0"]("s")
-            banks["Tm1.2"]("s")
-            banks["O06.0"]("s")
-            banks["O06.1"]("s")
             banks["D7.1"] = dh(3, 1, 1)
             banks["D7.1"]("s")
             interleave_dz1(3, 1)
-            banks["O10.2"] = output_1(0, 2)
-            banks["O10.3"] = output_1(0, 3)
-            banks["Ts11.0"] = turn_dz1(1, 1, 0)
-            banks["Ts11.0"]("v")
+            quantize_dz1_slots(0, 1)
             quantize_dz1_m(3, 1)
-            banks["O10.2"]("s")
-            banks["O10.3"]("s")
+            banks["O06.0"] = output_0(2, 1, 0)
+            banks["O06.1"] = output_0(2, 1, 1)
+            banks["Ts11.0"] = turn_dz1(1, 1, 0)
             banks["Ts11.1"] = turn_dz1(1, 1, 1)
+            load_mask(1, 2, 2)
+            banks["Tm1.2"] = turn_row("mask", 1, 2)
+            banks["Tm1.2"]("v")
+            banks["O06.0"]("s")
+            banks["O06.1"]("s")
+            banks["Ts11.0"]("s")
             banks["Ts11.1"]("s")
             quantize_dz1_slots(1, 1)
+            banks["Tm1.3"] = turn_row("mask", 1, 3)
             banks["Tm1.3"]("s")
             quantize_rows("mask", 1, 2)
-            output_1(1, 0, [0])
-            output_1(1, 1, [0])
             banks["O07.0"] = output_0(3, 1, 0)
             banks["O07.1"] = output_0(3, 1, 1)
-            banks["O07.1"]("v")
+            output_1(1, 0, [0])
+            output_1(1, 1, [0])
             banks["O11.0"] = output_1(1, 0, [1])
             banks["O11.0"]("v")
             banks["O11.1"] = output_1(1, 1, [1])
             banks["O11.2"] = output_1(1, 2)
             banks["O11.2"]("v")
             banks["O07.0"]("s")
+            banks["O07.1"]("s")
             banks["O11.1"]("s")
             banks["O11.3"] = output_1(1, 3)
             banks["O11.3"]("s")
             store_0((1, 0), 1, slice(0, 4), slice(0, N))
-            store_0((0, 0), 0, slice(0, 2), slice(0, E * C))
-            store_0((0, 1), 0, slice(2, 4), slice(0, E * C))
-            store_1(0, 0, 2)
+            store_0(0, 0, slice(0, 4), slice(0, E * C))
+            store_1(0, 0, 4)
             store_0((1, 1, 0), 1, slice(0, 4), slice(2 * C, 3 * C))
-            store_1(0, 2, 2)
             store_0((1, 1, 1, 0), 1, slice(0, 2), slice(3 * C, 4 * C))
             store_0((1, 1, 1, 1), 1, slice(2, 4), slice(3 * C, 4 * C))
             store_1(1, 0, 2)

@@ -18,13 +18,28 @@ P = 128
 N = 512
 PAIRS = E // 2
 
+UNITS = ((0, 0), (0, 1), (1, 0), (1, 1), (2, 0), (3, 0), (2, 1), (3, 1))
+BEHIND = (("x", 0), ("wi", 1), ("x", 1), ("wi", 2), ("wi", 3), ("mask", 0))
+WHOLE = (1, 2, 3, 4)
+
 BUFS = {
-    "pre": 5, "grad": 4, "rows": 3, "x": 2, "dz2": 3, "wide": 1, "narrow": 5,
-    "wi_codes": 2, "wi_scales": 2, "dz2_codes": 2, "dz2_scales": 2, "dz1": 4, "dz1_by_m": 3,
+    "pre": 5,
+    "grad": 4,
+    "rows": 3,
+    "x": 2,
+    "dz2": 3,
+    "wide": 1,
+    "narrow": 5,
+    "dz1": 4,
+    "dz1_by_m": 3,
+    "wi_codes": 2, "wi_scales": 2, "dz2_codes": 2, "dz2_scales": 2,
     "x_codes": 2, "x_scales": 2, "mask_codes": 2, "mask_scales": 2,
-    "dz1_m_codes": 3, "dz1_m_scales": 3, "dz1_k_codes": 4, "dz1_k_scales": 4, "result": 3, "result_all": 1,
+    "dz1_m_codes": 3, "dz1_m_scales": 3,
+    "dz1_k_codes": 4, "dz1_k_scales": 4,
+    "result_all": 1,
+    "result": 3,
 }
-SHARES = {"wi": "rows", "mask": "rows"}
+SHARES = {"wi": "rows", "mask": "rows", "result_1": "pre"}
 
 
 def tile_flaxpositionwisemoelayer_pa_v_kernel(tc, dispatch_mask, x, wi, pre, grad_out, out_0, out_1):
@@ -69,7 +84,7 @@ def tile_flaxpositionwisemoelayer_pa_v_kernel(tc, dispatch_mask, x, wi, pre, gra
                 pieces[kind, index, r] = (t, r - j)
             return t
 
-        def load_pre(e, g, j=0, n=2):
+        def load_pre(e, g, j, n):
             nc.sync.dma_start(out=piece("pre", (e, g), j, n, [P, n, H], F32)[:], in_=pre_rows[e, g, :, j : j + n, :])
 
         def load_grad(e, g):
@@ -95,17 +110,18 @@ def tile_flaxpositionwisemoelayer_pa_v_kernel(tc, dispatch_mask, x, wi, pre, gra
                 grouped()[:].bitcast(F32)[:, N * block : N * (block + 1)].rearrange("p (i r u) -> p i r u", i=2, u=2),
                 bank[:].rearrange("p i u r -> p i r u"))
 
-        parts = {("wi", 0): 2, ("mask", 1): 2}
+        def rows_together(kind, index):
+            return 2 if (kind, index) in (("wi", 0), ("mask", 1)) else 4
 
         def grouped_rows(kind, index, row):
-            n = parts.get((kind, index), 4)
+            n = rows_together(kind, index)
             return ring_tile("narrow" if n == 2 else "wide", (kind, index, row // n), [P, 1024 * n], BF16)
 
         def turn_row(kind, index, row):
             tile, at = pieces[kind, index, row]
             words = tile[:, at, :].bitcast(F32)
             return turn(lambda i, u: words[:, 256 * i + u : 256 * (i + 1) : 2],
-                        lambda: grouped_rows(kind, index, row), row % parts.get((kind, index), 4))
+                        lambda: grouped_rows(kind, index, row), row % rows_together(kind, index))
 
         def turn_x(g, h):
             rows = tiles["x", g]
@@ -130,7 +146,7 @@ def tile_flaxpositionwisemoelayer_pa_v_kernel(tc, dispatch_mask, x, wi, pre, gra
                         lambda: ring_tile("narrow", ("dz1", pair, g), [P, 2048], BF16), h)
 
 
-        def relu_backward(e, g, j=0, n=2):
+        def relu_backward(e, g, j, n):
             dz2 = piece("dz2", (e, g), j, n, [P, 2, n, N], BF16)
             pre_tile, pre_at = pieces["pre", (e, g), j]
             grad_tile, grad_at = pieces["grad", (e, g), j]
@@ -223,300 +239,147 @@ def tile_flaxpositionwisemoelayer_pa_v_kernel(tc, dispatch_mask, x, wi, pre, gra
                         operand("dz1_k", (pair, g), 0, N, E5M2), pair == 0, pair == 1)
             return lambda engine: copy(
                 engine,
-                ring_tile("pre", ("out_1", g), [P, 4, N], F32)[:, row, :].rearrange("p (m t) -> p m t", t=4),
+                ring_tile("result_1", g, [P, 4, N], F32)[:, row, :].rearrange("p (m t) -> p m t", t=4),
                 acc[:].rearrange("p (t m) -> p m t", t=4))
 
-        def warm_up(n):
-            unread = psum.tile([P, n, P], F32, tag="bank", name="unread")
-            for i in range(n):
-                nc.tensor.matmul(out=unread[:, i, :], lhsT=ident[:], rhs=ident[:], start=True, stop=True)
-
         def store_1(g, row, n):
-            nc.sync.dma_start(out=out1_rows[g, :, row : row + n, :], in_=tiles["pre", ("out_1", g)][:, row : row + n, :])
+            nc.sync.dma_start(out=out1_rows[g, :, row : row + n, :], in_=tiles["result_1", g][:, row : row + n, :])
 
 
-        banks = {}
+        def scalar(banks):
+            for bank in banks:
+                bank("s")
+
+        def both(step, *key):
+            return [step(*key, h) for h in range(2)]
+
+        def pre_pieces(k):
+            return [(0, 2)] if k in WHOLE else [(0, 1), (1, 1)]
+
+        def load_unit(k):
+            load_grad(*UNITS[k])
+            for j, n in pre_pieces(k):
+                load_pre(*UNITS[k], j, n)
+
+        def relu_unit(k):
+            for j, n in pre_pieces(k):
+                relu_backward(*UNITS[k], j, n)
+
+        def load_behind(kind, index):
+            {"x": load_x, "wi": load_wi, "mask": load_mask}[kind](index)
+
+        def turn_behind(kind, index):
+            return both(turn_x, index) if kind == "x" else [turn_row(kind, index, row) for row in range(4)]
+
+        def quantize_behind(kind, index):
+            if kind == "x":
+                quantize_x(index)
+            else:
+                quantize_rows(kind, index)
+
         with tc.manual_schedule():
             load_wi(0, 0, 2)
-            load_grad(0, 0)
-            load_pre(0, 0, 0, 1)
-            relu_backward(0, 0, 0, 1)
-            load_pre(0, 0, 1, 1)
-            relu_backward(0, 0, 1, 1)
-            banks["Tw0.0"] = turn_row("wi", 0, 0)
-            banks["Tw0.0"]("s")
-            banks["Tw0.1"] = turn_row("wi", 0, 1)
-            banks["Tw0.1"]("s")
-            quantize_rows("wi", 0, 0)
-            banks["T20.0"] = turn_dz2(0, 0, 0)
-            banks["T20.0"]("s")
-            banks["T20.1"] = turn_dz2(0, 0, 1)
-            banks["T20.1"]("s")
-            quantize_dz2(0, 0)
+            load_unit(0)
             load_wi(0, 2, 2)
-            banks["Tw0.2"] = turn_row("wi", 0, 2)
-            banks["Tw0.2"]("s")
-            banks["Tw0.3"] = turn_row("wi", 0, 3)
-            banks["Tw0.3"]("s")
+            load_behind(*BEHIND[0])
+            load_unit(1)
+            load_behind(*BEHIND[1])
+            scalar([turn_row("wi", 0, row) for row in range(2)])
+            relu_unit(0)
+            scalar(both(turn_dz2, *UNITS[0]))
+            quantize_rows("wi", 0, 0)
+            quantize_dz2(*UNITS[0])
+            scalar([turn_row("wi", 0, row) for row in range(2, 4)])
             quantize_rows("wi", 0, 2)
-            load_x(0)
-            load_grad(0, 1)
-            load_pre(0, 1, 0, 1)
-            relu_backward(0, 1, 0, 1)
-            load_pre(0, 1, 1, 1)
-            relu_backward(0, 1, 1, 1)
-            banks["Tx0.0"] = turn_x(0, 0)
-            banks["Tx0.0"]("s")
-            banks["Tx0.1"] = turn_x(0, 1)
-            banks["Tx0.1"]("s")
-            quantize_x(0)
-            banks["D0.0"] = dh(0, 0, 0)
-            banks["D0.0"]("s")
-            banks["D0.1"] = dh(0, 0, 1)
-            banks["D0.1"]("s")
-            interleave_dz1(0, 0)
-            banks["T21.0"] = turn_dz2(0, 1, 0)
-            banks["T21.0"]("s")
-            banks["T21.1"] = turn_dz2(0, 1, 1)
-            banks["T21.1"]("s")
-            quantize_dz2(0, 1)
-            quantize_dz1_m(0, 0)
-            load_wi(1, 0, 4)
-            load_grad(1, 0)
-            load_pre(1, 0, 0, 1)
-            relu_backward(1, 0, 0, 1)
-            load_pre(1, 0, 1, 1)
-            relu_backward(1, 0, 1, 1)
-            banks["Tw1.0"] = turn_row("wi", 1, 0)
-            banks["Tw1.0"]("s")
-            banks["Tw1.1"] = turn_row("wi", 1, 1)
-            banks["Tw1.1"]("s")
-            banks["Tw1.2"] = turn_row("wi", 1, 2)
-            banks["Tw1.2"]("s")
-            banks["Tw1.3"] = turn_row("wi", 1, 3)
-            banks["Tw1.3"]("s")
-            quantize_rows("wi", 1, 0)
-            banks["D1.0"] = dh(0, 1, 0)
-            banks["D1.0"]("s")
-            banks["D1.1"] = dh(0, 1, 1)
-            banks["D1.1"]("s")
-            interleave_dz1(0, 1)
-            banks["T22.0"] = turn_dz2(1, 0, 0)
-            banks["T22.0"]("s")
-            banks["T22.1"] = turn_dz2(1, 0, 1)
-            banks["T22.1"]("s")
-            quantize_dz2(1, 0)
-            load_x(1)
-            load_grad(1, 1)
-            load_pre(1, 1, 0, 1)
-            relu_backward(1, 1, 0, 1)
-            load_pre(1, 1, 1, 1)
-            relu_backward(1, 1, 1, 1)
-            banks["Tx1.0"] = turn_x(1, 0)
-            banks["Tx1.0"]("s")
-            banks["Tx1.1"] = turn_x(1, 1)
-            banks["Tx1.1"]("s")
-            quantize_x(1)
-            banks["O00.0"] = output_0(0, 0, 0)
-            banks["O00.0"]("s")
-            banks["O00.1"] = output_0(0, 0, 1)
-            banks["O00.1"]("s")
-            banks["D2.0"] = dh(1, 0, 0)
-            banks["D2.0"]("s")
-            banks["D2.1"] = dh(1, 0, 1)
-            banks["D2.1"]("s")
-            interleave_dz1(1, 0)
-            quantize_dz1_m(0, 1)
-            banks["T23.0"] = turn_dz2(1, 1, 0)
-            banks["Ts00.0"] = turn_dz1(0, 0, 0)
-            banks["T23.1"] = turn_dz2(1, 1, 1)
-            load_wi(2, 0, 4)
-            banks["Tw2.0"] = turn_row("wi", 2, 0)
-            banks["Tw2.0"]("v")
-            banks["T23.0"]("s")
-            banks["T23.1"]("s")
-            quantize_dz2(1, 1)
-            load_grad(2, 0)
-            load_pre(2, 0, 0, 1)
-            relu_backward(2, 0, 0, 1)
-            load_pre(2, 0, 1, 1)
-            relu_backward(2, 0, 1, 1)
-            banks["Ts00.0"]("s")
-            banks["Tw2.1"] = turn_row("wi", 2, 1)
-            banks["Tw2.1"]("s")
-            banks["Tw2.2"] = turn_row("wi", 2, 2)
-            banks["Tw2.2"]("s")
-            banks["Tw2.3"] = turn_row("wi", 2, 3)
-            banks["Tw2.3"]("s")
-            quantize_rows("wi", 2, 0)
-            banks["O01.0"] = output_0(0, 1, 0)
-            banks["O01.0"]("s")
-            banks["O01.1"] = output_0(0, 1, 1)
-            banks["O01.1"]("s")
-            banks["D3.0"] = dh(1, 1, 0)
-            banks["D3.0"]("s")
-            banks["D3.1"] = dh(1, 1, 1)
-            banks["D3.1"]("s")
-            interleave_dz1(1, 1)
-            quantize_dz1_m(1, 0)
-            banks["T24.0"] = turn_dz2(2, 0, 0)
-            banks["Ts00.1"] = turn_dz1(0, 0, 1)
-            banks["T24.1"] = turn_dz2(2, 0, 1)
-            load_wi(3, 0, 4)
-            banks["Tw3.0"] = turn_row("wi", 3, 0)
-            banks["Tw3.0"]("v")
-            banks["T24.0"]("s")
-            banks["T24.1"]("s")
-            quantize_dz2(2, 0)
-            load_grad(3, 0)
-            load_pre(3, 0, 0, 1)
-            relu_backward(3, 0, 0, 1)
-            load_pre(3, 0, 1, 1)
-            relu_backward(3, 0, 1, 1)
-            banks["Ts00.1"]("s")
-            banks["Tw3.1"] = turn_row("wi", 3, 1)
-            banks["Tw3.1"]("s")
-            banks["Tw3.2"] = turn_row("wi", 3, 2)
-            banks["Tw3.2"]("s")
-            banks["Tw3.3"] = turn_row("wi", 3, 3)
-            banks["Tw3.3"]("s")
-            quantize_rows("wi", 3, 0)
-            banks["O02.0"] = output_0(1, 0, 0)
-            banks["O02.0"]("s")
-            banks["O02.1"] = output_0(1, 0, 1)
-            banks["O02.1"]("s")
-            banks["D4.0"] = dh(2, 0, 0)
-            banks["D4.0"]("s")
-            banks["D4.1"] = dh(2, 0, 1)
-            banks["D4.1"]("s")
-            interleave_dz1(2, 0)
-            quantize_dz1_m(1, 1)
-            quantize_dz1_slots(0, 0)
-            banks["T25.0"] = turn_dz2(3, 0, 0)
-            banks["T25.0"]("s")
-            banks["T25.1"] = turn_dz2(3, 0, 1)
-            banks["T25.1"]("s")
-            quantize_dz2(3, 0)
-            quantize_dz1_m(2, 0)
-            load_mask(0, 0, 4)
-            load_grad(2, 1)
-            load_pre(2, 1, 0, 1)
-            relu_backward(2, 1, 0, 1)
-            load_pre(2, 1, 1, 1)
-            relu_backward(2, 1, 1, 1)
-            banks["Tm0.0"] = turn_row("mask", 0, 0)
-            banks["Tm0.0"]("s")
-            banks["Tm0.1"] = turn_row("mask", 0, 1)
-            banks["Tm0.1"]("s")
-            banks["Tm0.2"] = turn_row("mask", 0, 2)
-            banks["Tm0.2"]("s")
-            banks["Tm0.3"] = turn_row("mask", 0, 3)
-            banks["Tm0.3"]("s")
-            quantize_rows("mask", 0, 0)
-            banks["O03.0"] = output_0(1, 1, 0)
-            banks["O03.0"]("s")
-            banks["O03.1"] = output_0(1, 1, 1)
-            banks["O03.1"]("s")
-            banks["D5.0"] = dh(3, 0, 0)
-            banks["D5.0"]("s")
-            banks["D5.1"] = dh(3, 0, 1)
-            banks["D5.1"]("s")
-            interleave_dz1(3, 0)
-            banks["O04.0"] = output_0(2, 0, 0)
-            banks["O04.1"] = output_0(2, 0, 1)
-            banks["T26.0"] = turn_dz2(2, 1, 0)
-            banks["T26.0"]("s")
-            banks["T26.1"] = turn_dz2(2, 1, 1)
-            banks["T26.1"]("s")
-            quantize_dz2(2, 1)
-            quantize_dz1_m(3, 0)
+            scalar(turn_behind(*BEHIND[0]))
+            scalar(both(dh, *UNITS[0]))
+
+            for k in range(1, 6):
+                load_unit(k + 1)
+                if k < 5:
+                    load_behind(*BEHIND[k + 1])
+                relu_unit(k)
+                banks = [turn_dz2(*UNITS[k], 0)]
+                slots = [turn_dz1(0, 0, k - 3)] if k in (3, 4) else []
+                scalar(banks + [turn_dz2(*UNITS[k], 1)] + slots)
+                quantize_behind(*BEHIND[k - 1])
+                banks = turn_behind(*BEHIND[k])
+                interleave_dz1(*UNITS[k - 1])
+                if k >= 3:
+                    quantize_dz1_m(*UNITS[k - 2])
+                if k in (3, 4):
+                    banks.pop(0)("v")
+                if k == 5:
+                    quantize_dz1_slots(0, 0)
+                quantize_dz2(*UNITS[k])
+                if k in (1, 5):
+                    quantize_dz1_m(*UNITS[k - 1])
+                scalar(banks)
+                outs = both(output_0, *UNITS[k - 2]) if k >= 2 else []
+                scalar(outs + both(dh, *UNITS[k]))
+
             load_mask(1, 0, 2)
-            load_grad(3, 1)
-            load_pre(3, 1, 0, 1)
-            relu_backward(3, 1, 0, 1)
-            load_pre(3, 1, 1, 1)
-            relu_backward(3, 1, 1, 1)
-            banks["Ts10.0"] = turn_dz1(1, 0, 0)
-            banks["Ts10.0"]("s")
-            banks["O04.0"]("s")
-            banks["O04.1"]("s")
-            banks["Ts10.1"] = turn_dz1(1, 0, 1)
-            banks["Ts10.1"]("s")
-            quantize_dz1_slots(1, 0)
-            banks["Tm1.0"] = turn_row("mask", 1, 0)
-            banks["Tm1.1"] = turn_row("mask", 1, 1)
-            banks["Ts01.0"] = turn_dz1(0, 1, 0)
-            banks["Ts01.1"] = turn_dz1(0, 1, 1)
-            banks["O05.0"] = output_0(3, 0, 0)
-            banks["O05.1"] = output_0(3, 0, 1)
-            banks["D6.0"] = dh(2, 1, 0)
-            banks["D6.1"] = dh(2, 1, 1)
-            banks["D6.1"]("v")
-            banks["T27.0"] = turn_dz2(3, 1, 0)
-            banks["T27.1"] = turn_dz2(3, 1, 1)
-            banks["T27.1"]("v")
-            banks["O05.0"]("s")
-            banks["O05.1"]("s")
-            banks["D6.0"]("s")
-            interleave_dz1(2, 1)
-            banks["T27.0"]("s")
-            quantize_dz2(3, 1)
-            quantize_dz1_m(2, 1)
-            banks["O10.0"] = output_1(0, 0)
-            banks["O10.1"] = output_1(0, 1)
-            banks["O10.1"]("v")
-            banks["O10.2"] = output_1(0, 2)
-            banks["O10.3"] = output_1(0, 3)
-            banks["O10.3"]("v")
-            banks["D7.0"] = dh(3, 1, 0)
-            banks["D7.0"]("v")
-            banks["Tm1.0"]("s")
-            banks["O10.0"]("s")
-            banks["Tm1.1"]("s")
-            quantize_rows("mask", 1, 0)
-            banks["O10.2"]("s")
-            banks["Ts01.0"]("s")
-            banks["Ts01.1"]("s")
-            banks["D7.1"] = dh(3, 1, 1)
-            banks["D7.1"]("s")
-            interleave_dz1(3, 1)
-            quantize_dz1_slots(0, 1)
-            quantize_dz1_m(3, 1)
-            banks["O06.0"] = output_0(2, 1, 0)
-            banks["O06.1"] = output_0(2, 1, 1)
-            banks["Ts11.0"] = turn_dz1(1, 1, 0)
-            banks["Ts11.1"] = turn_dz1(1, 1, 1)
+            load_unit(7)
             load_mask(1, 2, 2)
-            banks["Tm1.2"] = turn_row("mask", 1, 2)
-            banks["Tm1.2"]("v")
-            banks["O06.0"]("s")
-            banks["O06.1"]("s")
-            banks["Ts11.0"]("s")
-            banks["Ts11.1"]("s")
-            quantize_dz1_slots(1, 1)
-            banks["Tm1.3"] = turn_row("mask", 1, 3)
-            banks["Tm1.3"]("s")
-            quantize_rows("mask", 1, 2)
-            banks["O07.0"] = output_0(3, 1, 0)
-            banks["O07.1"] = output_0(3, 1, 1)
-            output_1(1, 0, [0])
-            output_1(1, 1, [0])
-            banks["O11.0"] = output_1(1, 0, [1])
-            banks["O11.0"]("v")
-            banks["O11.1"] = output_1(1, 1, [1])
-            banks["O11.2"] = output_1(1, 2)
-            banks["O11.2"]("v")
-            banks["O07.0"]("s")
-            banks["O07.1"]("s")
-            banks["O11.1"]("s")
-            banks["O11.3"] = output_1(1, 3)
-            banks["O11.3"]("s")
+            outs = both(output_0, *UNITS[4])
+            relu_unit(6)
+            scalar(both(turn_dz2, *UNITS[6]))
+            slots_0 = both(turn_dz1, 1, 0)
+            mask_1 = [turn_row("mask", 1, row) for row in range(2)]
+            slots_1 = both(turn_dz1, 0, 1)
+            scalar(slots_0[:1] + outs + slots_0[1:])
+            quantize_behind(*BEHIND[5])
+            interleave_dz1(*UNITS[5])
+            quantize_dz2(*UNITS[6])
+            quantize_dz1_m(*UNITS[5])
+            scalar(both(output_0, *UNITS[5]))
             store_0((1, 0), 1, slice(0, 4), slice(0, N))
             store_0(0, 0, slice(0, 4), slice(0, E * C))
+            sums = both(dh, *UNITS[6])
+
+            relu_unit(7)
+            banks = both(turn_dz2, *UNITS[7])
+            quantize_dz1_slots(1, 0)
+            for h in range(2):
+                sums[h]("sv"[h])
+            for h in range(2):
+                banks[h]("sv"[h])
+            outs = [output_1(0, row) for row in range(4)]
+            interleave_dz1(*UNITS[6])
+            quantize_dz2(*UNITS[7])
+            quantize_dz1_m(*UNITS[6])
+            for h in range(2):
+                mask_1[h]("s")
+                outs[2 * h]("s")
+                outs[2 * h + 1]("v")
             store_1(0, 0, 4)
+            scalar(slots_1)
+            sums = both(dh, *UNITS[7])
+            outs = both(output_0, *UNITS[6])
+            for h in range(2):
+                sums[h]("vs"[h])
+            scalar(outs)
             store_0((1, 1, 0), 1, slice(0, 4), slice(2 * C, 3 * C))
-            store_0((1, 1, 1, 0), 1, slice(0, 2), slice(3 * C, 4 * C))
-            store_0((1, 1, 1, 1), 1, slice(2, 4), slice(3 * C, 4 * C))
-            store_1(1, 0, 2)
-            store_1(1, 2, 1)
-            store_1(1, 3, 1)
+            scalar(both(turn_dz1, 1, 1))
+            mask_1 = [turn_row("mask", 1, row) for row in range(2, 4)]
+            quantize_rows("mask", 1, 0)
+            interleave_dz1(*UNITS[7])
+            quantize_dz1_slots(0, 1)
+            quantize_dz1_m(*UNITS[7])
+            for h in range(2):
+                mask_1[h]("vs"[h])
+            outs = both(output_0, *UNITS[7])
+            for h in range(2):
+                outs[h]("s")
+                store_0((1, 1, 1, h), 1, slice(2 * h, 2 * h + 2), slice(3 * C, 4 * C))
+            for row in range(2):
+                output_1(1, row, [0])
+            quantize_dz1_slots(1, 1)
+            quantize_rows("mask", 1, 2)
+            outs = [output_1(1, row, [1]) for row in range(2)] + [output_1(1, row) for row in range(2, 4)]
+            for row in range(4):
+                outs[row]("vs"[row % 2])
+                if row == 1:
+                    store_1(1, 0, 2)
+                if row >= 2:
+                    store_1(1, row, 1)

from contextlib import ExitStack

import concourse.mybir as mybir
from concourse.masks import make_identity

G, S, M, H, E, C = 2, 512, 512, 1024, 4, 256
FLOPS = 2 * E * G * C * H * M + 2 * 2 * G * S * M * E * C

F32 = mybir.dt.float32
BF16 = mybir.dt.bfloat16
U32 = mybir.dt.uint32
U8 = mybir.dt.uint8
E4M3 = mybir.dt.float8_e4m3fn_x4
E5M2 = mybir.dt.float8_e5m2_x4
ALU = mybir.AluOpType

P = 128
N = 512
PAIRS = E // 2

UNITS = ((0, 0), (0, 1), (1, 0), (1, 1), (2, 0), (3, 0), (2, 1), (3, 1))
BEHIND = (("x", 0), ("wi", 1), ("x", 1), ("wi", 2), ("wi", 3), ("mask", 0))
WHOLE = (1, 2, 3, 4)

BUFS = {
    "pre": 5,
    "grad": 4,
    "rows": 3,
    "x": 2,
    "dz2": 3,
    "wide": 1,
    "narrow": 5,
    "dz1": 4,
    "dz1_by_m": 3,
    "wi_codes": 2, "wi_scales": 2, "dz2_codes": 2, "dz2_scales": 2,
    "x_codes": 2, "x_scales": 2, "mask_codes": 2, "mask_scales": 2,
    "dz1_m_codes": 3, "dz1_m_scales": 3,
    "dz1_k_codes": 4, "dz1_k_scales": 4,
    "result_all": 1,
    "result": 3,
}
SHARES = {"wi": "rows", "mask": "rows", "result_1": "pre"}


def tile_flaxpositionwisemoelayer_pa_v_kernel(tc, dispatch_mask, x, wi, pre, grad_out, out_0, out_1):
    nc = tc.nc

    mask_rows = dispatch_mask.rearrange("g (p t) e c -> g p t (e c)", t=4)
    x_rows = x.rearrange("g (p t) m -> g p t m", t=4)
    wi_rows = wi.rearrange("e (p t) h -> e p t h", t=4)
    pre_rows = pre.rearrange("e g (p j) h -> e g p j h", j=2)
    grad_rows = grad_out.rearrange("e g (p j) h -> e g p j h", j=2)
    out0_rows = out_0.rearrange("g (p t) e c -> g p t (e c)", t=4)
    out1_rows = out_1.rearrange("g (p t) m -> g p t m", t=4)

    with ExitStack() as ctx:
        keep = ctx.enter_context(tc.tile_pool(name="keep", bufs=1))
        ring = ctx.enter_context(tc.tile_pool(name="ring", bufs=1))
        psum = ctx.enter_context(tc.psum_pool(name="psum", bufs=8))

        ident = keep.tile([P, P], F32, name="ident")
        make_identity(nc, ident[:])

        tiles = {}

        def ring_tile(kind, key, shape, dtype):
            if (kind, key) not in tiles:
                tag = SHARES.get(kind, kind)
                tiles[kind, key] = ring.tile(shape, dtype, tag=tag, bufs=BUFS[tag], align_bytes=64, name=kind)
            return tiles[kind, key]

        def copy(engine, out, in_):
            if engine == "s":
                nc.scalar.copy(out=out, in_=in_)
            else:
                nc.vector.tensor_copy(out=out, in_=in_)


        pieces = {}

        def piece(kind, index, j, n, shape, dtype):
            t = ring_tile(kind, (index, j), shape, dtype)
            for r in range(j, j + n):
                pieces[kind, index, r] = (t, r - j)
            return t

        def load_pre(e, g, j, n):
            nc.sync.dma_start(out=piece("pre", (e, g), j, n, [P, n, H], F32)[:], in_=pre_rows[e, g, :, j : j + n, :])

        def load_grad(e, g):
            nc.sync.dma_start(out=piece("grad", (e, g), 0, 2, [P, 2, H], BF16)[:], in_=grad_rows[e, g])

        def load_wi(e, j=0, n=4):
            nc.sync.dma_start(out=piece("wi", e, j, n, [P, n, H], BF16)[:], in_=wi_rows[e, :, j : j + n, :])

        def load_mask(g, j=0, n=4):
            nc.sync.dma_start(out=piece("mask", g, j, n, [P, n, E * C], BF16)[:], in_=mask_rows[g, :, j : j + n, :])

        def load_x(g):
            nc.sync.dma_start(out=ring_tile("x", g, [P, 4, M], BF16)[:], in_=x_rows[g])


        def turn(source, grouped, block):
            bank = psum.tile([P, 2, 2, P], F32, tag="bank", name="bank")
            for i in range(2):
                for u in range(2):
                    nc.tensor.transpose(bank[:, i, u, :], source(i, u), ident[:])
            return lambda engine: copy(
                engine,
                grouped()[:].bitcast(F32)[:, N * block : N * (block + 1)].rearrange("p (i r u) -> p i r u", i=2, u=2),
                bank[:].rearrange("p i u r -> p i r u"))

        def rows_together(kind, index):
            return 2 if (kind, index) in (("wi", 0), ("mask", 1)) else 4

        def grouped_rows(kind, index, row):
            n = rows_together(kind, index)
            return ring_tile("narrow" if n == 2 else "wide", (kind, index, row // n), [P, 1024 * n], BF16)

        def turn_row(kind, index, row):
            tile, at = pieces[kind, index, row]
            words = tile[:, at, :].bitcast(F32)
            return turn(lambda i, u: words[:, 256 * i + u : 256 * (i + 1) : 2],
                        lambda: grouped_rows(kind, index, row), row % rows_together(kind, index))

        def turn_x(g, h):
            rows = tiles["x", g]
            return turn(lambda i, u: rows[:, 2 * h + i, :].bitcast(F32)[:, u::2],
                        lambda: ring_tile("narrow", ("x", g), [P, 2048], BF16), h)

        def turn_dz2(e, g, j):
            dz2, at = pieces["dz2", (e, g), j]
            bank = psum.tile([P, 2, 2, P], F32, tag="bank", name="bank")
            for u in range(2):
                for a in range(2):
                    nc.tensor.transpose(bank[:, a, u, :], dz2[:, u, at, 256 * a : 256 * (a + 1)].bitcast(F32), ident[:])
            return lambda engine: copy(
                engine,
                ring_tile("narrow", ("dz2", e, g), [P, 2048], BF16)[:].bitcast(F32).rearrange(
                    "p (a j r u) -> p a j r u", a=2, j=2, u=2)[:, :, j],
                bank[:].rearrange("p a u r -> p a r u"))

        def turn_dz1(pair, g, h):
            dz1 = tiles["dz1", (pair, g)]
            return turn(lambda i, u: dz1[:, 2 * h + i, u, :].bitcast(F32),
                        lambda: ring_tile("narrow", ("dz1", pair, g), [P, 2048], BF16), h)


        def relu_backward(e, g, j, n):
            dz2 = piece("dz2", (e, g), j, n, [P, 2, n, N], BF16)
            pre_tile, pre_at = pieces["pre", (e, g), j]
            grad_tile, grad_at = pieces["grad", (e, g), j]
            pre_words = pre_tile[:, pre_at : pre_at + n, :].rearrange("p j (k u b) -> p u j k b", u=2, b=2)
            grad = grad_tile[:, grad_at : grad_at + n, :].rearrange("p j (k u b) -> p u j k b", u=2, b=2)
            for u, rows in [(0, slice(0, n))] + [(1, slice(r, r + 1)) for r in range(n)]:
                nc.vector.scalar_tensor_tensor(
                    out=dz2[:, u, rows].rearrange("p j (k b) -> p j k b", b=2),
                    in0=pre_words[:, u, rows], scalar=0.0, in1=grad[:, u, rows], op0=ALU.is_gt, op1=ALU.mult)

        def quantize(kind, key, words, first, grouped, fmt):
            codes = ring_tile(kind + "_codes", key, [P, words], U32)
            scales = ring_tile(kind + "_scales", key, [P, words], U8)
            cols = slice(first, first + grouped.shape[1] // 4)
            nc.vector.quantize_mx(out=codes[:, cols].bitcast(fmt), scales=scales[:, cols], in_=grouped)

        def operand(kind, key, first, n, fmt):
            cols = slice(first, first + n)
            return tiles[kind + "_codes", key][:, cols].bitcast(fmt), tiles[kind + "_scales", key][:, cols]

        def quantize_rows(kind, index, row=0):
            quantize(kind, index, 1024, 256 * row, grouped_rows(kind, index, row)[:], E4M3)

        def quantize_x(g):
            quantize("x", g, N, 0, tiles["narrow", ("x", g)][:], E4M3)

        def quantize_dz2(e, g):
            quantize("dz2", (e, g), N, 0, tiles["narrow", ("dz2", e, g)][:], E5M2)

        def quantize_dz1_m(e, g):
            quantize("dz1_m", (e, g), C, 0, tiles["dz1_by_m", (e, g)][:].rearrange("p u s t -> p (u s t)"), E5M2)

        def quantize_dz1_slots(pair, g):
            quantize("dz1_k", (pair, g), N, 0, tiles["narrow", ("dz1", pair, g)][:], E5M2)

        def product(out, lhs, rhs, start, stop):
            nc.tensor.matmul_mx(out=out, lhsT=lhs[0], lhsT_scale=lhs[1], rhs=rhs[0], rhs_scale=rhs[1],
                                start=start, stop=stop)


        def dh(e, g, h):
            sums = psum.tile([P, 2, C], F32, tag="bank", name="dh")
            for t in range(2):
                for a in range(2):
                    product(sums[:, t, :], operand("wi", e, 256 * (2 * h + t) + P * a, P, E4M3),
                            operand("dz2", (e, g), C * a, C, E5M2), a == 0, a == 1)
            pair, i = divmod(e, 2)
            return lambda engine: copy(
                engine,
                ring_tile("dz1", (pair, g), [P, 4, 2, 256], BF16)[:, 2 * h : 2 * h + 2, :, P * i : P * (i + 1)].rearrange(
                    "p t u (q b) -> p t u q b", b=2),
                sums[:].rearrange("p t (b q u) -> p t u q b", b=2, u=2))

        def interleave_dz1(e, g):
            pair, i = divmod(e, 2)
            by_m = ring_tile("dz1_by_m", (e, g), [P, 2, P, 4], BF16)
            nc.vector.tensor_copy(
                out=by_m[:].rearrange("p u (c n) t -> p u c t n", n=4),
                in_=tiles["dz1", (pair, g)][:, :, :, P * i : P * (i + 1)].rearrange("p t u (c n) -> p u c t n", n=4))


        def result_0(e, g, h):
            if g == 0:
                return ring_tile("result_all", 0, [P, 4, E * C], F32)[:, 2 * h : 2 * h + 2, C * e : C * (e + 1)]
            pair, i = divmod(e, 2)
            if pair == 0:
                return ring_tile("result", (1, pair), [P, 4, N], F32)[:, 2 * h : 2 * h + 2, C * i : C * (i + 1)]
            if i == 1:
                return ring_tile("result", (1, pair, i, h), [P, 2, C], F32)[:]
            return ring_tile("result", (1, pair, i), [P, 4, C], F32)[:, 2 * h : 2 * h + 2, :]

        def output_0(e, g, h):
            acc = psum.tile([P, 2, C], F32, tag="bank", name="acc")
            for t in range(2):
                product(acc[:, t, :], operand("x", g, P * (2 * h + t), P, E4M3), operand("dz1_m", (e, g), 0, C, E5M2),
                        True, True)
            return lambda engine: copy(
                engine, result_0(e, g, h).rearrange("p t (q u b) -> p t q u b", u=2, b=2),
                acc[:].rearrange("p t (u q b) -> p t q u b", u=2, b=2))

        def store_0(key, g, rows, cols):
            nc.sync.dma_start(out=out0_rows[g, :, rows, cols], in_=tiles["result_all" if g == 0 else "result", key][:])

        def output_1(g, row, pairs=range(PAIRS)):
            if ("acc1", g, row) not in tiles:
                tiles["acc1", g, row] = psum.tile([P, N], F32, tag="bank", name="acc1")
            acc = tiles["acc1", g, row]
            for pair in pairs:
                product(acc[:], operand("mask", g, 256 * row + P * pair, P, E4M3),
                        operand("dz1_k", (pair, g), 0, N, E5M2), pair == 0, pair == 1)
            return lambda engine: copy(
                engine,
                ring_tile("result_1", g, [P, 4, N], F32)[:, row, :].rearrange("p (m t) -> p m t", t=4),
                acc[:].rearrange("p (t m) -> p m t", t=4))

        def store_1(g, row, n):
            nc.sync.dma_start(out=out1_rows[g, :, row : row + n, :], in_=tiles["result_1", g][:, row : row + n, :])


        def scalar(banks):
            for bank in banks:
                bank("s")

        def both(step, *key):
            return [step(*key, h) for h in range(2)]

        def pre_pieces(k):
            return [(0, 2)] if k in WHOLE else [(0, 1), (1, 1)]

        def load_unit(k):
            load_grad(*UNITS[k])
            for j, n in pre_pieces(k):
                load_pre(*UNITS[k], j, n)

        def relu_unit(k):
            for j, n in pre_pieces(k):
                relu_backward(*UNITS[k], j, n)

        def load_behind(kind, index):
            {"x": load_x, "wi": load_wi, "mask": load_mask}[kind](index)

        def turn_behind(kind, index):
            return both(turn_x, index) if kind == "x" else [turn_row(kind, index, row) for row in range(4)]

        def quantize_behind(kind, index):
            if kind == "x":
                quantize_x(index)
            else:
                quantize_rows(kind, index)

        with tc.manual_schedule():
            load_wi(0, 0, 2)
            load_unit(0)
            load_wi(0, 2, 2)
            load_behind(*BEHIND[0])
            load_unit(1)
            load_behind(*BEHIND[1])
            scalar([turn_row("wi", 0, row) for row in range(2)])
            relu_unit(0)
            scalar(both(turn_dz2, *UNITS[0]))
            quantize_rows("wi", 0, 0)
            quantize_dz2(*UNITS[0])
            scalar([turn_row("wi", 0, row) for row in range(2, 4)])
            quantize_rows("wi", 0, 2)
            scalar(turn_behind(*BEHIND[0]))
            scalar(both(dh, *UNITS[0]))

            for k in range(1, 6):
                load_unit(k + 1)
                if k < 5:
                    load_behind(*BEHIND[k + 1])
                relu_unit(k)
                banks = [turn_dz2(*UNITS[k], 0)]
                slots = [turn_dz1(0, 0, k - 3)] if k in (3, 4) else []
                scalar(banks + [turn_dz2(*UNITS[k], 1)] + slots)
                quantize_behind(*BEHIND[k - 1])
                banks = turn_behind(*BEHIND[k])
                interleave_dz1(*UNITS[k - 1])
                if k >= 3:
                    quantize_dz1_m(*UNITS[k - 2])
                if k in (3, 4):
                    banks.pop(0)("v")
                if k == 5:
                    quantize_dz1_slots(0, 0)
                quantize_dz2(*UNITS[k])
                if k in (1, 5):
                    quantize_dz1_m(*UNITS[k - 1])
                scalar(banks)
                outs = both(output_0, *UNITS[k - 2]) if k >= 2 else []
                scalar(outs + both(dh, *UNITS[k]))

            load_mask(1, 0, 2)
            load_unit(7)
            load_mask(1, 2, 2)
            outs = both(output_0, *UNITS[4])
            relu_unit(6)
            scalar(both(turn_dz2, *UNITS[6]))
            slots_0 = both(turn_dz1, 1, 0)
            mask_1 = [turn_row("mask", 1, row) for row in range(2)]
            slots_1 = both(turn_dz1, 0, 1)
            scalar(slots_0[:1] + outs + slots_0[1:])
            quantize_behind(*BEHIND[5])
            interleave_dz1(*UNITS[5])
            quantize_dz2(*UNITS[6])
            quantize_dz1_m(*UNITS[5])
            scalar(both(output_0, *UNITS[5]))
            store_0((1, 0), 1, slice(0, 4), slice(0, N))
            store_0(0, 0, slice(0, 4), slice(0, E * C))
            sums = both(dh, *UNITS[6])

            relu_unit(7)
            banks = both(turn_dz2, *UNITS[7])
            quantize_dz1_slots(1, 0)
            for h in range(2):
                sums[h]("sv"[h])
            for h in range(2):
                banks[h]("sv"[h])
            outs = [output_1(0, row) for row in range(4)]
            interleave_dz1(*UNITS[6])
            quantize_dz2(*UNITS[7])
            quantize_dz1_m(*UNITS[6])
            for h in range(2):
                mask_1[h]("s")
                outs[2 * h]("s")
                outs[2 * h + 1]("v")
            store_1(0, 0, 4)
            scalar(slots_1)
            sums = both(dh, *UNITS[7])
            outs = both(output_0, *UNITS[6])
            for h in range(2):
                sums[h]("vs"[h])
            scalar(outs)
            store_0((1, 1, 0), 1, slice(0, 4), slice(2 * C, 3 * C))
            scalar(both(turn_dz1, 1, 1))
            mask_1 = [turn_row("mask", 1, row) for row in range(2, 4)]
            quantize_rows("mask", 1, 0)
            interleave_dz1(*UNITS[7])
            quantize_dz1_slots(0, 1)
            quantize_dz1_m(*UNITS[7])
            for h in range(2):
                mask_1[h]("vs"[h])
            outs = both(output_0, *UNITS[7])
            for h in range(2):
                outs[h]("s")
                store_0((1, 1, 1, h), 1, slice(2 * h, 2 * h + 2), slice(3 * C, 4 * C))
            for row in range(2):
                output_1(1, row, [0])
            quantize_dz1_slots(1, 1)
            quantize_rows("mask", 1, 2)
            outs = [output_1(1, row, [1]) for row in range(2)] + [output_1(1, row) for row in range(2, 4)]
            for row in range(4):
                outs[row]("vs"[row % 2])
                if row == 1:
                    store_1(1, 0, 2)
                if row >= 2:
                    store_1(1, row, 1)
